import numpy as np
import ml_dtypes


def mxq(x, axis, fmt="e4m3"):
    dtype, down = {"e4m3": (ml_dtypes.float8_e4m3fn, 7), "e5m2": (ml_dtypes.float8_e5m2, 14)}[fmt]
    v = np.moveaxis(np.asarray(x, np.float32).astype(ml_dtypes.bfloat16).astype(np.float64), axis, -1)
    blocks = v.reshape(v.shape[:-1] + (-1, 32))
    amax = np.abs(blocks).max(-1, keepdims=True)
    byte = np.maximum(np.where(amax > 0, np.frexp(amax)[1] - 1 + 127, 0) - down, 1)
    scale = np.exp2(byte - 127.0)
    codes = (blocks / scale).astype(np.float32).astype(dtype).astype(np.float64)
    return np.moveaxis((codes * scale).reshape(v.shape), -1, axis)


WIDE = False


def mx_kscale(k):
    if not WIDE:
        return np.ones(k)
    levels = np.array([10, -10, 5, -5, 0])
    a = np.random.permutation(np.resize(levels, k // 512 * 4)).reshape(k // 512, 4)
    idx = np.arange(k)
    return np.exp2(a[idx // 512, idx % 128 // 32])


BF16 = ml_dtypes.bfloat16


def bf(x):
    return np.asarray(x, np.float32).astype(BF16)


def f64(x):
    return np.asarray(x).astype(np.float64)


B, L, E, H, WINDOW = 4, 1024, 512, 2, 4
D = E // H
NREL = 2 * WINDOW + 1


def band_of(p):
    t = np.arange(L)
    cols = []
    for j in range(NREL):
        s = t + j - WINDOW
        ok = (s >= 0) & (s < L)
        cols.append(np.where(ok[None, :], p[:, t, np.clip(s, 0, L - 1)], 0.0))
    return np.stack(cols, axis=-1)


def setup_inputs():
    u = mx_kscale(E)
    td = np.repeat(np.array([u.max(), u.min()]), D // 2)
    t = np.tile(td, H)
    return {
        "logits": bf(np.random.standard_normal((B * H, L, L)) * 1.5),
        "v": bf(np.random.standard_normal((B * H, L, D)) * td),
        "emb_rel_v": bf(np.random.standard_normal((1, NREL, D)) * td),
        "Wo": bf(np.random.standard_normal((E, E)) * 3.0 / np.sqrt(E) / t[:, None]),
        "bo": bf(np.random.standard_normal(E) * 0.1),
    }


def reference(logits, v, emb_rel_v, Wo, bo):
    a = f64(logits)
    e = np.exp(a - a.max(-1, keepdims=True))
    z = e.sum(-1, keepdims=True)
    ctx = mxq(e, 2, "e4m3") @ mxq(f64(v), 1, "e4m3")
    band = band_of(e)
    rv = f64(emb_rel_v)[0]
    rel = np.zeros_like(ctx)
    for j in range(NREL):
        rel = rel + band[:, :, j:j + 1] * rv[j][None, None, :]
    attn = (ctx + rel) / z
    merged = attn.reshape(B, H, L, D).transpose(0, 2, 1, 3).reshape(B, L, E)
    return (mxq(merged, 2, "e4m3") @ mxq(f64(Wo), 0, "e4m3")) + f64(bo)

@@ -1,0 +1,314 @@
+from contextlib import ExitStack
+
+import concourse.mybir as mybir
+from concourse.masks import make_identity
+
+F32 = mybir.dt.float32
+BF16 = mybir.dt.bfloat16
+U32 = mybir.dt.uint32
+U8 = mybir.dt.uint8
+FP8X4 = mybir.dt.float8_e4m3fn_x4
+ALU = mybir.AluOpType
+ACT = mybir.ActivationFunctionType
+AXIS = mybir.AxisListType
+
+P = 128
+PACK = 4
+K_PASS = P * PACK
+
+BATCH, HEADS, SEQ, HEAD_DIM, WINDOW = 4, 2, 1024, 256, 4
+FEATURES = HEADS * HEAD_DIM
+OFFSETS = 2 * WINDOW + 1
+SEQ_TILES = SEQ // P
+KEY_PASSES = SEQ // K_PASS
+
+CHUNK_TILES = 4
+CHUNK = CHUNK_TILES * P
+CHUNKS = SEQ // CHUNK
+PAIR = 2 * P
+SPLIT = 3
+BAND_SLOT = 16
+
+FLOPS = (
+    2 * BATCH * HEADS * SEQ * SEQ * HEAD_DIM
+    + 2 * BATCH * HEADS * SEQ * OFFSETS * HEAD_DIM
+    + 2 * BATCH * SEQ * FEATURES * FEATURES
+)
+
+
+def quantise(nc, grouped, codes, scales):
+    nc.vector.quantize_mx(out=codes.bitcast(FP8X4), scales=scales, in_=grouped)
+
+
+def transpose_pairs(nc, bank, rows_a, rows_b, first_word, identity):
+    for u in range(2):
+        words = slice(first_word + u * P, first_word + (u + 1) * P)
+        nc.tensor.transpose(out=bank[:, u, 0:P], in_=rows_a.bitcast(F32)[:, words], identity=identity)
+        nc.tensor.transpose(out=bank[:, u, P:PAIR], in_=rows_b.bitcast(F32)[:, words], identity=identity)
+
+
+def tile_vitsattention_pa_t_kernel(tc, logits, v, emb_rel_v, Wo, bo, out):
+    nc = tc.nc
+    with ExitStack() as stack:
+        const = stack.enter_context(tc.tile_pool(name="const", bufs=1))
+        loads = stack.enter_context(tc.tile_pool(name="loads", bufs=3))
+        work = stack.enter_context(tc.tile_pool(name="work", bufs=2))
+        small = stack.enter_context(tc.tile_pool(name="small", bufs=4))
+        psum_turn = stack.enter_context(tc.psum_pool(name="psum_turn", bufs=2))
+        psum_one = stack.enter_context(tc.psum_pool(name="psum_one", bufs=1))
+        psum_out = stack.enter_context(tc.psum_pool(name="psum_out", bufs=2))
+
+        identity_f32 = const.tile([P, P], F32)
+        make_identity(nc, identity_f32[:])
+        identity_bf16 = const.tile([P, P], BF16)
+        make_identity(nc, identity_bf16[:])
+
+        band_logits = const.tile([P, SEQ_TILES, BATCH * HEADS, BAND_SLOT], BF16)
+        nc.vector.memset(band_logits[:], 0.0)
+        flat = logits.rearrange("n q k -> n (q k)")
+        for i in range(SEQ_TILES):
+            first = 1 if i == 0 else 0
+            last = P - 1 if i == SEQ_TILES - 1 else P
+            start = (i * P + first) * (SEQ + 1) - WINDOW
+            windows = flat[:, start : start + (last - first) * (SEQ + 1)]
+            nc.scalar.dma_start(
+                out=band_logits[first:last, i, :, 0:OFFSETS],
+                in_=windows.rearrange("n (p c) -> p n c", c=SEQ + 1)[:, :, 0:OFFSETS],
+            )
+        nc.scalar.dma_start(
+            out=band_logits[0:1, 0, :, WINDOW:OFFSETS], in_=flat[:, 0 : WINDOW + 1].unsqueeze(0)
+        )
+        nc.scalar.dma_start(
+            out=band_logits[P - 1 : P, SEQ_TILES - 1, :, 0 : WINDOW + 1],
+            in_=flat[:, SEQ * SEQ - WINDOW - 1 : SEQ * SEQ].unsqueeze(0),
+        )
+
+        rel_values = const.tile([P, HEAD_DIM], BF16)
+        nc.vector.memset(rel_values[:], 0.0)
+        for piece in range(SPLIT):
+            nc.scalar.dma_start(
+                out=rel_values[piece * OFFSETS : (piece + 1) * OFFSETS, :], in_=emb_rel_v[0]
+            )
+        band_pieces = [
+            const.tile([P, CHUNK_TILES, P], BF16, name="band_pieces_%d" % k) for k in range(2)
+        ]
+        for k in range(2):
+            nc.vector.memset(band_pieces[k][:], 0.0)
+
+        w_rows = const.tile([P, PACK, FEATURES], BF16)
+        nc.scalar.dma_start(
+            out=w_rows[:].rearrange("p (u s) o -> p u s o", u=2),
+            in_=Wo.rearrange("(u p s) o -> p u s o", u=2, s=2),
+        )
+        w_grouped = const.tile([P, FEATURES, PACK], BF16, align_bytes=64)
+        nc.vector.tensor_copy(out=w_grouped[:], in_=w_rows[:].rearrange("p t o -> p o t"))
+        w_codes = const.tile([P, FEATURES], U32, align_bytes=64)
+        w_scales = const.tile([P, FEATURES], U8, align_bytes=64)
+        quantise(nc, w_grouped[:].rearrange("p o t -> p (o t)"), w_codes[:], w_scales[:])
+
+        bias_bf16 = const.tile([P, FEATURES], BF16)
+        nc.scalar.dma_start(out=bias_bf16[:], in_=bo.partition_broadcast(P))
+        bias = const.tile([P, FEATURES], F32)
+        nc.vector.tensor_copy(out=bias[:], in_=bias_bf16[:])
+
+        chunk_count = 0
+        for b in range(BATCH):
+            v_codes, v_scales = [], []
+            for h in range(HEADS):
+                v_rows = loads.tile([P, KEY_PASSES, PACK, HEAD_DIM], BF16, tag="v_rows")
+                nc.sync.dma_start(
+                    out=v_rows[:].rearrange("p g (u s) d -> p g u s d", u=2),
+                    in_=v[b * HEADS + h].rearrange("(g u p s) d -> p g u s d", g=KEY_PASSES, u=2, s=2),
+                )
+                v_grouped = work.tile([P, KEY_PASSES, HEAD_DIM, PACK], BF16, align_bytes=64, tag="v_grouped")
+                nc.vector.tensor_copy(out=v_grouped[:], in_=v_rows[:].rearrange("p g t d -> p g d t"))
+                codes = work.tile([P, KEY_PASSES, HEAD_DIM], U32, align_bytes=64, tag="v_codes", bufs=4)
+                scales = work.tile([P, KEY_PASSES, HEAD_DIM], U8, align_bytes=64, tag="v_scales", bufs=4)
+                quantise(
+                    nc,
+                    v_grouped[:].rearrange("p g d t -> p (g d t)"),
+                    codes[:].rearrange("p g d -> p (g d)"),
+                    scales[:].rearrange("p g d -> p (g d)"),
+                )
+                v_codes.append(codes)
+                v_scales.append(scales)
+
+            for c in range(CHUNKS):
+                rows = slice(c * CHUNK, (c + 1) * CHUNK)
+                merged = work.tile([P, CHUNK_TILES, FEATURES], BF16, tag="merged")
+                for h in range(HEADS):
+                    n = b * HEADS + h
+                    raw = loads.tile([P, CHUNK_TILES, SEQ], BF16, tag="raw")
+                    nc.sync.dma_start(out=raw[:], in_=logits[n, rows, :].rearrange("(i p) k -> p i k", p=P))
+
+                    fold = work.tile([P, CHUNK_TILES, SEQ // 2], BF16, tag="fold")
+                    nc.vector.tensor_tensor(
+                        out=fold[:], in0=raw[:, :, 0 : SEQ // 2], in1=raw[:, :, SEQ // 2 : SEQ], op=ALU.max
+                    )
+                    for width in (SEQ // 4, SEQ // 8):
+                        nc.vector.tensor_tensor(
+                            out=fold[:, :, 0:width],
+                            in0=fold[:, :, 0:width],
+                            in1=fold[:, :, width : 2 * width],
+                            op=ALU.max,
+                        )
+                    neg_max = small.tile([P, CHUNK_TILES], F32, tag="neg_max")
+                    nc.vector.tensor_reduce(
+                        out=neg_max[:], in_=fold[:, :, 0 : SEQ // 8], axis=AXIS.X, op=ALU.max, negate=True
+                    )
+
+                    e_rows = work.tile([P, CHUNK_TILES, SEQ], BF16, tag="e_rows")
+                    z = small.tile([P, CHUNK_TILES], F32, tag="z")
+                    for i in range(CHUNK_TILES):
+                        nc.scalar.activation(
+                            out=e_rows[:, i, :],
+                            in_=raw[:, i, :],
+                            func=ACT.Exp,
+                            bias=neg_max[:, i : i + 1],
+                            scale=1.0,
+                            accum_out=z[:, i : i + 1],
+                        )
+                    inv_z = small.tile([P, CHUNK_TILES], F32, tag="inv_z")
+                    nc.vector.reciprocal(out=inv_z[:], in_=z[:])
+
+                    band_shape = [P, CHUNK_TILES, OFFSETS]
+                    tiles = slice(c * CHUNK_TILES, (c + 1) * CHUNK_TILES)
+                    band = small.tile(band_shape, F32, tag="band")
+                    nc.gpsimd.tensor_tensor(
+                        out=band[:],
+                        in0=band_logits[:, tiles, n, 0:OFFSETS],
+                        in1=neg_max[:].unsqueeze(2).to_broadcast(band_shape),
+                        op=ALU.add,
+                    )
+                    nc.scalar.activation(out=band[:], in_=band[:], func=ACT.Exp)
+                    if c == 0:
+                        nc.gpsimd.affine_select(
+                            out=band[:, 0, :],
+                            in_=band[:, 0, :],
+                            pattern=[[1, OFFSETS]],
+                            compare_op=ALU.is_ge,
+                            fill=0.0,
+                            base=-WINDOW,
+                            channel_multiplier=1,
+                        )
+                    if c == CHUNKS - 1:
+                        nc.gpsimd.affine_select(
+                            out=band[:, CHUNK_TILES - 1, :],
+                            in_=band[:, CHUNK_TILES - 1, :],
+                            pattern=[[-1, OFFSETS]],
+                            compare_op=ALU.is_ge,
+                            fill=0.0,
+                            base=P - 1 + WINDOW,
+                            channel_multiplier=-1,
+                        )
+                    nc.gpsimd.tensor_tensor(
+                        out=band[:], in0=band[:], in1=inv_z[:].unsqueeze(2).to_broadcast(band_shape), op=ALU.mult
+                    )
+                    pieces = band_pieces[chunk_count % 2]
+                    rest = small.tile(band_shape, F32, tag="rest")
+                    nc.gpsimd.tensor_copy(out=pieces[:, :, 0:OFFSETS], in_=band[:])
+                    nc.gpsimd.tensor_tensor(out=rest[:], in0=band[:], in1=pieces[:, :, 0:OFFSETS], op=ALU.subtract)
+                    nc.gpsimd.tensor_copy(out=pieces[:, :, OFFSETS : 2 * OFFSETS], in_=rest[:])
+                    nc.gpsimd.tensor_tensor(
+                        out=pieces[:, :, 2 * OFFSETS : 3 * OFFSETS],
+                        in0=rest[:],
+                        in1=pieces[:, :, OFFSETS : 2 * OFFSETS],
+                        op=ALU.subtract,
+                    )
+                    band_bank = psum_one.tile([P, CHUNK_TILES, P], BF16, tag="band_bank")
+                    for i in range(CHUNK_TILES):
+                        nc.tensor.transpose(out=band_bank[:, i, :], in_=pieces[:, i, :], identity=identity_bf16[:])
+                    band_turned = work.tile([P, CHUNK_TILES, P], BF16, tag="band_turned")
+                    nc.scalar.copy(out=band_turned[:], in_=band_bank[:])
+
+                    e_words = work.tile([P, KEY_PASSES, CHUNK, 2], F32, align_bytes=64, tag="e_words")
+                    for g in range(KEY_PASSES):
+                        for pair in range(CHUNK_TILES // 2):
+                            e_bank = psum_turn.tile([P, 2, PAIR], F32, tag="e_bank")
+                            transpose_pairs(
+                                nc,
+                                e_bank,
+                                e_rows[:, 2 * pair, :],
+                                e_rows[:, 2 * pair + 1, :],
+                                g * K_PASS // 2,
+                                identity_f32[:],
+                            )
+                            copy = nc.vector.tensor_copy if g == 0 else nc.scalar.copy
+                            copy(
+                                out=e_words[:, g, pair * PAIR : (pair + 1) * PAIR, :],
+                                in_=e_bank[:].rearrange("p u q -> p q u"),
+                            )
+                    e_codes = work.tile([P, KEY_PASSES, CHUNK], U32, align_bytes=64, tag="e_codes")
+                    e_scales = work.tile([P, KEY_PASSES, CHUNK], U8, align_bytes=64, tag="e_scales")
+                    quantise(
+                        nc,
+                        e_words[:].rearrange("p g q u -> p (g q u)").bitcast(BF16),
+                        e_codes[:].rearrange("p g q -> p (g q)"),
+                        e_scales[:].rearrange("p g q -> p (g q)"),
+                    )
+
+                    for pair in range(CHUNK_TILES // 2):
+                        ctx_bank = psum_one.tile([P, 2, HEAD_DIM], F32, tag="ctx_bank")
+                        rel_bank = psum_one.tile([P, 2, HEAD_DIM], F32, tag="rel_bank")
+                        for a in range(2):
+                            i = 2 * pair + a
+                            queries = slice(i * P, (i + 1) * P)
+                            for g in range(KEY_PASSES):
+                                nc.tensor.matmul_mx(
+                                    out=ctx_bank[:, a, :],
+                                    lhsT=e_codes[:, g, queries].bitcast(FP8X4),
+                                    lhsT_scale=e_scales[:, g, queries],
+                                    rhs=v_codes[h][:, g, :].bitcast(FP8X4),
+                                    rhs_scale=v_scales[h][:, g, :],
+                                    start=(g == 0),
+                                    stop=(g == KEY_PASSES - 1),
+                                )
+                        for a in range(2):
+                            nc.tensor.matmul(
+                                out=rel_bank[:, a, :],
+                                lhsT=band_turned[:, 2 * pair + a, :],
+                                rhs=rel_values[:],
+                                start=True,
+                                stop=True,
+                            )
+                        rel = work.tile([P, 2, HEAD_DIM], F32, tag="rel")
+                        nc.scalar.copy(out=rel[:], in_=rel_bank[:])
+                        for a in range(2):
+                            i = 2 * pair + a
+                            nc.vector.scalar_tensor_tensor(
+                                out=merged[:, i, h * HEAD_DIM : (h + 1) * HEAD_DIM],
+                                in0=ctx_bank[:, a, :],
+                                scalar=inv_z[:, i : i + 1],
+                                in1=rel[:, a, :],
+                                op0=ALU.mult,
+                                op1=ALU.add,
+                            )
+                    chunk_count += 1
+
+                m_words = work.tile([P, CHUNK, 2], F32, align_bytes=64, tag="m_words")
+                for pair in range(CHUNK_TILES // 2):
+                    m_bank = psum_one.tile([P, 2, PAIR], F32, tag="m_bank")
+                    transpose_pairs(
+                        nc, m_bank, merged[:, 2 * pair, :], merged[:, 2 * pair + 1, :], 0, identity_f32[:]
+                    )
+                    nc.vector.tensor_copy(
+                        out=m_words[:, pair * PAIR : (pair + 1) * PAIR, :],
+                        in_=m_bank[:].rearrange("p u t -> p t u"),
+                    )
+                m_codes = work.tile([P, CHUNK], U32, align_bytes=64, tag="m_codes")
+                m_scales = work.tile([P, CHUNK], U8, align_bytes=64, tag="m_scales")
+                quantise(nc, m_words[:].rearrange("p t u -> p (t u)").bitcast(BF16), m_codes[:], m_scales[:])
+                result = work.tile([P, CHUNK_TILES, FEATURES], F32, tag="result")
+                for i in range(CHUNK_TILES):
+                    out_bank = psum_out.tile([P, FEATURES], F32, tag="out_bank")
+                    nc.tensor.matmul_mx(
+                        out=out_bank[:],
+                        lhsT=m_codes[:, i * P : (i + 1) * P].bitcast(FP8X4),
+                        lhsT_scale=m_scales[:, i * P : (i + 1) * P],
+                        rhs=w_codes[:].bitcast(FP8X4),
+                        rhs_scale=w_scales[:],
+                        start=True,
+                        stop=True,
+                    )
+                    nc.vector.tensor_tensor(out=result[:, i, :], in0=out_bank[:], in1=bias[:], op=ALU.add)
+                nc.sync.dma_start(out=out[b, rows, :].rearrange("(i p) o -> p i o", p=P), in_=result[:])

@@ -24,7 +24,10 @@ KEY_PASSES = SEQ // K_PASS
 
 CHUNK_TILES = 4
 CHUNK = CHUNK_TILES * P
-CHUNKS = SEQ // CHUNK
+HALVES = SEQ // CHUNK
+CHUNKS = BATCH * HEADS * HALVES
+GROUPS = CHUNKS // HEADS
+BANKS = KEY_PASSES * CHUNK_TILES // 2
 PAIR = 2 * P
 SPLIT = 3
 BAND_SLOT = 16
@@ -51,12 +54,11 @@ def tile_vitsattention_pa_t_kernel(tc, logits, v, emb_rel_v, Wo, bo, out):
     nc = tc.nc
     with ExitStack() as stack:
         const = stack.enter_context(tc.tile_pool(name="const", bufs=1))
-        loads = stack.enter_context(tc.tile_pool(name="loads", bufs=3))
+        loads = stack.enter_context(tc.tile_pool(name="loads", bufs=4))
         work = stack.enter_context(tc.tile_pool(name="work", bufs=2))
         small = stack.enter_context(tc.tile_pool(name="small", bufs=4))
-        psum_turn = stack.enter_context(tc.psum_pool(name="psum_turn", bufs=2))
+        psum_two = stack.enter_context(tc.psum_pool(name="psum_two", bufs=2))
         psum_one = stack.enter_context(tc.psum_pool(name="psum_one", bufs=1))
-        psum_out = stack.enter_context(tc.psum_pool(name="psum_out", bufs=2))
 
         identity_f32 = const.tile([P, P], F32)
         make_identity(nc, identity_f32[:])
@@ -65,22 +67,32 @@ def tile_vitsattention_pa_t_kernel(tc, logits, v, emb_rel_v, Wo, bo, out):
 
         band_logits = const.tile([P, SEQ_TILES, BATCH * HEADS, BAND_SLOT], BF16)
         nc.vector.memset(band_logits[:], 0.0)
-        flat = logits.rearrange("n q k -> n (q k)")
-        for i in range(SEQ_TILES):
-            first = 1 if i == 0 else 0
-            last = P - 1 if i == SEQ_TILES - 1 else P
-            start = (i * P + first) * (SEQ + 1) - WINDOW
-            windows = flat[:, start : start + (last - first) * (SEQ + 1)]
-            nc.scalar.dma_start(
-                out=band_logits[first:last, i, :, 0:OFFSETS],
-                in_=windows.rearrange("n (p c) -> p n c", c=SEQ + 1)[:, :, 0:OFFSETS],
-            )
+        NHEADS = BATCH * HEADS
+        MATRIX = SEQ * SEQ
+        LAST = SEQ_TILES - 1
+        by_head = logits.rearrange("n q k -> n (q k)")
+        flat = logits.rearrange("n q k -> (n q k)")
+
+        def load_windows(where, matrices, start, count):
+            rows = matrices[:, start : start + count * (SEQ + 1)].rearrange("n (p c) -> p n c", c=SEQ + 1)
+            nc.scalar.dma_start(out=where, in_=rows[:, :, 0:OFFSETS])
+
+        def from_element(start):
+            return flat[start : start + (NHEADS - 1) * MATRIX].rearrange("(n x) -> n x", x=MATRIX)
+
+        for i in range(1, LAST):
+            load_windows(band_logits[:, i, :, 0:OFFSETS], by_head, i * P * (SEQ + 1) - WINDOW, P)
+        load_windows(band_logits[:, 0, 1:NHEADS, 0:OFFSETS], from_element(MATRIX - WINDOW), 0, P)
+        load_windows(band_logits[1:P, 0, 0:1, 0:OFFSETS], by_head[0:1], SEQ + 1 - WINDOW, P - 1)
         nc.scalar.dma_start(
-            out=band_logits[0:1, 0, :, WINDOW:OFFSETS], in_=flat[:, 0 : WINDOW + 1].unsqueeze(0)
+            out=band_logits[0:1, 0, 0:1, WINDOW:OFFSETS], in_=by_head[0:1, 0 : WINDOW + 1].unsqueeze(0)
         )
+        last_start = LAST * P * (SEQ + 1) - WINDOW
+        load_windows(band_logits[:, LAST, 0 : NHEADS - 1, 0:OFFSETS], from_element(last_start), 0, P)
+        load_windows(band_logits[0 : P - 1, LAST, NHEADS - 1 : NHEADS, 0:OFFSETS], by_head[NHEADS - 1 : NHEADS], last_start, P - 1)
         nc.scalar.dma_start(
-            out=band_logits[P - 1 : P, SEQ_TILES - 1, :, 0 : WINDOW + 1],
-            in_=flat[:, SEQ * SEQ - WINDOW - 1 : SEQ * SEQ].unsqueeze(0),
+            out=band_logits[P - 1 : P, LAST, NHEADS - 1 : NHEADS, 0 : WINDOW + 1],
+            in_=by_head[NHEADS - 1 : NHEADS, MATRIX - WINDOW - 1 : MATRIX].unsqueeze(0),
         )
 
         rel_values = const.tile([P, HEAD_DIM], BF16)
@@ -100,215 +112,352 @@ def tile_vitsattention_pa_t_kernel(tc, logits, v, emb_rel_v, Wo, bo, out):
             out=w_rows[:].rearrange("p (u s) o -> p u s o", u=2),
             in_=Wo.rearrange("(u p s) o -> p u s o", u=2, s=2),
         )
-        w_grouped = const.tile([P, FEATURES, PACK], BF16, align_bytes=64)
-        nc.vector.tensor_copy(out=w_grouped[:], in_=w_rows[:].rearrange("p t o -> p o t"))
-        w_codes = const.tile([P, FEATURES], U32, align_bytes=64)
-        w_scales = const.tile([P, FEATURES], U8, align_bytes=64)
-        quantise(nc, w_grouped[:].rearrange("p o t -> p (o t)"), w_codes[:], w_scales[:])
-
         bias_bf16 = const.tile([P, FEATURES], BF16)
         nc.scalar.dma_start(out=bias_bf16[:], in_=bo.partition_broadcast(P))
+        w_codes = const.tile([P, FEATURES], U32, align_bytes=64)
+        w_scales = const.tile([P, FEATURES], U8, align_bytes=64)
         bias = const.tile([P, FEATURES], F32)
-        nc.vector.tensor_copy(out=bias[:], in_=bias_bf16[:])
 
-        chunk_count = 0
-        for b in range(BATCH):
-            v_codes, v_scales = [], []
-            for h in range(HEADS):
-                v_rows = loads.tile([P, KEY_PASSES, PACK, HEAD_DIM], BF16, tag="v_rows")
+        def prepare_weights():
+            w_grouped = const.tile([P, FEATURES, PACK], BF16, align_bytes=64)
+            nc.vector.tensor_copy(out=w_grouped[:], in_=w_rows[:].rearrange("p t o -> p o t"))
+            quantise(nc, w_grouped[:].rearrange("p o t -> p (o t)"), w_codes[:], w_scales[:])
+            nc.vector.tensor_copy(out=bias[:], in_=bias_bf16[:])
+
+        raw, v_rows, v_codes, v_scales = {}, {}, {}, {}
+        neg_max, band, e_rows, z, inv_z = {}, {}, {}, {}, {}
+        e_bank, e_words, e_codes, e_scales = {}, {}, {}, {}
+        band_bank, band_turned, ctx_bank, rel_bank, rel = {}, {}, {}, {}, {}
+        merged, m_bank, m_words, m_codes, m_scales, out_bank, result = {}, {}, {}, {}, {}, {}, {}
+        band_shape = [P, CHUNK_TILES, OFFSETS]
+
+        def head_of(k):
+            return (k // (HEADS * HALVES)) * HEADS + k % HEADS
+
+        def half_of(k):
+            return (k // HEADS) % HALVES
+
+        def rows_of(k):
+            return slice(half_of(k) * CHUNK, (half_of(k) + 1) * CHUNK)
+
+        def load(k):
+            n = head_of(k)
+            raw[k] = loads.tile([P, CHUNK_TILES, SEQ], BF16, name="raw", tag="raw")
+            nc.sync.dma_start(out=raw[k][:], in_=logits[n, rows_of(k), :].rearrange("(i p) k -> p i k", p=P))
+            if half_of(k) == 0:
+                v_rows[n] = loads.tile([P, KEY_PASSES, PACK, HEAD_DIM], BF16, name="v_rows", tag="v_rows", bufs=2)
                 nc.sync.dma_start(
-                    out=v_rows[:].rearrange("p g (u s) d -> p g u s d", u=2),
-                    in_=v[b * HEADS + h].rearrange("(g u p s) d -> p g u s d", g=KEY_PASSES, u=2, s=2),
+                    out=v_rows[n][:].rearrange("p g (u s) d -> p g u s d", u=2),
+                    in_=v[n].rearrange("(g u p s) d -> p g u s d", g=KEY_PASSES, u=2, s=2),
                 )
-                v_grouped = work.tile([P, KEY_PASSES, HEAD_DIM, PACK], BF16, align_bytes=64, tag="v_grouped")
-                nc.vector.tensor_copy(out=v_grouped[:], in_=v_rows[:].rearrange("p g t d -> p g d t"))
-                codes = work.tile([P, KEY_PASSES, HEAD_DIM], U32, align_bytes=64, tag="v_codes", bufs=4)
-                scales = work.tile([P, KEY_PASSES, HEAD_DIM], U8, align_bytes=64, tag="v_scales", bufs=4)
-                quantise(
-                    nc,
-                    v_grouped[:].rearrange("p g d t -> p (g d t)"),
-                    codes[:].rearrange("p g d -> p (g d)"),
-                    scales[:].rearrange("p g d -> p (g d)"),
+
+        def quantise_values(k):
+            if half_of(k) != 0:
+                return
+            n = head_of(k)
+            v_grouped = work.tile([P, KEY_PASSES, HEAD_DIM, PACK], BF16, align_bytes=64, tag="v_grouped")
+            nc.vector.tensor_copy(out=v_grouped[:], in_=v_rows[n][:].rearrange("p g t d -> p g d t"))
+            v_codes[n] = work.tile([P, KEY_PASSES, HEAD_DIM], U32, align_bytes=64, name="v_codes", tag="v_codes", bufs=4)
+            v_scales[n] = work.tile([P, KEY_PASSES, HEAD_DIM], U8, align_bytes=64, name="v_scales", tag="v_scales", bufs=4)
+            quantise(
+                nc,
+                v_grouped[:].rearrange("p g d t -> p (g d t)"),
+                v_codes[n][:].rearrange("p g d -> p (g d)"),
+                v_scales[n][:].rearrange("p g d -> p (g d)"),
+            )
+
+        def row_maximum(k):
+            fold = work.tile([P, CHUNK_TILES, SEQ // 2], BF16, tag="fold")
+            nc.vector.tensor_tensor(
+                out=fold[:], in0=raw[k][:, :, 0 : SEQ // 2], in1=raw[k][:, :, SEQ // 2 : SEQ], op=ALU.max
+            )
+            for width in (SEQ // 4, SEQ // 8):
+                nc.vector.tensor_tensor(
+                    out=fold[:, :, 0:width], in0=fold[:, :, 0:width], in1=fold[:, :, width : 2 * width], op=ALU.max
                 )
-                v_codes.append(codes)
-                v_scales.append(scales)
+            neg_max[k] = small.tile([P, CHUNK_TILES], F32, name="neg_max", tag="neg_max")
+            nc.vector.tensor_reduce(
+                out=neg_max[k][:], in_=fold[:, :, 0 : SEQ // 8], axis=AXIS.X, op=ALU.max, negate=True
+            )
+            tiles = slice(half_of(k) * CHUNK_TILES, (half_of(k) + 1) * CHUNK_TILES)
+            band[k] = small.tile(band_shape, F32, name="band", tag="band")
+            nc.gpsimd.tensor_tensor(
+                out=band[k][:],
+                in0=band_logits[:, tiles, head_of(k), 0:OFFSETS],
+                in1=neg_max[k][:].unsqueeze(2).to_broadcast(band_shape),
+                op=ALU.add,
+            )
 
-            for c in range(CHUNKS):
-                rows = slice(c * CHUNK, (c + 1) * CHUNK)
-                merged = work.tile([P, CHUNK_TILES, FEATURES], BF16, tag="merged")
-                for h in range(HEADS):
-                    n = b * HEADS + h
-                    raw = loads.tile([P, CHUNK_TILES, SEQ], BF16, tag="raw")
-                    nc.sync.dma_start(out=raw[:], in_=logits[n, rows, :].rearrange("(i p) k -> p i k", p=P))
+        def exponential(k, i):
+            if i == 0:
+                e_rows[k] = work.tile([P, CHUNK_TILES, SEQ], BF16, name="e_rows", tag="e_rows", bufs=3)
+                z[k] = small.tile([P, CHUNK_TILES], F32, name="z", tag="z")
+            nc.scalar.activation(
+                out=e_rows[k][:, i, :],
+                in_=raw[k][:, i, :],
+                func=ACT.Exp,
+                bias=neg_max[k][:, i : i + 1],
+                scale=1.0,
+                accum_out=z[k][:, i : i + 1],
+            )
 
-                    fold = work.tile([P, CHUNK_TILES, SEQ // 2], BF16, tag="fold")
-                    nc.vector.tensor_tensor(
-                        out=fold[:], in0=raw[:, :, 0 : SEQ // 2], in1=raw[:, :, SEQ // 2 : SEQ], op=ALU.max
-                    )
-                    for width in (SEQ // 4, SEQ // 8):
-                        nc.vector.tensor_tensor(
-                            out=fold[:, :, 0:width],
-                            in0=fold[:, :, 0:width],
-                            in1=fold[:, :, width : 2 * width],
-                            op=ALU.max,
-                        )
-                    neg_max = small.tile([P, CHUNK_TILES], F32, tag="neg_max")
-                    nc.vector.tensor_reduce(
-                        out=neg_max[:], in_=fold[:, :, 0 : SEQ // 8], axis=AXIS.X, op=ALU.max, negate=True
-                    )
+        def turn_e(k, bank):
+            pair, g = bank // KEY_PASSES, bank % KEY_PASSES
+            e_bank[k, bank] = psum_two.tile([P, 2, PAIR], F32, name="e_bank", tag="e_bank")
+            transpose_pairs(
+                nc,
+                e_bank[k, bank],
+                e_rows[k][:, 2 * pair, :],
+                e_rows[k][:, 2 * pair + 1, :],
+                g * K_PASS // 2,
+                identity_f32[:],
+            )
 
-                    e_rows = work.tile([P, CHUNK_TILES, SEQ], BF16, tag="e_rows")
-                    z = small.tile([P, CHUNK_TILES], F32, tag="z")
-                    for i in range(CHUNK_TILES):
-                        nc.scalar.activation(
-                            out=e_rows[:, i, :],
-                            in_=raw[:, i, :],
-                            func=ACT.Exp,
-                            bias=neg_max[:, i : i + 1],
-                            scale=1.0,
-                            accum_out=z[:, i : i + 1],
-                        )
-                    inv_z = small.tile([P, CHUNK_TILES], F32, tag="inv_z")
-                    nc.vector.reciprocal(out=inv_z[:], in_=z[:])
+        def empty_e(k, bank):
+            pair, g = bank // KEY_PASSES, bank % KEY_PASSES
+            if bank == 0:
+                e_words[k] = work.tile([P, KEY_PASSES, CHUNK, 2], F32, align_bytes=64, name="e_words", tag="e_words")
+            copy = nc.vector.tensor_copy if bank == BANKS - 1 else nc.scalar.copy
+            copy(
+                out=e_words[k][:, g, pair * PAIR : (pair + 1) * PAIR, :],
+                in_=e_bank[k, bank][:].rearrange("p u q -> p q u"),
+            )
 
-                    band_shape = [P, CHUNK_TILES, OFFSETS]
-                    tiles = slice(c * CHUNK_TILES, (c + 1) * CHUNK_TILES)
-                    band = small.tile(band_shape, F32, tag="band")
-                    nc.gpsimd.tensor_tensor(
-                        out=band[:],
-                        in0=band_logits[:, tiles, n, 0:OFFSETS],
-                        in1=neg_max[:].unsqueeze(2).to_broadcast(band_shape),
-                        op=ALU.add,
-                    )
-                    nc.scalar.activation(out=band[:], in_=band[:], func=ACT.Exp)
-                    if c == 0:
-                        nc.gpsimd.affine_select(
-                            out=band[:, 0, :],
-                            in_=band[:, 0, :],
-                            pattern=[[1, OFFSETS]],
-                            compare_op=ALU.is_ge,
-                            fill=0.0,
-                            base=-WINDOW,
-                            channel_multiplier=1,
-                        )
-                    if c == CHUNKS - 1:
-                        nc.gpsimd.affine_select(
-                            out=band[:, CHUNK_TILES - 1, :],
-                            in_=band[:, CHUNK_TILES - 1, :],
-                            pattern=[[-1, OFFSETS]],
-                            compare_op=ALU.is_ge,
-                            fill=0.0,
-                            base=P - 1 + WINDOW,
-                            channel_multiplier=-1,
-                        )
-                    nc.gpsimd.tensor_tensor(
-                        out=band[:], in0=band[:], in1=inv_z[:].unsqueeze(2).to_broadcast(band_shape), op=ALU.mult
-                    )
-                    pieces = band_pieces[chunk_count % 2]
-                    rest = small.tile(band_shape, F32, tag="rest")
-                    nc.gpsimd.tensor_copy(out=pieces[:, :, 0:OFFSETS], in_=band[:])
-                    nc.gpsimd.tensor_tensor(out=rest[:], in0=band[:], in1=pieces[:, :, 0:OFFSETS], op=ALU.subtract)
-                    nc.gpsimd.tensor_copy(out=pieces[:, :, OFFSETS : 2 * OFFSETS], in_=rest[:])
-                    nc.gpsimd.tensor_tensor(
-                        out=pieces[:, :, 2 * OFFSETS : 3 * OFFSETS],
-                        in0=rest[:],
-                        in1=pieces[:, :, OFFSETS : 2 * OFFSETS],
-                        op=ALU.subtract,
-                    )
-                    band_bank = psum_one.tile([P, CHUNK_TILES, P], BF16, tag="band_bank")
-                    for i in range(CHUNK_TILES):
-                        nc.tensor.transpose(out=band_bank[:, i, :], in_=pieces[:, i, :], identity=identity_bf16[:])
-                    band_turned = work.tile([P, CHUNK_TILES, P], BF16, tag="band_turned")
-                    nc.scalar.copy(out=band_turned[:], in_=band_bank[:])
+        def quantise_e(k):
+            e_codes[k] = work.tile([P, KEY_PASSES, CHUNK], U32, align_bytes=64, name="e_codes", tag="e_codes")
+            e_scales[k] = work.tile([P, KEY_PASSES, CHUNK], U8, align_bytes=64, name="e_scales", tag="e_scales")
+            quantise(
+                nc,
+                e_words[k][:].rearrange("p g q u -> p (g q u)").bitcast(BF16),
+                e_codes[k][:].rearrange("p g q -> p (g q)"),
+                e_scales[k][:].rearrange("p g q -> p (g q)"),
+            )
 
-                    e_words = work.tile([P, KEY_PASSES, CHUNK, 2], F32, align_bytes=64, tag="e_words")
+        def band_exponential(k):
+            nc.scalar.activation(out=band[k][:], in_=band[k][:], func=ACT.Exp)
+
+        def reciprocal(k):
+            inv_z[k] = small.tile([P, CHUNK_TILES], F32, name="inv_z", tag="inv_z")
+            nc.vector.reciprocal(out=inv_z[k][:], in_=z[k][:])
+
+        def cut_band(k):
+            if half_of(k) == 0:
+                nc.gpsimd.affine_select(
+                    out=band[k][:, 0, :],
+                    in_=band[k][:, 0, :],
+                    pattern=[[1, OFFSETS]],
+                    compare_op=ALU.is_ge,
+                    fill=0.0,
+                    base=-WINDOW,
+                    channel_multiplier=1,
+                )
+            if half_of(k) == HALVES - 1:
+                nc.gpsimd.affine_select(
+                    out=band[k][:, CHUNK_TILES - 1, :],
+                    in_=band[k][:, CHUNK_TILES - 1, :],
+                    pattern=[[-1, OFFSETS]],
+                    compare_op=ALU.is_ge,
+                    fill=0.0,
+                    base=P - 1 + WINDOW,
+                    channel_multiplier=-1,
+                )
+            nc.gpsimd.tensor_tensor(
+                out=band[k][:], in0=band[k][:], in1=inv_z[k][:].unsqueeze(2).to_broadcast(band_shape), op=ALU.mult
+            )
+            pieces = band_pieces[k % 2]
+            rest = small.tile(band_shape, F32, tag="rest")
+            nc.gpsimd.tensor_copy(out=pieces[:, :, 0:OFFSETS], in_=band[k][:])
+            nc.gpsimd.tensor_tensor(out=rest[:], in0=band[k][:], in1=pieces[:, :, 0:OFFSETS], op=ALU.subtract)
+            nc.gpsimd.tensor_copy(out=pieces[:, :, OFFSETS : 2 * OFFSETS], in_=rest[:])
+            nc.gpsimd.tensor_tensor(
+                out=pieces[:, :, 2 * OFFSETS : 3 * OFFSETS],
+                in0=rest[:],
+                in1=pieces[:, :, OFFSETS : 2 * OFFSETS],
+                op=ALU.subtract,
+            )
+
+        def turn_band(k):
+            band_bank[k] = psum_one.tile([P, CHUNK_TILES, P], BF16, name="band_bank", tag="band_bank")
+            for i in range(CHUNK_TILES):
+                nc.tensor.transpose(out=band_bank[k][:, i, :], in_=band_pieces[k % 2][:, i, :], identity=identity_bf16[:])
+
+        def empty_band(k):
+            band_turned[k] = work.tile([P, CHUNK_TILES, P], BF16, name="band_turned", tag="band_turned")
+            nc.scalar.copy(out=band_turned[k][:], in_=band_bank[k][:])
+
+        def relative(k, pair):
+            rel_bank[k, pair] = psum_one.tile([P, 2, HEAD_DIM], F32, name="rel_bank", tag="rel_bank")
+            for a in range(2):
+                nc.tensor.matmul(
+                    out=rel_bank[k, pair][:, a, :],
+                    lhsT=band_turned[k][:, 2 * pair + a, :],
+                    rhs=rel_values[:],
+                    start=True,
+                    stop=True,
+                )
+
+        def empty_relative(k, pair):
+            rel[k, pair] = work.tile([P, 2, HEAD_DIM], F32, name="rel", tag="rel", bufs=4)
+            nc.scalar.copy(out=rel[k, pair][:], in_=rel_bank[k, pair][:])
+
+        def attend(k):
+            n = head_of(k)
+            for pair in range(CHUNK_TILES // 2):
+                ctx_bank[k, pair] = psum_two.tile([P, 2, HEAD_DIM], F32, name="ctx_bank", tag="ctx_bank")
+                for a in range(2):
+                    queries = slice((2 * pair + a) * P, (2 * pair + a + 1) * P)
                     for g in range(KEY_PASSES):
-                        for pair in range(CHUNK_TILES // 2):
-                            e_bank = psum_turn.tile([P, 2, PAIR], F32, tag="e_bank")
-                            transpose_pairs(
-                                nc,
-                                e_bank,
-                                e_rows[:, 2 * pair, :],
-                                e_rows[:, 2 * pair + 1, :],
-                                g * K_PASS // 2,
-                                identity_f32[:],
-                            )
-                            copy = nc.vector.tensor_copy if g == 0 else nc.scalar.copy
-                            copy(
-                                out=e_words[:, g, pair * PAIR : (pair + 1) * PAIR, :],
-                                in_=e_bank[:].rearrange("p u q -> p q u"),
-                            )
-                    e_codes = work.tile([P, KEY_PASSES, CHUNK], U32, align_bytes=64, tag="e_codes")
-                    e_scales = work.tile([P, KEY_PASSES, CHUNK], U8, align_bytes=64, tag="e_scales")
-                    quantise(
-                        nc,
-                        e_words[:].rearrange("p g q u -> p (g q u)").bitcast(BF16),
-                        e_codes[:].rearrange("p g q -> p (g q)"),
-                        e_scales[:].rearrange("p g q -> p (g q)"),
-                    )
+                        nc.tensor.matmul_mx(
+                            out=ctx_bank[k, pair][:, a, :],
+                            lhsT=e_codes[k][:, g, queries].bitcast(FP8X4),
+                            lhsT_scale=e_scales[k][:, g, queries],
+                            rhs=v_codes[n][:, g, :].bitcast(FP8X4),
+                            rhs_scale=v_scales[n][:, g, :],
+                            start=(g == 0),
+                            stop=(g == KEY_PASSES - 1),
+                        )
 
-                    for pair in range(CHUNK_TILES // 2):
-                        ctx_bank = psum_one.tile([P, 2, HEAD_DIM], F32, tag="ctx_bank")
-                        rel_bank = psum_one.tile([P, 2, HEAD_DIM], F32, tag="rel_bank")
-                        for a in range(2):
-                            i = 2 * pair + a
-                            queries = slice(i * P, (i + 1) * P)
-                            for g in range(KEY_PASSES):
-                                nc.tensor.matmul_mx(
-                                    out=ctx_bank[:, a, :],
-                                    lhsT=e_codes[:, g, queries].bitcast(FP8X4),
-                                    lhsT_scale=e_scales[:, g, queries],
-                                    rhs=v_codes[h][:, g, :].bitcast(FP8X4),
-                                    rhs_scale=v_scales[h][:, g, :],
-                                    start=(g == 0),
-                                    stop=(g == KEY_PASSES - 1),
-                                )
-                        for a in range(2):
-                            nc.tensor.matmul(
-                                out=rel_bank[:, a, :],
-                                lhsT=band_turned[:, 2 * pair + a, :],
-                                rhs=rel_values[:],
-                                start=True,
-                                stop=True,
-                            )
-                        rel = work.tile([P, 2, HEAD_DIM], F32, tag="rel")
-                        nc.scalar.copy(out=rel[:], in_=rel_bank[:])
-                        for a in range(2):
-                            i = 2 * pair + a
-                            nc.vector.scalar_tensor_tensor(
-                                out=merged[:, i, h * HEAD_DIM : (h + 1) * HEAD_DIM],
-                                in0=ctx_bank[:, a, :],
-                                scalar=inv_z[:, i : i + 1],
-                                in1=rel[:, a, :],
-                                op0=ALU.mult,
-                                op1=ALU.add,
-                            )
-                    chunk_count += 1
+        def normalise(k):
+            j, h = k // HEADS, k % HEADS
+            if h == 0:
+                merged[j] = work.tile([P, CHUNK_TILES, FEATURES], BF16, name="merged", tag="merged")
+            for i in range(CHUNK_TILES):
+                nc.vector.scalar_tensor_tensor(
+                    out=merged[j][:, i, h * HEAD_DIM : (h + 1) * HEAD_DIM],
+                    in0=ctx_bank[k, i // 2][:, i % 2, :],
+                    scalar=inv_z[k][:, i : i + 1],
+                    in1=rel[k, i // 2][:, i % 2, :],
+                    op0=ALU.mult,
+                    op1=ALU.add,
+                )
 
-                m_words = work.tile([P, CHUNK, 2], F32, align_bytes=64, tag="m_words")
-                for pair in range(CHUNK_TILES // 2):
-                    m_bank = psum_one.tile([P, 2, PAIR], F32, tag="m_bank")
-                    transpose_pairs(
-                        nc, m_bank, merged[:, 2 * pair, :], merged[:, 2 * pair + 1, :], 0, identity_f32[:]
-                    )
-                    nc.vector.tensor_copy(
-                        out=m_words[:, pair * PAIR : (pair + 1) * PAIR, :],
-                        in_=m_bank[:].rearrange("p u t -> p t u"),
-                    )
-                m_codes = work.tile([P, CHUNK], U32, align_bytes=64, tag="m_codes")
-                m_scales = work.tile([P, CHUNK], U8, align_bytes=64, tag="m_scales")
-                quantise(nc, m_words[:].rearrange("p t u -> p (t u)").bitcast(BF16), m_codes[:], m_scales[:])
-                result = work.tile([P, CHUNK_TILES, FEATURES], F32, tag="result")
-                for i in range(CHUNK_TILES):
-                    out_bank = psum_out.tile([P, FEATURES], F32, tag="out_bank")
-                    nc.tensor.matmul_mx(
-                        out=out_bank[:],
-                        lhsT=m_codes[:, i * P : (i + 1) * P].bitcast(FP8X4),
-                        lhsT_scale=m_scales[:, i * P : (i + 1) * P],
-                        rhs=w_codes[:].bitcast(FP8X4),
-                        rhs_scale=w_scales[:],
-                        start=True,
-                        stop=True,
-                    )
-                    nc.vector.tensor_tensor(out=result[:, i, :], in0=out_bank[:], in1=bias[:], op=ALU.add)
-                nc.sync.dma_start(out=out[b, rows, :].rearrange("(i p) o -> p i o", p=P), in_=result[:])
+        def turn_merged(j, pair):
+            m_bank[j, pair] = psum_one.tile([P, 2, PAIR], F32, name="m_bank", tag="m_bank")
+            transpose_pairs(
+                nc, m_bank[j, pair], merged[j][:, 2 * pair, :], merged[j][:, 2 * pair + 1, :], 0, identity_f32[:]
+            )
+
+        def empty_merged(j, pair):
+            if pair == 0:
+                m_words[j] = work.tile([P, CHUNK, 2], F32, align_bytes=64, name="m_words", tag="m_words")
+            nc.scalar.copy(
+                out=m_words[j][:, pair * PAIR : (pair + 1) * PAIR, :],
+                in_=m_bank[j, pair][:].rearrange("p u t -> p t u"),
+            )
+
+        def quantise_merged(j):
+            m_codes[j] = work.tile([P, CHUNK], U32, align_bytes=64, name="m_codes", tag="m_codes")
+            m_scales[j] = work.tile([P, CHUNK], U8, align_bytes=64, name="m_scales", tag="m_scales")
+            quantise(nc, m_words[j][:].rearrange("p t u -> p (t u)").bitcast(BF16), m_codes[j][:], m_scales[j][:])
+            result[j] = work.tile([P, CHUNK_TILES, FEATURES], F32, name="result", tag="result")
+
+        def project(j, i):
+            out_bank[j, i] = psum_one.tile([P, FEATURES], F32, name="out_bank", tag="out_bank")
+            nc.tensor.matmul_mx(
+                out=out_bank[j, i][:],
+                lhsT=m_codes[j][:, i * P : (i + 1) * P].bitcast(FP8X4),
+                lhsT_scale=m_scales[j][:, i * P : (i + 1) * P],
+                rhs=w_codes[:].bitcast(FP8X4),
+                rhs_scale=w_scales[:],
+                start=True,
+                stop=True,
+            )
+
+        def add_bias(j, i):
+            nc.vector.tensor_tensor(out=result[j][:, i, :], in0=out_bank[j, i][:], in1=bias[:], op=ALU.add)
+
+        def store(j):
+            k = j * HEADS
+            nc.sync.dma_start(
+                out=out[k // (HEADS * HALVES), rows_of(k), :].rearrange("(i p) o -> p i o", p=P), in_=result[j][:]
+            )
+
+        def is_chunk(k):
+            return 0 <= k < CHUNKS
+
+        def is_group(j):
+            return 0 <= j < GROUPS
+
+        AHEAD = 3
+        with tc.manual_schedule():
+            for k in range(AHEAD):
+                load(k)
+            row_maximum(0)
+            prepare_weights()
+            for r in range(CHUNKS + 5):
+                now, turned, divided = r, r - 1, r - 2
+                t = (r - 4) // 2 if r % 2 == 0 and is_group((r - 4) // 2) else None
+                o = (r - 5) // 2 if is_group((r - 5) // 2) else None
+                tile_a = 2 * ((r - 5) % 2)
+
+                if is_chunk(r + AHEAD):
+                    load(r + AHEAD)
+                if is_chunk(r + 1):
+                    row_maximum(r + 1)
+                if is_chunk(divided):
+                    relative(divided, 0)
+                    attend(divided)
+
+                if is_chunk(now):
+                    exponential(now, 0)
+                if is_chunk(turned):
+                    empty_e(turned, 0)
+                    turn_e(turned, 2)
+                if is_chunk(divided):
+                    empty_relative(divided, 0)
+                    relative(divided, 1)
+                if t is not None:
+                    turn_merged(t, 0)
+                if o is not None:
+                    if tile_a == 0:
+                        quantise_merged(o)
+                    project(o, tile_a)
+
+                if is_chunk(now):
+                    exponential(now, 1)
+                if is_chunk(turned):
+                    empty_e(turned, 1)
+                    turn_e(turned, 3)
+                    turn_band(turned)
+                if is_chunk(divided):
+                    empty_relative(divided, 1)
+                if is_chunk(now):
+                    quantise_values(now)
+                if is_chunk(divided):
+                    normalise(divided)
+                if o is not None:
+                    add_bias(o, tile_a)
+
+                if is_chunk(now):
+                    exponential(now, 2)
+                if is_chunk(turned):
+                    empty_e(turned, 2)
+                if is_chunk(now):
+                    turn_e(now, 0)
+                if t is not None:
+                    empty_merged(t, 0)
+                    turn_merged(t, 1)
+                if o is not None:
+                    project(o, tile_a + 1)
+
+                if is_chunk(now):
+                    exponential(now, 3)
+                if is_chunk(turned):
+                    empty_e(turned, 3)
+                if is_chunk(now):
+                    turn_e(now, 1)
+                if is_chunk(turned):
+                    empty_band(turned)
+                if t is not None:
+                    empty_merged(t, 1)
+                if is_chunk(now):
+                    band_exponential(now)
+                if is_chunk(turned):
+                    quantise_e(turned)
+                if o is not None:
+                    add_bias(o, tile_a + 1)
+                if is_chunk(now):
+                    reciprocal(now)
+                    cut_band(now)
+                if o is not None and tile_a == 2:
+                    store(o)

@@ -29,7 +29,6 @@ CHUNKS = BATCH * HEADS * HALVES
 GROUPS = CHUNKS // HEADS
 BANKS = KEY_PASSES * CHUNK_TILES // 2
 PAIR = 2 * P
-SPLIT = 3
 BAND_SLOT = 16
 
 FLOPS = (
@@ -62,8 +61,6 @@ def tile_vitsattention_pa_t_kernel(tc, logits, v, emb_rel_v, Wo, bo, out):
 
         identity_f32 = const.tile([P, P], F32)
         make_identity(nc, identity_f32[:])
-        identity_bf16 = const.tile([P, P], BF16)
-        make_identity(nc, identity_bf16[:])
 
         band_logits = const.tile([P, SEQ_TILES, BATCH * HEADS, BAND_SLOT], BF16)
         nc.vector.memset(band_logits[:], 0.0)
@@ -75,37 +72,38 @@ def tile_vitsattention_pa_t_kernel(tc, logits, v, emb_rel_v, Wo, bo, out):
 
         def load_windows(where, matrices, start, count):
             rows = matrices[:, start : start + count * (SEQ + 1)].rearrange("n (p c) -> p n c", c=SEQ + 1)
-            nc.scalar.dma_start(out=where, in_=rows[:, :, 0:OFFSETS])
+            nc.sync.dma_start(out=where, in_=rows[:, :, 0:OFFSETS])
 
         def from_element(start):
             return flat[start : start + (NHEADS - 1) * MATRIX].rearrange("(n x) -> n x", x=MATRIX)
 
-        for i in range(1, LAST):
-            load_windows(band_logits[:, i, :, 0:OFFSETS], by_head, i * P * (SEQ + 1) - WINDOW, P)
-        load_windows(band_logits[:, 0, 1:NHEADS, 0:OFFSETS], from_element(MATRIX - WINDOW), 0, P)
-        load_windows(band_logits[1:P, 0, 0:1, 0:OFFSETS], by_head[0:1], SEQ + 1 - WINDOW, P - 1)
-        nc.scalar.dma_start(
-            out=band_logits[0:1, 0, 0:1, WINDOW:OFFSETS], in_=by_head[0:1, 0 : WINDOW + 1].unsqueeze(0)
-        )
-        last_start = LAST * P * (SEQ + 1) - WINDOW
-        load_windows(band_logits[:, LAST, 0 : NHEADS - 1, 0:OFFSETS], from_element(last_start), 0, P)
-        load_windows(band_logits[0 : P - 1, LAST, NHEADS - 1 : NHEADS, 0:OFFSETS], by_head[NHEADS - 1 : NHEADS], last_start, P - 1)
-        nc.scalar.dma_start(
-            out=band_logits[P - 1 : P, LAST, NHEADS - 1 : NHEADS, 0 : WINDOW + 1],
-            in_=by_head[NHEADS - 1 : NHEADS, MATRIX - WINDOW - 1 : MATRIX].unsqueeze(0),
-        )
-
-        rel_values = const.tile([P, HEAD_DIM], BF16)
-        nc.vector.memset(rel_values[:], 0.0)
-        for piece in range(SPLIT):
-            nc.scalar.dma_start(
-                out=rel_values[piece * OFFSETS : (piece + 1) * OFFSETS, :], in_=emb_rel_v[0]
+        def load_band():
+            for i in range(1, LAST):
+                load_windows(band_logits[:, i, :, 0:OFFSETS], by_head, i * P * (SEQ + 1) - WINDOW, P)
+            load_windows(band_logits[:, 0, 1:NHEADS, 0:OFFSETS], from_element(MATRIX - WINDOW), 0, P)
+            load_windows(band_logits[1:P, 0, 0:1, 0:OFFSETS], by_head[0:1], SEQ + 1 - WINDOW, P - 1)
+            nc.sync.dma_start(
+                out=band_logits[0:1, 0, 0:1, WINDOW:OFFSETS], in_=by_head[0:1, 0 : WINDOW + 1].unsqueeze(0)
             )
-        band_pieces = [
-            const.tile([P, CHUNK_TILES, P], BF16, name="band_pieces_%d" % k) for k in range(2)
+            last_start = LAST * P * (SEQ + 1) - WINDOW
+            load_windows(band_logits[:, LAST, 0 : NHEADS - 1, 0:OFFSETS], from_element(last_start), 0, P)
+            load_windows(
+                band_logits[0 : P - 1, LAST, NHEADS - 1 : NHEADS, 0:OFFSETS], by_head[NHEADS - 1 : NHEADS], last_start, P - 1
+            )
+            nc.sync.dma_start(
+                out=band_logits[P - 1 : P, LAST, NHEADS - 1 : NHEADS, 0 : WINDOW + 1],
+                in_=by_head[NHEADS - 1 : NHEADS, MATRIX - WINDOW - 1 : MATRIX].unsqueeze(0),
+            )
+
+        rel_rows = const.tile([P, HEAD_DIM], BF16)
+        nc.vector.memset(rel_rows[:], 0.0)
+        nc.scalar.dma_start(out=rel_rows[0:OFFSETS, :], in_=emb_rel_v[0])
+        rel_values = const.tile([P, HEAD_DIM], F32)
+        band_padded = [
+            const.tile([P, CHUNK_TILES, P], F32, name="band_padded_%d" % k) for k in range(2)
         ]
         for k in range(2):
-            nc.vector.memset(band_pieces[k][:], 0.0)
+            nc.vector.memset(band_padded[k][:], 0.0)
 
         w_rows = const.tile([P, PACK, FEATURES], BF16)
         nc.scalar.dma_start(
@@ -123,6 +121,7 @@ def tile_vitsattention_pa_t_kernel(tc, logits, v, emb_rel_v, Wo, bo, out):
             nc.vector.tensor_copy(out=w_grouped[:], in_=w_rows[:].rearrange("p t o -> p o t"))
             quantise(nc, w_grouped[:].rearrange("p o t -> p (o t)"), w_codes[:], w_scales[:])
             nc.vector.tensor_copy(out=bias[:], in_=bias_bf16[:])
+            nc.vector.tensor_copy(out=rel_values[:], in_=rel_rows[:])
 
         raw, v_rows, v_codes, v_scales = {}, {}, {}, {}
         neg_max, band, e_rows, z, inv_z = {}, {}, {}, {}, {}
@@ -168,17 +167,24 @@ def tile_vitsattention_pa_t_kernel(tc, logits, v, emb_rel_v, Wo, bo, out):
 
         def row_maximum(k):
             fold = work.tile([P, CHUNK_TILES, SEQ // 2], BF16, tag="fold")
-            nc.vector.tensor_tensor(
-                out=fold[:], in0=raw[k][:, :, 0 : SEQ // 2], in1=raw[k][:, :, SEQ // 2 : SEQ], op=ALU.max
-            )
-            for width in (SEQ // 4, SEQ // 8):
-                nc.vector.tensor_tensor(
-                    out=fold[:, :, 0:width], in0=fold[:, :, 0:width], in1=fold[:, :, width : 2 * width], op=ALU.max
-                )
             neg_max[k] = small.tile([P, CHUNK_TILES], F32, name="neg_max", tag="neg_max")
-            nc.vector.tensor_reduce(
-                out=neg_max[k][:], in_=fold[:, :, 0 : SEQ // 8], axis=AXIS.X, op=ALU.max, negate=True
-            )
+            pairs = (slice(0, 2), slice(2, 4))
+            for pair in pairs:
+                nc.vector.tensor_tensor(
+                    out=fold[:, pair, :], in0=raw[k][:, pair, 0 : SEQ // 2], in1=raw[k][:, pair, SEQ // 2 : SEQ], op=ALU.max
+                )
+            for width in (SEQ // 4, SEQ // 8):
+                for pair in pairs:
+                    nc.vector.tensor_tensor(
+                        out=fold[:, pair, 0:width],
+                        in0=fold[:, pair, 0:width],
+                        in1=fold[:, pair, width : 2 * width],
+                        op=ALU.max,
+                    )
+            for pair in pairs:
+                nc.vector.tensor_reduce(
+                    out=neg_max[k][:, pair], in_=fold[:, pair, 0 : SEQ // 8], axis=AXIS.X, op=ALU.max, negate=True
+                )
             tiles = slice(half_of(k) * CHUNK_TILES, (half_of(k) + 1) * CHUNK_TILES)
             band[k] = small.tile(band_shape, F32, name="band", tag="band")
             nc.gpsimd.tensor_tensor(
@@ -240,7 +246,7 @@ def tile_vitsattention_pa_t_kernel(tc, logits, v, emb_rel_v, Wo, bo, out):
             inv_z[k] = small.tile([P, CHUNK_TILES], F32, name="inv_z", tag="inv_z")
             nc.vector.reciprocal(out=inv_z[k][:], in_=z[k][:])
 
-        def cut_band(k):
+        def finish_band(k):
             if half_of(k) == 0:
                 nc.gpsimd.affine_select(
                     out=band[k][:, 0, :],
@@ -262,39 +268,28 @@ def tile_vitsattention_pa_t_kernel(tc, logits, v, emb_rel_v, Wo, bo, out):
                     channel_multiplier=-1,
                 )
             nc.gpsimd.tensor_tensor(
-                out=band[k][:], in0=band[k][:], in1=inv_z[k][:].unsqueeze(2).to_broadcast(band_shape), op=ALU.mult
-            )
-            pieces = band_pieces[k % 2]
-            rest = small.tile(band_shape, F32, tag="rest")
-            nc.gpsimd.tensor_copy(out=pieces[:, :, 0:OFFSETS], in_=band[k][:])
-            nc.gpsimd.tensor_tensor(out=rest[:], in0=band[k][:], in1=pieces[:, :, 0:OFFSETS], op=ALU.subtract)
-            nc.gpsimd.tensor_copy(out=pieces[:, :, OFFSETS : 2 * OFFSETS], in_=rest[:])
-            nc.gpsimd.tensor_tensor(
-                out=pieces[:, :, 2 * OFFSETS : 3 * OFFSETS],
-                in0=rest[:],
-                in1=pieces[:, :, OFFSETS : 2 * OFFSETS],
-                op=ALU.subtract,
+                out=band_padded[k % 2][:, :, 0:OFFSETS],
+                in0=band[k][:],
+                in1=inv_z[k][:].unsqueeze(2).to_broadcast(band_shape),
+                op=ALU.mult,
             )
 
         def turn_band(k):
-            band_bank[k] = psum_one.tile([P, CHUNK_TILES, P], BF16, name="band_bank", tag="band_bank")
+            band_bank[k] = psum_one.tile([P, CHUNK_TILES, P], F32, name="band_bank", tag="band_bank")
             for i in range(CHUNK_TILES):
-                nc.tensor.transpose(out=band_bank[k][:, i, :], in_=band_pieces[k % 2][:, i, :], identity=identity_bf16[:])
+                nc.tensor.transpose(out=band_bank[k][:, i, :], in_=band_padded[k % 2][:, i, :], identity=identity_f32[:])
 
         def empty_band(k):
-            band_turned[k] = work.tile([P, CHUNK_TILES, P], BF16, name="band_turned", tag="band_turned")
+            band_turned[k] = work.tile([P, CHUNK_TILES, P], F32, name="band_turned", tag="band_turned")
             nc.scalar.copy(out=band_turned[k][:], in_=band_bank[k][:])
 
-        def relative(k, pair):
-            rel_bank[k, pair] = psum_one.tile([P, 2, HEAD_DIM], F32, name="rel_bank", tag="rel_bank")
-            for a in range(2):
-                nc.tensor.matmul(
-                    out=rel_bank[k, pair][:, a, :],
-                    lhsT=band_turned[k][:, 2 * pair + a, :],
-                    rhs=rel_values[:],
-                    start=True,
-                    stop=True,
-                )
+        def relative(k, i):
+            pair = i // 2
+            if i % 2 == 0:
+                rel_bank[k, pair] = psum_one.tile([P, 2, HEAD_DIM], F32, name="rel_bank", tag="rel_bank")
+            nc.tensor.matmul(
+                out=rel_bank[k, pair][:, i % 2, :], lhsT=band_turned[k][:, i, :], rhs=rel_values[:], start=True, stop=True
+            )
 
         def empty_relative(k, pair):
             rel[k, pair] = work.tile([P, 2, HEAD_DIM], F32, name="rel", tag="rel", bufs=4)
@@ -366,10 +361,12 @@ def tile_vitsattention_pa_t_kernel(tc, logits, v, emb_rel_v, Wo, bo, out):
         def add_bias(j, i):
             nc.vector.tensor_tensor(out=result[j][:, i, :], in0=out_bank[j, i][:], in1=bias[:], op=ALU.add)
 
-        def store(j):
+        def store(j, pair):
             k = j * HEADS
+            first_row = half_of(k) * CHUNK + pair * PAIR
             nc.sync.dma_start(
-                out=out[k // (HEADS * HALVES), rows_of(k), :].rearrange("(i p) o -> p i o", p=P), in_=result[j][:]
+                out=out[k // (HEADS * HALVES), first_row : first_row + PAIR, :].rearrange("(i p) o -> p i o", p=P),
+                in_=result[j][:, 2 * pair : 2 * pair + 2, :],
             )
 
         def is_chunk(k):
@@ -380,7 +377,9 @@ def tile_vitsattention_pa_t_kernel(tc, logits, v, emb_rel_v, Wo, bo, out):
 
         AHEAD = 3
         with tc.manual_schedule():
-            for k in range(AHEAD):
+            load(0)
+            load_band()
+            for k in range(1, AHEAD):
                 load(k)
             row_maximum(0)
             prepare_weights()
@@ -395,7 +394,6 @@ def tile_vitsattention_pa_t_kernel(tc, logits, v, emb_rel_v, Wo, bo, out):
                 if is_chunk(r + 1):
                     row_maximum(r + 1)
                 if is_chunk(divided):
-                    relative(divided, 0)
                     attend(divided)
 
                 if is_chunk(now):
@@ -405,7 +403,7 @@ def tile_vitsattention_pa_t_kernel(tc, logits, v, emb_rel_v, Wo, bo, out):
                     turn_e(turned, 2)
                 if is_chunk(divided):
                     empty_relative(divided, 0)
-                    relative(divided, 1)
+                    relative(divided, 2)
                 if t is not None:
                     turn_merged(t, 0)
                 if o is not None:
@@ -415,12 +413,16 @@ def tile_vitsattention_pa_t_kernel(tc, logits, v, emb_rel_v, Wo, bo, out):
 
                 if is_chunk(now):
                     exponential(now, 1)
+                if is_chunk(divided):
+                    relative(divided, 3)
                 if is_chunk(turned):
+                    turn_band(turned)
                     empty_e(turned, 1)
                     turn_e(turned, 3)
-                    turn_band(turned)
                 if is_chunk(divided):
                     empty_relative(divided, 1)
+                if is_chunk(turned):
+                    empty_band(turned)
                 if is_chunk(now):
                     quantise_values(now)
                 if is_chunk(divided):
@@ -431,6 +433,7 @@ def tile_vitsattention_pa_t_kernel(tc, logits, v, emb_rel_v, Wo, bo, out):
                 if is_chunk(now):
                     exponential(now, 2)
                 if is_chunk(turned):
+                    relative(turned, 0)
                     empty_e(turned, 2)
                 if is_chunk(now):
                     turn_e(now, 0)
@@ -443,21 +446,19 @@ def tile_vitsattention_pa_t_kernel(tc, logits, v, emb_rel_v, Wo, bo, out):
                 if is_chunk(now):
                     exponential(now, 3)
                 if is_chunk(turned):
+                    relative(turned, 1)
                     empty_e(turned, 3)
                 if is_chunk(now):
                     turn_e(now, 1)
-                if is_chunk(turned):
-                    empty_band(turned)
                 if t is not None:
                     empty_merged(t, 1)
                 if is_chunk(now):
                     band_exponential(now)
-                if is_chunk(turned):
-                    quantise_e(turned)
                 if o is not None:
                     add_bias(o, tile_a + 1)
+                    store(o, tile_a // 2)
+                if is_chunk(turned):
+                    quantise_e(turned)
                 if is_chunk(now):
                     reciprocal(now)
-                    cut_band(now)
-                if o is not None and tile_a == 2:
-                    store(o)
+                    finish_band(now)

@@ -17,24 +17,28 @@ PACK = 4
 K_PASS = P * PACK
 
 BATCH, HEADS, SEQ, HEAD_DIM, WINDOW = 4, 2, 1024, 256, 4
+NHEADS = BATCH * HEADS
 FEATURES = HEADS * HEAD_DIM
 OFFSETS = 2 * WINDOW + 1
 SEQ_TILES = SEQ // P
 KEY_PASSES = SEQ // K_PASS
+MATRIX = SEQ * SEQ
 
 CHUNK_TILES = 4
 CHUNK = CHUNK_TILES * P
 HALVES = SEQ // CHUNK
-CHUNKS = BATCH * HEADS * HALVES
-GROUPS = CHUNKS // HEADS
-BANKS = KEY_PASSES * CHUNK_TILES // 2
+CHUNKS = NHEADS * HALVES
 PAIR = 2 * P
+BANKS = KEY_PASSES * CHUNK_TILES // 2
+SLABS = BATCH * SEQ // PAIR
+SPLIT = 3
 BAND_SLOT = 16
+AHEAD = 3
+SLAB_IN = 3
+SLAB_OUT = 4
 
 FLOPS = (
-    2 * BATCH * HEADS * SEQ * SEQ * HEAD_DIM
-    + 2 * BATCH * HEADS * SEQ * OFFSETS * HEAD_DIM
-    + 2 * BATCH * SEQ * FEATURES * FEATURES
+    2 * NHEADS * SEQ * SEQ * HEAD_DIM + 2 * NHEADS * SEQ * OFFSETS * HEAD_DIM + 2 * BATCH * SEQ * FEATURES * FEATURES
 )
 
 
@@ -53,7 +57,7 @@ def tile_vitsattention_pa_t_kernel(tc, logits, v, emb_rel_v, Wo, bo, out):
     nc = tc.nc
     with ExitStack() as stack:
         const = stack.enter_context(tc.tile_pool(name="const", bufs=1))
-        loads = stack.enter_context(tc.tile_pool(name="loads", bufs=4))
+        loads = stack.enter_context(tc.tile_pool(name="loads", bufs=AHEAD + 1))
         work = stack.enter_context(tc.tile_pool(name="work", bufs=2))
         small = stack.enter_context(tc.tile_pool(name="small", bufs=4))
         psum_two = stack.enter_context(tc.psum_pool(name="psum_two", bufs=2))
@@ -61,12 +65,11 @@ def tile_vitsattention_pa_t_kernel(tc, logits, v, emb_rel_v, Wo, bo, out):
 
         identity_f32 = const.tile([P, P], F32)
         make_identity(nc, identity_f32[:])
+        identity_bf16 = const.tile([P, P], BF16)
+        make_identity(nc, identity_bf16[:])
 
-        band_logits = const.tile([P, SEQ_TILES, BATCH * HEADS, BAND_SLOT], BF16)
+        band_logits = const.tile([P, SEQ_TILES, NHEADS, BAND_SLOT], BF16)
         nc.vector.memset(band_logits[:], 0.0)
-        NHEADS = BATCH * HEADS
-        MATRIX = SEQ * SEQ
-        LAST = SEQ_TILES - 1
         by_head = logits.rearrange("n q k -> n (q k)")
         flat = logits.rearrange("n q k -> (n q k)")
 
@@ -78,37 +81,33 @@ def tile_vitsattention_pa_t_kernel(tc, logits, v, emb_rel_v, Wo, bo, out):
             return flat[start : start + (NHEADS - 1) * MATRIX].rearrange("(n x) -> n x", x=MATRIX)
 
         def load_band():
-            for i in range(1, LAST):
-                load_windows(band_logits[:, i, :, 0:OFFSETS], by_head, i * P * (SEQ + 1) - WINDOW, P)
+            end = SEQ_TILES - 1
             load_windows(band_logits[:, 0, 1:NHEADS, 0:OFFSETS], from_element(MATRIX - WINDOW), 0, P)
             load_windows(band_logits[1:P, 0, 0:1, 0:OFFSETS], by_head[0:1], SEQ + 1 - WINDOW, P - 1)
             nc.sync.dma_start(
                 out=band_logits[0:1, 0, 0:1, WINDOW:OFFSETS], in_=by_head[0:1, 0 : WINDOW + 1].unsqueeze(0)
             )
-            last_start = LAST * P * (SEQ + 1) - WINDOW
-            load_windows(band_logits[:, LAST, 0 : NHEADS - 1, 0:OFFSETS], from_element(last_start), 0, P)
-            load_windows(
-                band_logits[0 : P - 1, LAST, NHEADS - 1 : NHEADS, 0:OFFSETS], by_head[NHEADS - 1 : NHEADS], last_start, P - 1
-            )
+            for i in range(1, end):
+                load_windows(band_logits[:, i, :, 0:OFFSETS], by_head, i * P * (SEQ + 1) - WINDOW, P)
+            start = end * P * (SEQ + 1) - WINDOW
+            load_windows(band_logits[:, end, 0 : NHEADS - 1, 0:OFFSETS], from_element(start), 0, P)
+            load_windows(band_logits[0 : P - 1, end, NHEADS - 1 : NHEADS, 0:OFFSETS], by_head[NHEADS - 1 : NHEADS], start, P - 1)
             nc.sync.dma_start(
-                out=band_logits[P - 1 : P, LAST, NHEADS - 1 : NHEADS, 0 : WINDOW + 1],
+                out=band_logits[P - 1 : P, end, NHEADS - 1 : NHEADS, 0 : WINDOW + 1],
                 in_=by_head[NHEADS - 1 : NHEADS, MATRIX - WINDOW - 1 : MATRIX].unsqueeze(0),
             )
 
-        rel_rows = const.tile([P, HEAD_DIM], BF16)
-        nc.vector.memset(rel_rows[:], 0.0)
-        nc.scalar.dma_start(out=rel_rows[0:OFFSETS, :], in_=emb_rel_v[0])
-        rel_values = const.tile([P, HEAD_DIM], F32)
-        band_padded = [
-            const.tile([P, CHUNK_TILES, P], F32, name="band_padded_%d" % k) for k in range(2)
-        ]
+        rel_values = const.tile([P, HEAD_DIM], BF16)
+        nc.vector.memset(rel_values[:], 0.0)
+        for piece in range(SPLIT):
+            nc.scalar.dma_start(out=rel_values[piece * OFFSETS : (piece + 1) * OFFSETS, :], in_=emb_rel_v[0])
+        band_pieces = [const.tile([P, CHUNK_TILES, P], BF16, name="band_pieces_%d" % k) for k in range(2)]
         for k in range(2):
-            nc.vector.memset(band_padded[k][:], 0.0)
+            nc.vector.memset(band_pieces[k][:], 0.0)
 
         w_rows = const.tile([P, PACK, FEATURES], BF16)
         nc.scalar.dma_start(
-            out=w_rows[:].rearrange("p (u s) o -> p u s o", u=2),
-            in_=Wo.rearrange("(u p s) o -> p u s o", u=2, s=2),
+            out=w_rows[:].rearrange("p (u s) o -> p u s o", u=2), in_=Wo.rearrange("(u p s) o -> p u s o", u=2, s=2)
         )
         bias_bf16 = const.tile([P, FEATURES], BF16)
         nc.scalar.dma_start(out=bias_bf16[:], in_=bo.partition_broadcast(P))
@@ -119,9 +118,8 @@ def tile_vitsattention_pa_t_kernel(tc, logits, v, emb_rel_v, Wo, bo, out):
         def prepare_weights():
             w_grouped = const.tile([P, FEATURES, PACK], BF16, align_bytes=64)
             nc.vector.tensor_copy(out=w_grouped[:], in_=w_rows[:].rearrange("p t o -> p o t"))
-            quantise(nc, w_grouped[:].rearrange("p o t -> p (o t)"), w_codes[:], w_scales[:])
             nc.vector.tensor_copy(out=bias[:], in_=bias_bf16[:])
-            nc.vector.tensor_copy(out=rel_values[:], in_=rel_rows[:])
+            quantise(nc, w_grouped[:].rearrange("p o t -> p (o t)"), w_codes[:], w_scales[:])
 
         raw, v_rows, v_codes, v_scales = {}, {}, {}, {}
         neg_max, band, e_rows, z, inv_z = {}, {}, {}, {}, {}
@@ -136,34 +134,25 @@ def tile_vitsattention_pa_t_kernel(tc, logits, v, emb_rel_v, Wo, bo, out):
         def half_of(k):
             return (k // HEADS) % HALVES
 
-        def rows_of(k):
-            return slice(half_of(k) * CHUNK, (half_of(k) + 1) * CHUNK)
-
         def load(k):
             n = head_of(k)
+            rows = slice(half_of(k) * CHUNK, (half_of(k) + 1) * CHUNK)
             raw[k] = loads.tile([P, CHUNK_TILES, SEQ], BF16, name="raw", tag="raw")
-            nc.sync.dma_start(out=raw[k][:], in_=logits[n, rows_of(k), :].rearrange("(i p) k -> p i k", p=P))
+            nc.sync.dma_start(out=raw[k][:], in_=logits[n, rows, :].rearrange("(i p) k -> p i k", p=P))
             if half_of(k) == 0:
-                v_rows[n] = loads.tile([P, KEY_PASSES, PACK, HEAD_DIM], BF16, name="v_rows", tag="v_rows", bufs=2)
+                v_rows[n] = loads.tile([P, KEY_PASSES, PACK, HEAD_DIM], BF16, name="v_rows", tag="v_rows", bufs=3)
                 nc.sync.dma_start(
                     out=v_rows[n][:].rearrange("p g (u s) d -> p g u s d", u=2),
                     in_=v[n].rearrange("(g u p s) d -> p g u s d", g=KEY_PASSES, u=2, s=2),
                 )
 
-        def quantise_values(k):
-            if half_of(k) != 0:
-                return
-            n = head_of(k)
-            v_grouped = work.tile([P, KEY_PASSES, HEAD_DIM, PACK], BF16, align_bytes=64, tag="v_grouped")
-            nc.vector.tensor_copy(out=v_grouped[:], in_=v_rows[n][:].rearrange("p g t d -> p g d t"))
-            v_codes[n] = work.tile([P, KEY_PASSES, HEAD_DIM], U32, align_bytes=64, name="v_codes", tag="v_codes", bufs=4)
-            v_scales[n] = work.tile([P, KEY_PASSES, HEAD_DIM], U8, align_bytes=64, name="v_scales", tag="v_scales", bufs=4)
-            quantise(
-                nc,
-                v_grouped[:].rearrange("p g d t -> p (g d t)"),
-                v_codes[n][:].rearrange("p g d -> p (g d)"),
-                v_scales[n][:].rearrange("p g d -> p (g d)"),
-            )
+        def prepare_values(n, g):
+            if g == 0:
+                v_codes[n] = work.tile([P, KEY_PASSES, HEAD_DIM], U32, align_bytes=64, name="v_codes", tag="v_codes", bufs=4)
+                v_scales[n] = work.tile([P, KEY_PASSES, HEAD_DIM], U8, align_bytes=64, name="v_scales", tag="v_scales", bufs=4)
+            v_grouped = work.tile([P, HEAD_DIM, PACK], BF16, align_bytes=64, tag="v_grouped")
+            nc.vector.tensor_copy(out=v_grouped[:], in_=v_rows[n][:, g, :, :].rearrange("p t d -> p d t"))
+            quantise(nc, v_grouped[:].rearrange("p d t -> p (d t)"), v_codes[n][:, g, :], v_scales[n][:, g, :])
 
         def row_maximum(k):
             fold = work.tile([P, CHUNK_TILES, SEQ // 2], BF16, tag="fold")
@@ -207,16 +196,15 @@ def tile_vitsattention_pa_t_kernel(tc, logits, v, emb_rel_v, Wo, bo, out):
                 accum_out=z[k][:, i : i + 1],
             )
 
+        def reciprocal(k):
+            inv_z[k] = small.tile([P, CHUNK_TILES], F32, name="inv_z", tag="inv_z")
+            nc.vector.reciprocal(out=inv_z[k][:], in_=z[k][:])
+
         def turn_e(k, bank):
             pair, g = bank // KEY_PASSES, bank % KEY_PASSES
             e_bank[k, bank] = psum_two.tile([P, 2, PAIR], F32, name="e_bank", tag="e_bank")
             transpose_pairs(
-                nc,
-                e_bank[k, bank],
-                e_rows[k][:, 2 * pair, :],
-                e_rows[k][:, 2 * pair + 1, :],
-                g * K_PASS // 2,
-                identity_f32[:],
+                nc, e_bank[k, bank], e_rows[k][:, 2 * pair, :], e_rows[k][:, 2 * pair + 1, :], g * K_PASS // 2, identity_f32[:]
             )
 
         def empty_e(k, bank):
@@ -224,10 +212,7 @@ def tile_vitsattention_pa_t_kernel(tc, logits, v, emb_rel_v, Wo, bo, out):
             if bank == 0:
                 e_words[k] = work.tile([P, KEY_PASSES, CHUNK, 2], F32, align_bytes=64, name="e_words", tag="e_words")
             copy = nc.vector.tensor_copy if bank == BANKS - 1 else nc.scalar.copy
-            copy(
-                out=e_words[k][:, g, pair * PAIR : (pair + 1) * PAIR, :],
-                in_=e_bank[k, bank][:].rearrange("p u q -> p q u"),
-            )
+            copy(out=e_words[k][:, g, pair * PAIR : (pair + 1) * PAIR, :], in_=e_bank[k, bank][:].rearrange("p u q -> p q u"))
 
         def quantise_e(k):
             e_codes[k] = work.tile([P, KEY_PASSES, CHUNK], U32, align_bytes=64, name="e_codes", tag="e_codes")
@@ -242,11 +227,7 @@ def tile_vitsattention_pa_t_kernel(tc, logits, v, emb_rel_v, Wo, bo, out):
         def band_exponential(k):
             nc.scalar.activation(out=band[k][:], in_=band[k][:], func=ACT.Exp)
 
-        def reciprocal(k):
-            inv_z[k] = small.tile([P, CHUNK_TILES], F32, name="inv_z", tag="inv_z")
-            nc.vector.reciprocal(out=inv_z[k][:], in_=z[k][:])
-
-        def finish_band(k):
+        def cut_band(k):
             if half_of(k) == 0:
                 nc.gpsimd.affine_select(
                     out=band[k][:, 0, :],
@@ -267,33 +248,38 @@ def tile_vitsattention_pa_t_kernel(tc, logits, v, emb_rel_v, Wo, bo, out):
                     base=P - 1 + WINDOW,
                     channel_multiplier=-1,
                 )
+            pieces = band_pieces[k % 2]
+            rest = small.tile(band_shape, F32, tag="rest")
+            nc.gpsimd.tensor_copy(out=pieces[:, :, 0:OFFSETS], in_=band[k][:])
+            nc.gpsimd.tensor_tensor(out=rest[:], in0=band[k][:], in1=pieces[:, :, 0:OFFSETS], op=ALU.subtract)
+            nc.gpsimd.tensor_copy(out=pieces[:, :, OFFSETS : 2 * OFFSETS], in_=rest[:])
             nc.gpsimd.tensor_tensor(
-                out=band_padded[k % 2][:, :, 0:OFFSETS],
-                in0=band[k][:],
-                in1=inv_z[k][:].unsqueeze(2).to_broadcast(band_shape),
-                op=ALU.mult,
+                out=pieces[:, :, 2 * OFFSETS : 3 * OFFSETS], in0=rest[:], in1=pieces[:, :, OFFSETS : 2 * OFFSETS], op=ALU.subtract
             )
 
         def turn_band(k):
-            band_bank[k] = psum_one.tile([P, CHUNK_TILES, P], F32, name="band_bank", tag="band_bank")
+            band_bank[k] = psum_one.tile([P, CHUNK_TILES, P], BF16, name="band_bank", tag="band_bank")
             for i in range(CHUNK_TILES):
-                nc.tensor.transpose(out=band_bank[k][:, i, :], in_=band_padded[k % 2][:, i, :], identity=identity_f32[:])
+                nc.tensor.transpose(out=band_bank[k][:, i, :], in_=band_pieces[k % 2][:, i, :], identity=identity_bf16[:])
 
         def empty_band(k):
-            band_turned[k] = work.tile([P, CHUNK_TILES, P], F32, name="band_turned", tag="band_turned")
+            band_turned[k] = work.tile([P, CHUNK_TILES, P], BF16, name="band_turned", tag="band_turned")
             nc.scalar.copy(out=band_turned[k][:], in_=band_bank[k][:])
 
-        def relative(k, i):
-            pair = i // 2
-            if i % 2 == 0:
-                rel_bank[k, pair] = psum_one.tile([P, 2, HEAD_DIM], F32, name="rel_bank", tag="rel_bank")
-            nc.tensor.matmul(
-                out=rel_bank[k, pair][:, i % 2, :], lhsT=band_turned[k][:, i, :], rhs=rel_values[:], start=True, stop=True
-            )
+        def relative(k, pair):
+            rel_bank[k, pair] = psum_one.tile([P, 2, HEAD_DIM], F32, name="rel_bank", tag="rel_bank")
+            for a in range(2):
+                nc.tensor.matmul(
+                    out=rel_bank[k, pair][:, a, :], lhsT=band_turned[k][:, 2 * pair + a, :], rhs=rel_values[:], start=True, stop=True
+                )
 
         def empty_relative(k, pair):
             rel[k, pair] = work.tile([P, 2, HEAD_DIM], F32, name="rel", tag="rel", bufs=4)
-            nc.scalar.copy(out=rel[k, pair][:], in_=rel_bank[k, pair][:])
+            for a in range(2):
+                i = 2 * pair + a
+                nc.scalar.activation(
+                    out=rel[k, pair][:, a, :], in_=rel_bank[k, pair][:, a, :], func=ACT.Copy, scale=inv_z[k][:, i : i + 1]
+                )
 
         def attend(k):
             n = head_of(k)
@@ -315,7 +301,7 @@ def tile_vitsattention_pa_t_kernel(tc, logits, v, emb_rel_v, Wo, bo, out):
         def normalise(k):
             j, h = k // HEADS, k % HEADS
             if h == 0:
-                merged[j] = work.tile([P, CHUNK_TILES, FEATURES], BF16, name="merged", tag="merged")
+                merged[j] = work.tile([P, CHUNK_TILES, FEATURES], BF16, name="merged", tag="merged", bufs=3)
             for i in range(CHUNK_TILES):
                 nc.vector.scalar_tensor_tensor(
                     out=merged[j][:, i, h * HEAD_DIM : (h + 1) * HEAD_DIM],
@@ -326,139 +312,125 @@ def tile_vitsattention_pa_t_kernel(tc, logits, v, emb_rel_v, Wo, bo, out):
                     op1=ALU.add,
                 )
 
-        def turn_merged(j, pair):
-            m_bank[j, pair] = psum_one.tile([P, 2, PAIR], F32, name="m_bank", tag="m_bank")
-            transpose_pairs(
-                nc, m_bank[j, pair], merged[j][:, 2 * pair, :], merged[j][:, 2 * pair + 1, :], 0, identity_f32[:]
-            )
+        def turn_merged(s):
+            j, pair = s // 2, s % 2
+            m_bank[s] = psum_one.tile([P, 2, PAIR], F32, name="m_bank", tag="m_bank")
+            transpose_pairs(nc, m_bank[s], merged[j][:, 2 * pair, :], merged[j][:, 2 * pair + 1, :], 0, identity_f32[:])
 
-        def empty_merged(j, pair):
-            if pair == 0:
-                m_words[j] = work.tile([P, CHUNK, 2], F32, align_bytes=64, name="m_words", tag="m_words")
-            nc.scalar.copy(
-                out=m_words[j][:, pair * PAIR : (pair + 1) * PAIR, :],
-                in_=m_bank[j, pair][:].rearrange("p u t -> p t u"),
-            )
+        def empty_merged(s):
+            m_words[s] = work.tile([P, PAIR, 2], F32, align_bytes=64, name="m_words", tag="m_words")
+            nc.scalar.copy(out=m_words[s][:], in_=m_bank[s][:].rearrange("p u t -> p t u"))
 
-        def quantise_merged(j):
-            m_codes[j] = work.tile([P, CHUNK], U32, align_bytes=64, name="m_codes", tag="m_codes")
-            m_scales[j] = work.tile([P, CHUNK], U8, align_bytes=64, name="m_scales", tag="m_scales")
-            quantise(nc, m_words[j][:].rearrange("p t u -> p (t u)").bitcast(BF16), m_codes[j][:], m_scales[j][:])
-            result[j] = work.tile([P, CHUNK_TILES, FEATURES], F32, name="result", tag="result")
+        def quantise_merged(s):
+            m_codes[s] = work.tile([P, PAIR], U32, align_bytes=64, name="m_codes", tag="m_codes")
+            m_scales[s] = work.tile([P, PAIR], U8, align_bytes=64, name="m_scales", tag="m_scales")
+            quantise(nc, m_words[s][:].rearrange("p t u -> p (t u)").bitcast(BF16), m_codes[s][:], m_scales[s][:])
+            result[s] = work.tile([P, 2, FEATURES], F32, name="result", tag="result", bufs=3)
 
-        def project(j, i):
-            out_bank[j, i] = psum_one.tile([P, FEATURES], F32, name="out_bank", tag="out_bank")
+        def project(s, a):
+            out_bank[s, a] = psum_one.tile([P, FEATURES], F32, name="out_bank", tag="out_bank")
             nc.tensor.matmul_mx(
-                out=out_bank[j, i][:],
-                lhsT=m_codes[j][:, i * P : (i + 1) * P].bitcast(FP8X4),
-                lhsT_scale=m_scales[j][:, i * P : (i + 1) * P],
+                out=out_bank[s, a][:],
+                lhsT=m_codes[s][:, a * P : (a + 1) * P].bitcast(FP8X4),
+                lhsT_scale=m_scales[s][:, a * P : (a + 1) * P],
                 rhs=w_codes[:].bitcast(FP8X4),
                 rhs_scale=w_scales[:],
                 start=True,
                 stop=True,
             )
 
-        def add_bias(j, i):
-            nc.vector.tensor_tensor(out=result[j][:, i, :], in0=out_bank[j, i][:], in1=bias[:], op=ALU.add)
+        def add_bias(s, a):
+            nc.vector.tensor_tensor(out=result[s][:, a, :], in0=out_bank[s, a][:], in1=bias[:], op=ALU.add)
 
-        def store(j, pair):
-            k = j * HEADS
-            first_row = half_of(k) * CHUNK + pair * PAIR
-            nc.sync.dma_start(
-                out=out[k // (HEADS * HALVES), first_row : first_row + PAIR, :].rearrange("(i p) o -> p i o", p=P),
-                in_=result[j][:, 2 * pair : 2 * pair + 2, :],
-            )
+        def store(s):
+            per_batch = SEQ // PAIR
+            rows = slice((s % per_batch) * PAIR, (s % per_batch + 1) * PAIR)
+            nc.sync.dma_start(out=out[s // per_batch, rows, :].rearrange("(a p) o -> p a o", p=P), in_=result[s][:])
 
         def is_chunk(k):
             return 0 <= k < CHUNKS
 
-        def is_group(j):
-            return 0 <= j < GROUPS
+        def is_slab(s):
+            return 0 <= s < SLABS
 
-        AHEAD = 3
+        def one_round(r):
+            ahead, now, turned, divided = r + 1, r, r - 1, r - 2
+            slab_in, slab_out = r - SLAB_IN, r - SLAB_OUT
+
+            if is_chunk(r + AHEAD):
+                load(r + AHEAD)
+            if is_slab(slab_out):
+                quantise_merged(slab_out)
+            if is_chunk(ahead):
+                row_maximum(ahead)
+                prepare_values(ahead // KEY_PASSES, ahead % KEY_PASSES)
+            if is_chunk(turned):
+                relative(turned, 0)
+            if is_chunk(divided):
+                attend(divided)
+
+            if is_chunk(now):
+                exponential(now, 0)
+            if is_chunk(turned):
+                empty_e(turned, 0)
+                turn_e(turned, 2)
+                empty_relative(turned, 0)
+                relative(turned, 1)
+            if is_slab(slab_out):
+                project(slab_out, 0)
+
+            if is_chunk(now):
+                exponential(now, 1)
+            if is_chunk(turned):
+                empty_e(turned, 1)
+                turn_e(turned, 3)
+            if is_chunk(now):
+                turn_band(now)
+            if is_chunk(turned):
+                empty_relative(turned, 1)
+            if is_chunk(divided):
+                normalise(divided)
+            if is_slab(slab_out):
+                add_bias(slab_out, 0)
+
+            if is_chunk(now):
+                exponential(now, 2)
+            if is_chunk(turned):
+                empty_e(turned, 2)
+            if is_chunk(now):
+                turn_e(now, 0)
+            if is_slab(slab_in):
+                turn_merged(slab_in)
+            if is_slab(slab_out):
+                project(slab_out, 1)
+
+            if is_chunk(now):
+                exponential(now, 3)
+            if is_chunk(turned):
+                empty_e(turned, 3)
+            if is_chunk(now):
+                turn_e(now, 1)
+                empty_band(now)
+            if is_slab(slab_in):
+                empty_merged(slab_in)
+            if is_chunk(ahead):
+                band_exponential(ahead)
+                cut_band(ahead)
+            if is_slab(slab_out):
+                add_bias(slab_out, 1)
+                store(slab_out)
+            if is_chunk(now):
+                reciprocal(now)
+            if is_chunk(turned):
+                quantise_e(turned)
+            if r == 0:
+                prepare_weights()
+
         with tc.manual_schedule():
             load(0)
             load_band()
-            for k in range(1, AHEAD):
-                load(k)
-            row_maximum(0)
-            prepare_weights()
-            for r in range(CHUNKS + 5):
-                now, turned, divided = r, r - 1, r - 2
-                t = (r - 4) // 2 if r % 2 == 0 and is_group((r - 4) // 2) else None
-                o = (r - 5) // 2 if is_group((r - 5) // 2) else None
-                tile_a = 2 * ((r - 5) % 2)
-
-                if is_chunk(r + AHEAD):
-                    load(r + AHEAD)
-                if is_chunk(r + 1):
-                    row_maximum(r + 1)
-                if is_chunk(divided):
-                    attend(divided)
-
-                if is_chunk(now):
-                    exponential(now, 0)
-                if is_chunk(turned):
-                    empty_e(turned, 0)
-                    turn_e(turned, 2)
-                if is_chunk(divided):
-                    empty_relative(divided, 0)
-                    relative(divided, 2)
-                if t is not None:
-                    turn_merged(t, 0)
-                if o is not None:
-                    if tile_a == 0:
-                        quantise_merged(o)
-                    project(o, tile_a)
-
-                if is_chunk(now):
-                    exponential(now, 1)
-                if is_chunk(divided):
-                    relative(divided, 3)
-                if is_chunk(turned):
-                    turn_band(turned)
-                    empty_e(turned, 1)
-                    turn_e(turned, 3)
-                if is_chunk(divided):
-                    empty_relative(divided, 1)
-                if is_chunk(turned):
-                    empty_band(turned)
-                if is_chunk(now):
-                    quantise_values(now)
-                if is_chunk(divided):
-                    normalise(divided)
-                if o is not None:
-                    add_bias(o, tile_a)
-
-                if is_chunk(now):
-                    exponential(now, 2)
-                if is_chunk(turned):
-                    relative(turned, 0)
-                    empty_e(turned, 2)
-                if is_chunk(now):
-                    turn_e(now, 0)
-                if t is not None:
-                    empty_merged(t, 0)
-                    turn_merged(t, 1)
-                if o is not None:
-                    project(o, tile_a + 1)
-
-                if is_chunk(now):
-                    exponential(now, 3)
-                if is_chunk(turned):
-                    relative(turned, 1)
-                    empty_e(turned, 3)
-                if is_chunk(now):
-                    turn_e(now, 1)
-                if t is not None:
-                    empty_merged(t, 1)
-                if is_chunk(now):
-                    band_exponential(now)
-                if o is not None:
-                    add_bias(o, tile_a + 1)
-                    store(o, tile_a // 2)
-                if is_chunk(turned):
-                    quantise_e(turned)
-                if is_chunk(now):
-                    reciprocal(now)
-                    finish_band(now)
+            load(1)
+            for r in range(-1, CHUNKS):
+                one_round(r)
+        for r in range(CHUNKS, SLABS + SLAB_OUT):
+            one_round(r)

@@ -20,7 +20,6 @@ BATCH, HEADS, SEQ, HEAD_DIM, WINDOW = 4, 2, 1024, 256, 4
 NHEADS = BATCH * HEADS
 FEATURES = HEADS * HEAD_DIM
 OFFSETS = 2 * WINDOW + 1
-SEQ_TILES = SEQ // P
 KEY_PASSES = SEQ // K_PASS
 MATRIX = SEQ * SEQ
 
@@ -68,35 +67,6 @@ def tile_vitsattention_pa_t_kernel(tc, logits, v, emb_rel_v, Wo, bo, out):
         identity_bf16 = const.tile([P, P], BF16)
         make_identity(nc, identity_bf16[:])
 
-        band_logits = const.tile([P, SEQ_TILES, NHEADS, BAND_SLOT], BF16)
-        nc.vector.memset(band_logits[:], 0.0)
-        by_head = logits.rearrange("n q k -> n (q k)")
-        flat = logits.rearrange("n q k -> (n q k)")
-
-        def load_windows(where, matrices, start, count):
-            rows = matrices[:, start : start + count * (SEQ + 1)].rearrange("n (p c) -> p n c", c=SEQ + 1)
-            nc.sync.dma_start(out=where, in_=rows[:, :, 0:OFFSETS])
-
-        def from_element(start):
-            return flat[start : start + (NHEADS - 1) * MATRIX].rearrange("(n x) -> n x", x=MATRIX)
-
-        def load_band():
-            end = SEQ_TILES - 1
-            load_windows(band_logits[:, 0, 1:NHEADS, 0:OFFSETS], from_element(MATRIX - WINDOW), 0, P)
-            load_windows(band_logits[1:P, 0, 0:1, 0:OFFSETS], by_head[0:1], SEQ + 1 - WINDOW, P - 1)
-            nc.sync.dma_start(
-                out=band_logits[0:1, 0, 0:1, WINDOW:OFFSETS], in_=by_head[0:1, 0 : WINDOW + 1].unsqueeze(0)
-            )
-            for i in range(1, end):
-                load_windows(band_logits[:, i, :, 0:OFFSETS], by_head, i * P * (SEQ + 1) - WINDOW, P)
-            start = end * P * (SEQ + 1) - WINDOW
-            load_windows(band_logits[:, end, 0 : NHEADS - 1, 0:OFFSETS], from_element(start), 0, P)
-            load_windows(band_logits[0 : P - 1, end, NHEADS - 1 : NHEADS, 0:OFFSETS], by_head[NHEADS - 1 : NHEADS], start, P - 1)
-            nc.sync.dma_start(
-                out=band_logits[P - 1 : P, end, NHEADS - 1 : NHEADS, 0 : WINDOW + 1],
-                in_=by_head[NHEADS - 1 : NHEADS, MATRIX - WINDOW - 1 : MATRIX].unsqueeze(0),
-            )
-
         rel_values = const.tile([P, HEAD_DIM], BF16)
         nc.vector.memset(rel_values[:], 0.0)
         for piece in range(SPLIT):
@@ -122,14 +92,17 @@ def tile_vitsattention_pa_t_kernel(tc, logits, v, emb_rel_v, Wo, bo, out):
             quantise(nc, w_grouped[:].rearrange("p o t -> p (o t)"), w_codes[:], w_scales[:])
 
         raw, v_rows, v_codes, v_scales = {}, {}, {}, {}
-        neg_max, band, e_rows, z, inv_z = {}, {}, {}, {}, {}
+        band_logits, neg_max, band, e_rows, z, inv_z = {}, {}, {}, {}, {}, {}
         e_bank, e_words, e_codes, e_scales = {}, {}, {}, {}
         band_bank, band_turned, ctx_bank, rel_bank, rel = {}, {}, {}, {}, {}
         merged, m_bank, m_words, m_codes, m_scales, out_bank, result = {}, {}, {}, {}, {}, {}, {}
         band_shape = [P, CHUNK_TILES, OFFSETS]
 
+        def batch_of(k):
+            return (k // (HEADS * HALVES) + 1) % BATCH
+
         def head_of(k):
-            return (k // (HEADS * HALVES)) * HEADS + k % HEADS
+            return batch_of(k) * HEADS + k % HEADS
 
         def half_of(k):
             return (k // HEADS) % HALVES
@@ -154,6 +127,34 @@ def tile_vitsattention_pa_t_kernel(tc, logits, v, emb_rel_v, Wo, bo, out):
             nc.vector.tensor_copy(out=v_grouped[:], in_=v_rows[n][:, g, :, :].rearrange("p t d -> p d t"))
             quantise(nc, v_grouped[:].rearrange("p d t -> p (d t)"), v_codes[n][:, g, :], v_scales[n][:, g, :])
 
+        def load_band(k):
+            flat = logits.rearrange("n q k -> (n q k)")
+            first_row = half_of(k) * CHUNK
+            start = head_of(k) * MATRIX + first_row * (SEQ + 1) - WINDOW
+            band_logits[k] = small.tile([P, CHUNK_TILES, BAND_SLOT], BF16, name="band_logits", tag="band_logits", bufs=AHEAD + 1)
+            slots = band_logits[k]
+
+            def load_windows(where, begin, tiles, rows):
+                source = flat[begin : begin + tiles * rows * (SEQ + 1)].rearrange("(i p c) -> p i c", p=rows, c=SEQ + 1)
+                nc.sync.dma_start(out=where, in_=source[:, :, 0:OFFSETS])
+
+            if start < 0:
+                nc.gpsimd.memset(slots[:], 0.0)
+                nc.sync.dma_start(out=slots[0:1, 0, WINDOW:OFFSETS], in_=flat[0 : WINDOW + 1].unsqueeze(0))
+                load_windows(slots[1:P, 0:1, 0:OFFSETS], start + SEQ + 1, 1, P - 1)
+                load_windows(slots[:, 1:CHUNK_TILES, 0:OFFSETS], start + P * (SEQ + 1), CHUNK_TILES - 1, P)
+            elif start + CHUNK * (SEQ + 1) > NHEADS * MATRIX:
+                end = CHUNK_TILES - 1
+                nc.gpsimd.memset(slots[:], 0.0)
+                load_windows(slots[:, 0:end, 0:OFFSETS], start, end, P)
+                load_windows(slots[0 : P - 1, end : end + 1, 0:OFFSETS], start + end * P * (SEQ + 1), 1, P - 1)
+                nc.sync.dma_start(
+                    out=slots[P - 1 : P, end, 0 : WINDOW + 1],
+                    in_=flat[NHEADS * MATRIX - WINDOW - 1 : NHEADS * MATRIX].unsqueeze(0),
+                )
+            else:
+                load_windows(slots[:, :, 0:OFFSETS], start, CHUNK_TILES, P)
+
         def row_maximum(k):
             fold = work.tile([P, CHUNK_TILES, SEQ // 2], BF16, tag="fold")
             neg_max[k] = small.tile([P, CHUNK_TILES], F32, name="neg_max", tag="neg_max")
@@ -174,11 +175,10 @@ def tile_vitsattention_pa_t_kernel(tc, logits, v, emb_rel_v, Wo, bo, out):
                 nc.vector.tensor_reduce(
                     out=neg_max[k][:, pair], in_=fold[:, pair, 0 : SEQ // 8], axis=AXIS.X, op=ALU.max, negate=True
                 )
-            tiles = slice(half_of(k) * CHUNK_TILES, (half_of(k) + 1) * CHUNK_TILES)
             band[k] = small.tile(band_shape, F32, name="band", tag="band")
             nc.gpsimd.tensor_tensor(
                 out=band[k][:],
-                in0=band_logits[:, tiles, head_of(k), 0:OFFSETS],
+                in0=band_logits[k][:, :, 0:OFFSETS],
                 in1=neg_max[k][:].unsqueeze(2).to_broadcast(band_shape),
                 op=ALU.add,
             )
@@ -345,7 +345,7 @@ def tile_vitsattention_pa_t_kernel(tc, logits, v, emb_rel_v, Wo, bo, out):
         def store(s):
             per_batch = SEQ // PAIR
             rows = slice((s % per_batch) * PAIR, (s % per_batch + 1) * PAIR)
-            nc.sync.dma_start(out=out[s // per_batch, rows, :].rearrange("(a p) o -> p a o", p=P), in_=result[s][:])
+            nc.sync.dma_start(out=out[batch_of(s), rows, :].rearrange("(a p) o -> p a o", p=P), in_=result[s][:])
 
         def is_chunk(k):
             return 0 <= k < CHUNKS
@@ -359,11 +359,12 @@ def tile_vitsattention_pa_t_kernel(tc, logits, v, emb_rel_v, Wo, bo, out):
 
             if is_chunk(r + AHEAD):
                 load(r + AHEAD)
+                load_band(r + AHEAD)
             if is_slab(slab_out):
                 quantise_merged(slab_out)
             if is_chunk(ahead):
                 row_maximum(ahead)
-                prepare_values(ahead // KEY_PASSES, ahead % KEY_PASSES)
+                prepare_values(batch_of(ahead) * HEADS + (ahead // KEY_PASSES) % HEADS, ahead % KEY_PASSES)
             if is_chunk(turned):
                 relative(turned, 0)
             if is_chunk(divided):
@@ -427,9 +428,9 @@ def tile_vitsattention_pa_t_kernel(tc, logits, v, emb_rel_v, Wo, bo, out):
                 prepare_weights()
 
         with tc.manual_schedule():
-            load(0)
-            load_band()
-            load(1)
+            for k in range(AHEAD - 1):
+                load(k)
+                load_band(k)
             for r in range(-1, CHUNKS):
                 one_round(r)
         for r in range(CHUNKS, SLABS + SLAB_OUT):

@@ -23,18 +23,16 @@ OFFSETS = 2 * WINDOW + 1
 KEY_PASSES = SEQ // K_PASS
 MATRIX = SEQ * SEQ
 
-CHUNK_TILES = 4
-CHUNK = CHUNK_TILES * P
-HALVES = SEQ // CHUNK
-CHUNKS = NHEADS * HALVES
-PAIR = 2 * P
-BANKS = KEY_PASSES * CHUNK_TILES // 2
-SLABS = BATCH * SEQ // PAIR
+TILES = 2
+ROWS = TILES * P
+SLABS_PER_BATCH = SEQ // ROWS
+SLABS = BATCH * SLABS_PER_BATCH
+PAIRS = SLABS * HEADS
+HALF_HEADS = NHEADS * KEY_PASSES
 SPLIT = 3
+BAND_ROWS = P // TILES
 BAND_SLOT = 16
-AHEAD = 3
-SLAB_IN = 3
-SLAB_OUT = 4
+AHEAD = 5
 
 FLOPS = (
     2 * NHEADS * SEQ * SEQ * HEAD_DIM + 2 * NHEADS * SEQ * OFFSETS * HEAD_DIM + 2 * BATCH * SEQ * FEATURES * FEATURES
@@ -43,13 +41,6 @@ FLOPS = (
 
 def quantise(nc, grouped, codes, scales):
     nc.vector.quantize_mx(out=codes.bitcast(FP8X4), scales=scales, in_=grouped)
-
-
-def transpose_pairs(nc, bank, rows_a, rows_b, first_word, identity):
-    for u in range(2):
-        words = slice(first_word + u * P, first_word + (u + 1) * P)
-        nc.tensor.transpose(out=bank[:, u, 0:P], in_=rows_a.bitcast(F32)[:, words], identity=identity)
-        nc.tensor.transpose(out=bank[:, u, P:PAIR], in_=rows_b.bitcast(F32)[:, words], identity=identity)
 
 
 def tile_vitsattention_pa_t_kernel(tc, logits, v, emb_rel_v, Wo, bo, out):
@@ -66,85 +57,82 @@ def tile_vitsattention_pa_t_kernel(tc, logits, v, emb_rel_v, Wo, bo, out):
         make_identity(nc, identity_f32[:])
         identity_bf16 = const.tile([P, P], BF16)
         make_identity(nc, identity_bf16[:])
-
-        rel_values = const.tile([P, HEAD_DIM], BF16)
+        rel_values = const.tile([P, TILES, HEAD_DIM], BF16)
         nc.vector.memset(rel_values[:], 0.0)
-        for piece in range(SPLIT):
-            nc.scalar.dma_start(out=rel_values[piece * OFFSETS : (piece + 1) * OFFSETS, :], in_=emb_rel_v[0])
-        band_pieces = [const.tile([P, CHUNK_TILES, P], BF16, name="band_pieces_%d" % k) for k in range(2)]
+        band_pieces = [const.tile([P, TILES, BAND_ROWS], BF16, name="band_pieces_%d" % k) for k in range(2)]
         for k in range(2):
             nc.vector.memset(band_pieces[k][:], 0.0)
-
+        ones = const.tile([P, P], BF16)
+        nc.vector.memset(ones[:], 1.0)
+        bias_row = const.tile([P, FEATURES], BF16)
+        nc.vector.memset(bias_row[:], 0.0)
+        bias = const.tile([P, FEATURES], F32)
         w_rows = const.tile([P, PACK, FEATURES], BF16)
-        nc.scalar.dma_start(
-            out=w_rows[:].rearrange("p (u s) o -> p u s o", u=2), in_=Wo.rearrange("(u p s) o -> p u s o", u=2, s=2)
-        )
-        bias_bf16 = const.tile([P, FEATURES], BF16)
-        nc.scalar.dma_start(out=bias_bf16[:], in_=bo.partition_broadcast(P))
+        w_grouped = const.tile([P, FEATURES, PACK], BF16, align_bytes=64)
         w_codes = const.tile([P, FEATURES], U32, align_bytes=64)
         w_scales = const.tile([P, FEATURES], U8, align_bytes=64)
-        bias = const.tile([P, FEATURES], F32)
 
-        def prepare_weights():
-            w_grouped = const.tile([P, FEATURES, PACK], BF16, align_bytes=64)
+        def load_constants():
+            for a in range(TILES):
+                for piece in range(SPLIT):
+                    row = a * BAND_ROWS + piece * OFFSETS
+                    nc.sync.dma_start(out=rel_values[row : row + OFFSETS, a, :], in_=emb_rel_v[0])
+            nc.sync.dma_start(out=bias_row[0:1, :], in_=bo.unsqueeze(0))
+            nc.sync.dma_start(
+                out=w_rows[:].rearrange("p (u s) o -> p u s o", u=2),
+                in_=Wo.rearrange("(u p s) o -> p u s o", u=2, s=2),
+            )
+
+        def group_weights():
             nc.vector.tensor_copy(out=w_grouped[:], in_=w_rows[:].rearrange("p t o -> p o t"))
-            nc.vector.tensor_copy(out=bias[:], in_=bias_bf16[:])
-            quantise(nc, w_grouped[:].rearrange("p o t -> p (o t)"), w_codes[:], w_scales[:])
 
-        raw, v_rows, v_codes, v_scales = {}, {}, {}, {}
-        band_logits, neg_max, band, e_rows, z, inv_z = {}, {}, {}, {}, {}, {}
+        def finish_weights():
+            bias_bank = psum_one.tile([P, FEATURES], F32, name="out_bank", tag="out_bank")
+            nc.tensor.matmul(out=bias_bank[:], lhsT=ones[:], rhs=bias_row[:], start=True, stop=True)
+            quantise(nc, w_grouped[:].rearrange("p o t -> p (o t)"), w_codes[:], w_scales[:])
+            nc.vector.tensor_copy(out=bias[:], in_=bias_bank[:])
+
+        raw, band_logits, v_rows, v_grouped, v_codes, v_scales = {}, {}, {}, {}, {}, {}
+        folded, neg_max, band, e_rows, z, inv_z = {}, {}, {}, {}, {}, {}
         e_bank, e_words, e_codes, e_scales = {}, {}, {}, {}
         band_bank, band_turned, ctx_bank, rel_bank, rel = {}, {}, {}, {}, {}
         merged, m_bank, m_words, m_codes, m_scales, out_bank, result = {}, {}, {}, {}, {}, {}, {}
-        band_shape = [P, CHUNK_TILES, OFFSETS]
+        band_shape = [P, TILES, OFFSETS]
 
-        def batch_of(k):
-            return (k // (HEADS * HALVES) + 1) % BATCH
+        def batch_of(s):
+            return (s // SLABS_PER_BATCH + 1) % BATCH
 
-        def head_of(k):
-            return batch_of(k) * HEADS + k % HEADS
+        def first_row_of(s):
+            return (s % SLABS_PER_BATCH) * ROWS
 
-        def half_of(k):
-            return (k // HEADS) % HALVES
+        def head_of(m):
+            return batch_of(m // HEADS) * HEADS + m % HEADS
 
-        def load(k):
-            n = head_of(k)
-            rows = slice(half_of(k) * CHUNK, (half_of(k) + 1) * CHUNK)
-            raw[k] = loads.tile([P, CHUNK_TILES, SEQ], BF16, name="raw", tag="raw")
-            nc.sync.dma_start(out=raw[k][:], in_=logits[n, rows, :].rearrange("(i p) k -> p i k", p=P))
-            if half_of(k) == 0:
-                v_rows[n] = loads.tile([P, KEY_PASSES, PACK, HEAD_DIM], BF16, name="v_rows", tag="v_rows", bufs=3)
-                nc.sync.dma_start(
-                    out=v_rows[n][:].rearrange("p g (u s) d -> p g u s d", u=2),
-                    in_=v[n].rearrange("(g u p s) d -> p g u s d", g=KEY_PASSES, u=2, s=2),
-                )
+        def head_of_piece(q):
+            return ((q // (HEADS * KEY_PASSES) + 1) % BATCH) * HEADS + (q // KEY_PASSES) % HEADS
 
-        def prepare_values(n, g):
-            if g == 0:
-                v_codes[n] = work.tile([P, KEY_PASSES, HEAD_DIM], U32, align_bytes=64, name="v_codes", tag="v_codes", bufs=4)
-                v_scales[n] = work.tile([P, KEY_PASSES, HEAD_DIM], U8, align_bytes=64, name="v_scales", tag="v_scales", bufs=4)
-            v_grouped = work.tile([P, HEAD_DIM, PACK], BF16, align_bytes=64, tag="v_grouped")
-            nc.vector.tensor_copy(out=v_grouped[:], in_=v_rows[n][:, g, :, :].rearrange("p t d -> p d t"))
-            quantise(nc, v_grouped[:].rearrange("p d t -> p (d t)"), v_codes[n][:, g, :], v_scales[n][:, g, :])
+        def load(m):
+            rows = slice(first_row_of(m // HEADS), first_row_of(m // HEADS) + ROWS)
+            raw[m] = loads.tile([P, TILES, SEQ], BF16, name="raw", tag="raw")
+            nc.sync.dma_start(out=raw[m][:], in_=logits[head_of(m), rows, :].rearrange("(a p) k -> p a k", p=P))
 
-        def load_band(k):
+        def load_band(m):
             flat = logits.rearrange("n q k -> (n q k)")
-            first_row = half_of(k) * CHUNK
-            start = head_of(k) * MATRIX + first_row * (SEQ + 1) - WINDOW
-            band_logits[k] = small.tile([P, CHUNK_TILES, BAND_SLOT], BF16, name="band_logits", tag="band_logits", bufs=AHEAD + 1)
-            slots = band_logits[k]
+            start = head_of(m) * MATRIX + first_row_of(m // HEADS) * (SEQ + 1) - WINDOW
+            band_logits[m] = small.tile([P, TILES, BAND_SLOT], BF16, name="band_logits", tag="band_logits", bufs=AHEAD + 1)
+            slots = band_logits[m]
 
             def load_windows(where, begin, tiles, rows):
-                source = flat[begin : begin + tiles * rows * (SEQ + 1)].rearrange("(i p c) -> p i c", p=rows, c=SEQ + 1)
+                source = flat[begin : begin + tiles * rows * (SEQ + 1)].rearrange("(a p c) -> p a c", p=rows, c=SEQ + 1)
                 nc.sync.dma_start(out=where, in_=source[:, :, 0:OFFSETS])
 
             if start < 0:
                 nc.gpsimd.memset(slots[:], 0.0)
                 nc.sync.dma_start(out=slots[0:1, 0, WINDOW:OFFSETS], in_=flat[0 : WINDOW + 1].unsqueeze(0))
                 load_windows(slots[1:P, 0:1, 0:OFFSETS], start + SEQ + 1, 1, P - 1)
-                load_windows(slots[:, 1:CHUNK_TILES, 0:OFFSETS], start + P * (SEQ + 1), CHUNK_TILES - 1, P)
-            elif start + CHUNK * (SEQ + 1) > NHEADS * MATRIX:
-                end = CHUNK_TILES - 1
+                load_windows(slots[:, 1:TILES, 0:OFFSETS], start + P * (SEQ + 1), TILES - 1, P)
+            elif start + ROWS * (SEQ + 1) > NHEADS * MATRIX:
+                end = TILES - 1
                 nc.gpsimd.memset(slots[:], 0.0)
                 load_windows(slots[:, 0:end, 0:OFFSETS], start, end, P)
                 load_windows(slots[0 : P - 1, end : end + 1, 0:OFFSETS], start + end * P * (SEQ + 1), 1, P - 1)
@@ -153,179 +141,200 @@ def tile_vitsattention_pa_t_kernel(tc, logits, v, emb_rel_v, Wo, bo, out):
                     in_=flat[NHEADS * MATRIX - WINDOW - 1 : NHEADS * MATRIX].unsqueeze(0),
                 )
             else:
-                load_windows(slots[:, :, 0:OFFSETS], start, CHUNK_TILES, P)
+                load_windows(slots[:, :, 0:OFFSETS], start, TILES, P)
 
-        def row_maximum(k):
-            fold = work.tile([P, CHUNK_TILES, SEQ // 2], BF16, tag="fold")
-            neg_max[k] = small.tile([P, CHUNK_TILES], F32, name="neg_max", tag="neg_max")
-            pairs = (slice(0, 2), slice(2, 4))
-            for pair in pairs:
-                nc.vector.tensor_tensor(
-                    out=fold[:, pair, :], in0=raw[k][:, pair, 0 : SEQ // 2], in1=raw[k][:, pair, SEQ // 2 : SEQ], op=ALU.max
-                )
-            for width in (SEQ // 4, SEQ // 8):
-                for pair in pairs:
-                    nc.vector.tensor_tensor(
-                        out=fold[:, pair, 0:width],
-                        in0=fold[:, pair, 0:width],
-                        in1=fold[:, pair, width : 2 * width],
-                        op=ALU.max,
-                    )
-            for pair in pairs:
-                nc.vector.tensor_reduce(
-                    out=neg_max[k][:, pair], in_=fold[:, pair, 0 : SEQ // 8], axis=AXIS.X, op=ALU.max, negate=True
-                )
-            band[k] = small.tile(band_shape, F32, name="band", tag="band")
+        def load_values(q):
+            n = head_of_piece(q)
+            v_rows[n] = loads.tile([P, KEY_PASSES, PACK, HEAD_DIM], BF16, name="v_rows", tag="v_rows", bufs=3)
+            nc.sync.dma_start(
+                out=v_rows[n][:].rearrange("p g (u s) d -> p g u s d", u=2),
+                in_=v[n].rearrange("(g u p s) d -> p g u s d", g=KEY_PASSES, u=2, s=2),
+            )
+
+        def group_values(q):
+            v_grouped[q] = work.tile([P, HEAD_DIM, PACK], BF16, align_bytes=64, name="v_grouped", tag="v_grouped", bufs=3)
+            nc.vector.tensor_copy(
+                out=v_grouped[q][:], in_=v_rows[head_of_piece(q)][:, q % KEY_PASSES, :, :].rearrange("p t d -> p d t")
+            )
+
+        def quantise_values(q):
+            n, g = head_of_piece(q), q % KEY_PASSES
+            if g == 0:
+                v_codes[n] = work.tile([P, KEY_PASSES, HEAD_DIM], U32, align_bytes=64, name="v_codes", tag="v_codes", bufs=4)
+                v_scales[n] = work.tile([P, KEY_PASSES, HEAD_DIM], U8, align_bytes=64, name="v_scales", tag="v_scales", bufs=4)
+            quantise(nc, v_grouped[q][:].rearrange("p d t -> p (d t)"), v_codes[n][:, g, :], v_scales[n][:, g, :])
+
+        def fold(m, width):
+            if width == SEQ // 2:
+                folded[m] = work.tile([P, TILES, SEQ // 2], BF16, name="folded", tag="folded")
+            source = raw[m] if width == SEQ // 2 else folded[m]
+            nc.vector.tensor_tensor(
+                out=folded[m][:, :, 0:width], in0=source[:, :, 0:width], in1=source[:, :, width : 2 * width], op=ALU.max
+            )
+
+        def row_maximum(m):
+            neg_max[m] = small.tile([P, TILES], F32, name="neg_max", tag="neg_max")
+            nc.vector.tensor_reduce(
+                out=neg_max[m][:], in_=folded[m][:, :, 0 : SEQ // 8], axis=AXIS.X, op=ALU.max, negate=True
+            )
+            band[m] = small.tile(band_shape, F32, name="band", tag="band")
             nc.gpsimd.tensor_tensor(
-                out=band[k][:],
-                in0=band_logits[k][:, :, 0:OFFSETS],
-                in1=neg_max[k][:].unsqueeze(2).to_broadcast(band_shape),
+                out=band[m][:],
+                in0=band_logits[m][:, :, 0:OFFSETS],
+                in1=neg_max[m][:].unsqueeze(2).to_broadcast(band_shape),
                 op=ALU.add,
             )
 
-        def exponential(k, i):
-            if i == 0:
-                e_rows[k] = work.tile([P, CHUNK_TILES, SEQ], BF16, name="e_rows", tag="e_rows", bufs=3)
-                z[k] = small.tile([P, CHUNK_TILES], F32, name="z", tag="z")
+        def exponential(m, a):
+            if a == 0:
+                e_rows[m] = work.tile([P, TILES, SEQ], BF16, name="e_rows", tag="e_rows", bufs=3)
+                z[m] = small.tile([P, TILES], F32, name="z", tag="z")
             nc.scalar.activation(
-                out=e_rows[k][:, i, :],
-                in_=raw[k][:, i, :],
+                out=e_rows[m][:, a, :],
+                in_=raw[m][:, a, :],
                 func=ACT.Exp,
-                bias=neg_max[k][:, i : i + 1],
+                bias=neg_max[m][:, a : a + 1],
                 scale=1.0,
-                accum_out=z[k][:, i : i + 1],
+                accum_out=z[m][:, a : a + 1],
             )
 
-        def reciprocal(k):
-            inv_z[k] = small.tile([P, CHUNK_TILES], F32, name="inv_z", tag="inv_z")
-            nc.vector.reciprocal(out=inv_z[k][:], in_=z[k][:])
+        def reciprocal(m):
+            inv_z[m] = small.tile([P, TILES], F32, name="inv_z", tag="inv_z")
+            nc.vector.reciprocal(out=inv_z[m][:], in_=z[m][:])
 
-        def turn_e(k, bank):
-            pair, g = bank // KEY_PASSES, bank % KEY_PASSES
-            e_bank[k, bank] = psum_two.tile([P, 2, PAIR], F32, name="e_bank", tag="e_bank")
-            transpose_pairs(
-                nc, e_bank[k, bank], e_rows[k][:, 2 * pair, :], e_rows[k][:, 2 * pair + 1, :], g * K_PASS // 2, identity_f32[:]
-            )
+        def turn_e(m, a):
+            e_bank[m, a] = psum_two.tile([P, KEY_PASSES, 2, P], F32, name="e_bank", tag="e_bank")
+            words = e_rows[m][:, a, :].bitcast(F32)
+            for g in range(KEY_PASSES):
+                for u in range(2):
+                    first = (2 * g + u) * P
+                    nc.tensor.transpose(
+                        out=e_bank[m, a][:, g, u, :], in_=words[:, first : first + P], identity=identity_f32[:]
+                    )
 
-        def empty_e(k, bank):
-            pair, g = bank // KEY_PASSES, bank % KEY_PASSES
-            if bank == 0:
-                e_words[k] = work.tile([P, KEY_PASSES, CHUNK, 2], F32, align_bytes=64, name="e_words", tag="e_words")
-            copy = nc.vector.tensor_copy if bank == BANKS - 1 else nc.scalar.copy
-            copy(out=e_words[k][:, g, pair * PAIR : (pair + 1) * PAIR, :], in_=e_bank[k, bank][:].rearrange("p u q -> p q u"))
+        def empty_e(m, a, copy):
+            if a == 0:
+                e_words[m] = work.tile([P, KEY_PASSES, ROWS, 2], F32, align_bytes=64, name="e_words", tag="e_words")
+            copy(out=e_words[m][:, :, a * P : (a + 1) * P, :], in_=e_bank[m, a][:].rearrange("p g u q -> p g q u"))
 
-        def quantise_e(k):
-            e_codes[k] = work.tile([P, KEY_PASSES, CHUNK], U32, align_bytes=64, name="e_codes", tag="e_codes")
-            e_scales[k] = work.tile([P, KEY_PASSES, CHUNK], U8, align_bytes=64, name="e_scales", tag="e_scales")
+        def quantise_e(m):
+            e_codes[m] = work.tile([P, KEY_PASSES, ROWS], U32, align_bytes=64, name="e_codes", tag="e_codes")
+            e_scales[m] = work.tile([P, KEY_PASSES, ROWS], U8, align_bytes=64, name="e_scales", tag="e_scales")
             quantise(
                 nc,
-                e_words[k][:].rearrange("p g q u -> p (g q u)").bitcast(BF16),
-                e_codes[k][:].rearrange("p g q -> p (g q)"),
-                e_scales[k][:].rearrange("p g q -> p (g q)"),
+                e_words[m][:].rearrange("p g q u -> p (g q u)").bitcast(BF16),
+                e_codes[m][:].rearrange("p g q -> p (g q)"),
+                e_scales[m][:].rearrange("p g q -> p (g q)"),
             )
 
-        def band_exponential(k):
-            nc.scalar.activation(out=band[k][:], in_=band[k][:], func=ACT.Exp)
+        def band_exponential(m):
+            nc.scalar.activation(out=band[m][:], in_=band[m][:], func=ACT.Exp)
 
-        def cut_band(k):
-            if half_of(k) == 0:
+        def cut_band(m):
+            first_row = first_row_of(m // HEADS)
+            if first_row == 0:
                 nc.gpsimd.affine_select(
-                    out=band[k][:, 0, :],
-                    in_=band[k][:, 0, :],
+                    out=band[m][:, 0, :],
+                    in_=band[m][:, 0, :],
                     pattern=[[1, OFFSETS]],
                     compare_op=ALU.is_ge,
                     fill=0.0,
                     base=-WINDOW,
                     channel_multiplier=1,
                 )
-            if half_of(k) == HALVES - 1:
+            if first_row == SEQ - ROWS:
                 nc.gpsimd.affine_select(
-                    out=band[k][:, CHUNK_TILES - 1, :],
-                    in_=band[k][:, CHUNK_TILES - 1, :],
+                    out=band[m][:, TILES - 1, :],
+                    in_=band[m][:, TILES - 1, :],
                     pattern=[[-1, OFFSETS]],
                     compare_op=ALU.is_ge,
                     fill=0.0,
                     base=P - 1 + WINDOW,
                     channel_multiplier=-1,
                 )
-            pieces = band_pieces[k % 2]
+            pieces = band_pieces[m % 2]
             rest = small.tile(band_shape, F32, tag="rest")
-            nc.gpsimd.tensor_copy(out=pieces[:, :, 0:OFFSETS], in_=band[k][:])
-            nc.gpsimd.tensor_tensor(out=rest[:], in0=band[k][:], in1=pieces[:, :, 0:OFFSETS], op=ALU.subtract)
+            nc.gpsimd.tensor_copy(out=pieces[:, :, 0:OFFSETS], in_=band[m][:])
+            nc.gpsimd.tensor_tensor(out=rest[:], in0=band[m][:], in1=pieces[:, :, 0:OFFSETS], op=ALU.subtract)
             nc.gpsimd.tensor_copy(out=pieces[:, :, OFFSETS : 2 * OFFSETS], in_=rest[:])
             nc.gpsimd.tensor_tensor(
                 out=pieces[:, :, 2 * OFFSETS : 3 * OFFSETS], in0=rest[:], in1=pieces[:, :, OFFSETS : 2 * OFFSETS], op=ALU.subtract
             )
 
-        def turn_band(k):
-            band_bank[k] = psum_one.tile([P, CHUNK_TILES, P], BF16, name="band_bank", tag="band_bank")
-            for i in range(CHUNK_TILES):
-                nc.tensor.transpose(out=band_bank[k][:, i, :], in_=band_pieces[k % 2][:, i, :], identity=identity_bf16[:])
+        def turn_band(m):
+            band_bank[m] = psum_one.tile([P, P], BF16, name="band_bank", tag="band_bank")
+            nc.tensor.transpose(
+                out=band_bank[m][:], in_=band_pieces[m % 2][:].rearrange("p a c -> p (a c)"), identity=identity_bf16[:]
+            )
 
-        def empty_band(k):
-            band_turned[k] = work.tile([P, CHUNK_TILES, P], BF16, name="band_turned", tag="band_turned")
-            nc.scalar.copy(out=band_turned[k][:], in_=band_bank[k][:])
+        def empty_band(m):
+            band_turned[m] = work.tile([P, P], BF16, name="band_turned", tag="band_turned")
+            nc.scalar.copy(out=band_turned[m][:], in_=band_bank[m][:])
 
-        def relative(k, pair):
-            rel_bank[k, pair] = psum_one.tile([P, 2, HEAD_DIM], F32, name="rel_bank", tag="rel_bank")
-            for a in range(2):
-                nc.tensor.matmul(
-                    out=rel_bank[k, pair][:, a, :], lhsT=band_turned[k][:, 2 * pair + a, :], rhs=rel_values[:], start=True, stop=True
-                )
+        def relative(m):
+            rel_bank[m] = psum_one.tile([P, TILES, HEAD_DIM], F32, name="rel_bank", tag="rel_bank")
+            nc.tensor.matmul(
+                out=rel_bank[m][:].rearrange("p a d -> p (a d)"),
+                lhsT=band_turned[m][:],
+                rhs=rel_values[:].rearrange("p a d -> p (a d)"),
+                start=True,
+                stop=True,
+            )
 
-        def empty_relative(k, pair):
-            rel[k, pair] = work.tile([P, 2, HEAD_DIM], F32, name="rel", tag="rel", bufs=4)
-            for a in range(2):
-                i = 2 * pair + a
+        def empty_relative(m):
+            rel[m] = work.tile([P, TILES, HEAD_DIM], F32, name="rel", tag="rel", bufs=3)
+            for a in range(TILES):
                 nc.scalar.activation(
-                    out=rel[k, pair][:, a, :], in_=rel_bank[k, pair][:, a, :], func=ACT.Copy, scale=inv_z[k][:, i : i + 1]
+                    out=rel[m][:, a, :], in_=rel_bank[m][:, a, :], func=ACT.Copy, scale=inv_z[m][:, a : a + 1]
                 )
 
-        def attend(k):
-            n = head_of(k)
-            for pair in range(CHUNK_TILES // 2):
-                ctx_bank[k, pair] = psum_two.tile([P, 2, HEAD_DIM], F32, name="ctx_bank", tag="ctx_bank")
-                for a in range(2):
-                    queries = slice((2 * pair + a) * P, (2 * pair + a + 1) * P)
-                    for g in range(KEY_PASSES):
-                        nc.tensor.matmul_mx(
-                            out=ctx_bank[k, pair][:, a, :],
-                            lhsT=e_codes[k][:, g, queries].bitcast(FP8X4),
-                            lhsT_scale=e_scales[k][:, g, queries],
-                            rhs=v_codes[n][:, g, :].bitcast(FP8X4),
-                            rhs_scale=v_scales[n][:, g, :],
-                            start=(g == 0),
-                            stop=(g == KEY_PASSES - 1),
-                        )
+        def attend(m):
+            n = head_of(m)
+            ctx_bank[m] = psum_two.tile([P, TILES, HEAD_DIM], F32, name="ctx_bank", tag="ctx_bank")
+            for a in range(TILES):
+                queries = slice(a * P, (a + 1) * P)
+                for g in range(KEY_PASSES):
+                    nc.tensor.matmul_mx(
+                        out=ctx_bank[m][:, a, :],
+                        lhsT=e_codes[m][:, g, queries].bitcast(FP8X4),
+                        lhsT_scale=e_scales[m][:, g, queries],
+                        rhs=v_codes[n][:, g, :].bitcast(FP8X4),
+                        rhs_scale=v_scales[n][:, g, :],
+                        start=(g == 0),
+                        stop=(g == KEY_PASSES - 1),
+                    )
 
-        def normalise(k):
-            j, h = k // HEADS, k % HEADS
-            if h == 0:
-                merged[j] = work.tile([P, CHUNK_TILES, FEATURES], BF16, name="merged", tag="merged", bufs=3)
-            for i in range(CHUNK_TILES):
-                nc.vector.scalar_tensor_tensor(
-                    out=merged[j][:, i, h * HEAD_DIM : (h + 1) * HEAD_DIM],
-                    in0=ctx_bank[k, i // 2][:, i % 2, :],
-                    scalar=inv_z[k][:, i : i + 1],
-                    in1=rel[k, i // 2][:, i % 2, :],
-                    op0=ALU.mult,
-                    op1=ALU.add,
-                )
+        def normalise(m, a):
+            s, h = m // HEADS, m % HEADS
+            if h == 0 and a == 0:
+                merged[s] = work.tile([P, TILES, FEATURES], BF16, name="merged", tag="merged")
+            nc.vector.scalar_tensor_tensor(
+                out=merged[s][:, a, h * HEAD_DIM : (h + 1) * HEAD_DIM],
+                in0=ctx_bank[m][:, a, :],
+                scalar=inv_z[m][:, a : a + 1],
+                in1=rel[m][:, a, :],
+                op0=ALU.mult,
+                op1=ALU.add,
+            )
 
         def turn_merged(s):
-            j, pair = s // 2, s % 2
-            m_bank[s] = psum_one.tile([P, 2, PAIR], F32, name="m_bank", tag="m_bank")
-            transpose_pairs(nc, m_bank[s], merged[j][:, 2 * pair, :], merged[j][:, 2 * pair + 1, :], 0, identity_f32[:])
+            m_bank[s] = psum_one.tile([P, 2, ROWS], F32, name="m_bank", tag="m_bank")
+            for a in range(TILES):
+                words = merged[s][:, a, :].bitcast(F32)
+                for u in range(2):
+                    nc.tensor.transpose(
+                        out=m_bank[s][:, u, a * P : (a + 1) * P], in_=words[:, u * P : (u + 1) * P], identity=identity_f32[:]
+                    )
 
         def empty_merged(s):
-            m_words[s] = work.tile([P, PAIR, 2], F32, align_bytes=64, name="m_words", tag="m_words")
+            m_words[s] = work.tile([P, ROWS, 2], F32, align_bytes=64, name="m_words", tag="m_words")
             nc.scalar.copy(out=m_words[s][:], in_=m_bank[s][:].rearrange("p u t -> p t u"))
 
         def quantise_merged(s):
-            m_codes[s] = work.tile([P, PAIR], U32, align_bytes=64, name="m_codes", tag="m_codes")
-            m_scales[s] = work.tile([P, PAIR], U8, align_bytes=64, name="m_scales", tag="m_scales")
+            m_codes[s] = work.tile([P, ROWS], U32, align_bytes=64, name="m_codes", tag="m_codes")
+            m_scales[s] = work.tile([P, ROWS], U8, align_bytes=64, name="m_scales", tag="m_scales")
             quantise(nc, m_words[s][:].rearrange("p t u -> p (t u)").bitcast(BF16), m_codes[s][:], m_scales[s][:])
-            result[s] = work.tile([P, 2, FEATURES], F32, name="result", tag="result", bufs=3)
+            result[s] = work.tile([P, TILES, FEATURES], F32, name="result", tag="result")
 
         def project(s, a):
             out_bank[s, a] = psum_one.tile([P, FEATURES], F32, name="out_bank", tag="out_bank")
@@ -343,95 +352,110 @@ def tile_vitsattention_pa_t_kernel(tc, logits, v, emb_rel_v, Wo, bo, out):
             nc.vector.tensor_tensor(out=result[s][:, a, :], in0=out_bank[s, a][:], in1=bias[:], op=ALU.add)
 
         def store(s):
-            per_batch = SEQ // PAIR
-            rows = slice((s % per_batch) * PAIR, (s % per_batch + 1) * PAIR)
+            rows = slice(first_row_of(s), first_row_of(s) + ROWS)
             nc.sync.dma_start(out=out[batch_of(s), rows, :].rearrange("(a p) o -> p a o", p=P), in_=result[s][:])
 
-        def is_chunk(k):
-            return 0 <= k < CHUNKS
+        def is_pair(m):
+            return 0 <= m < PAIRS
 
-        def is_slab(s):
-            return 0 <= s < SLABS
+        def slab_at(step):
+            return step // 2 if step % 2 == 0 and 0 <= step < PAIRS else None
 
-        def one_round(r):
-            ahead, now, turned, divided = r + 1, r, r - 1, r - 2
-            slab_in, slab_out = r - SLAB_IN, r - SLAB_OUT
+        def group_step(q):
+            return q // 2 if q < HEADS * KEY_PASSES else 2 * q - 5
 
-            if is_chunk(r + AHEAD):
-                load(r + AHEAD)
-                load_band(r + AHEAD)
-            if is_slab(slab_out):
-                quantise_merged(slab_out)
-            if is_chunk(ahead):
-                row_maximum(ahead)
-                prepare_values(batch_of(ahead) * HEADS + (ahead // KEY_PASSES) % HEADS, ahead % KEY_PASSES)
-            if is_chunk(turned):
-                relative(turned, 0)
-            if is_chunk(divided):
-                attend(divided)
+        def one_step(h):
+            ahead, now, before, divided = h + 1, h, h - 1, h - 2
+            turned_slab = slab_at(h - 4)
+            first_slab = slab_at(h - 5)
+            second_slab = slab_at(h - 6)
 
-            if is_chunk(now):
+            if is_pair(h + AHEAD):
+                load(h + AHEAD)
+                load_band(h + AHEAD)
+            for q in range(2 * HEADS * KEY_PASSES // 2, HALF_HEADS, KEY_PASSES):
+                if h == group_step(q) - 3:
+                    load_values(q)
+
+            if is_pair(before):
+                turn_band(before)
+                turn_e(before, 1)
+                reciprocal(before)
+            if is_pair(ahead):
+                fold(ahead, SEQ // 2)
+            for q in range(HALF_HEADS):
+                if h == group_step(q) + 1:
+                    quantise_values(q)
+            if is_pair(now):
                 exponential(now, 0)
-            if is_chunk(turned):
-                empty_e(turned, 0)
-                turn_e(turned, 2)
-                empty_relative(turned, 0)
-                relative(turned, 1)
-            if is_slab(slab_out):
-                project(slab_out, 0)
+            if is_pair(before):
+                empty_band(before)
+            if is_pair(now):
+                band_exponential(now)
+                cut_band(now)
+            if turned_slab is not None:
+                turn_merged(turned_slab)
+            if first_slab is not None:
+                quantise_merged(first_slab)
+            if is_pair(ahead):
+                fold(ahead, SEQ // 4)
+            if first_slab is not None:
+                project(first_slab, 0)
+            if second_slab is not None:
+                project(second_slab, 1)
+            if is_pair(before):
+                relative(before)
 
-            if is_chunk(now):
+            if is_pair(before):
+                empty_e(before, 1, nc.scalar.copy)
+            for q in range(HALF_HEADS):
+                if h == group_step(q):
+                    group_values(q)
+            if h == 3:
+                group_weights()
+            if h == 4:
+                finish_weights()
+            if first_slab is not None:
+                add_bias(first_slab, 0)
+            if second_slab is not None:
+                add_bias(second_slab, 1)
+                store(second_slab)
+            if is_pair(ahead):
+                fold(ahead, SEQ // 8)
+            if is_pair(now):
                 exponential(now, 1)
-            if is_chunk(turned):
-                empty_e(turned, 1)
-                turn_e(turned, 3)
-            if is_chunk(now):
-                turn_band(now)
-            if is_chunk(turned):
-                empty_relative(turned, 1)
-            if is_chunk(divided):
-                normalise(divided)
-            if is_slab(slab_out):
-                add_bias(slab_out, 0)
-
-            if is_chunk(now):
-                exponential(now, 2)
-            if is_chunk(turned):
-                empty_e(turned, 2)
-            if is_chunk(now):
+            if is_pair(before):
+                quantise_e(before)
+            if is_pair(now):
                 turn_e(now, 0)
-            if is_slab(slab_in):
-                turn_merged(slab_in)
-            if is_slab(slab_out):
-                project(slab_out, 1)
 
-            if is_chunk(now):
-                exponential(now, 3)
-            if is_chunk(turned):
-                empty_e(turned, 3)
-            if is_chunk(now):
-                turn_e(now, 1)
-                empty_band(now)
-            if is_slab(slab_in):
-                empty_merged(slab_in)
-            if is_chunk(ahead):
-                band_exponential(ahead)
-                cut_band(ahead)
-            if is_slab(slab_out):
-                add_bias(slab_out, 1)
-                store(slab_out)
-            if is_chunk(now):
-                reciprocal(now)
-            if is_chunk(turned):
-                quantise_e(turned)
-            if r == 0:
-                prepare_weights()
+            if is_pair(before):
+                attend(before)
+            if is_pair(divided):
+                normalise(divided, 0)
+            if is_pair(ahead):
+                row_maximum(ahead)
+            if is_pair(divided):
+                normalise(divided, 1)
+            if is_pair(now):
+                empty_e(now, 0, nc.vector.tensor_copy if now % 2 == 0 else nc.scalar.copy)
+            if is_pair(before):
+                empty_relative(before)
+            if turned_slab is not None:
+                empty_merged(turned_slab)
 
         with tc.manual_schedule():
-            for k in range(AHEAD - 1):
-                load(k)
-                load_band(k)
-            for r in range(-1, CHUNKS):
-                one_round(r)
-        for r in range(CHUNKS, SLABS + SLAB_OUT):
-            one_round(r)
+            load(0)
+            load_band(0)
+            load(1)
+            load_values(0)
+            load_band(1)
+            load_values(KEY_PASSES)
+            load_constants()
+            for m in range(2, AHEAD - 1):
+                load(m)
+                load_band(m)
+            for h in range(-1, PAIRS):
+                one_step(h)
+        for h in range(PAIRS, PAIRS + 5):
+            one_step(h)

@@ -29,7 +29,6 @@ SLABS_PER_BATCH = SEQ // ROWS
 SLABS = BATCH * SLABS_PER_BATCH
 PAIRS = SLABS * HEADS
 HALF_HEADS = NHEADS * KEY_PASSES
-SPLIT = 3
 BAND_ROWS = P // TILES
 BAND_SLOT = 16
 AHEAD = 5
@@ -55,13 +54,12 @@ def tile_vitsattention_pa_t_kernel(tc, logits, v, emb_rel_v, Wo, bo, out):
 
         identity_f32 = const.tile([P, P], F32)
         make_identity(nc, identity_f32[:])
-        identity_bf16 = const.tile([P, P], BF16)
-        make_identity(nc, identity_bf16[:])
-        rel_values = const.tile([P, TILES, HEAD_DIM], BF16)
-        nc.vector.memset(rel_values[:], 0.0)
-        band_pieces = [const.tile([P, TILES, BAND_ROWS], BF16, name="band_pieces_%d" % k) for k in range(2)]
+        rel_values_bf16 = const.tile([P, TILES, HEAD_DIM], BF16)
+        nc.vector.memset(rel_values_bf16[:], 0.0)
+        rel_values = const.tile([P, TILES, HEAD_DIM], F32)
+        band = [const.tile([P, TILES, BAND_ROWS], F32, name="band_%d" % k) for k in range(2)]
         for k in range(2):
-            nc.vector.memset(band_pieces[k][:], 0.0)
+            nc.gpsimd.memset(band[k][:], 0.0)
         ones = const.tile([P, P], BF16)
         nc.vector.memset(ones[:], 1.0)
         bias_row = const.tile([P, FEATURES], BF16)
@@ -74,9 +72,7 @@ def tile_vitsattention_pa_t_kernel(tc, logits, v, emb_rel_v, Wo, bo, out):
 
         def load_constants():
             for a in range(TILES):
-                for piece in range(SPLIT):
-                    row = a * BAND_ROWS + piece * OFFSETS
-                    nc.sync.dma_start(out=rel_values[row : row + OFFSETS, a, :], in_=emb_rel_v[0])
+                nc.sync.dma_start(out=rel_values_bf16[a * BAND_ROWS : a * BAND_ROWS + OFFSETS, a, :], in_=emb_rel_v[0])
             nc.sync.dma_start(out=bias_row[0:1, :], in_=bo.unsqueeze(0))
             nc.sync.dma_start(
                 out=w_rows[:].rearrange("p (u s) o -> p u s o", u=2),
@@ -93,7 +89,7 @@ def tile_vitsattention_pa_t_kernel(tc, logits, v, emb_rel_v, Wo, bo, out):
             nc.vector.tensor_copy(out=bias[:], in_=bias_bank[:])
 
         raw, band_logits, v_rows, v_grouped, v_codes, v_scales = {}, {}, {}, {}, {}, {}
-        folded, neg_max, band, e_rows, z, inv_z = {}, {}, {}, {}, {}, {}
+        folded, neg_max, shifted, e_rows, z, inv_z = {}, {}, {}, {}, {}, {}
         e_bank, e_words, e_codes, e_scales = {}, {}, {}, {}
         band_bank, band_turned, ctx_bank, rel_bank, rel = {}, {}, {}, {}, {}
         merged, m_bank, m_words, m_codes, m_scales, out_bank, result = {}, {}, {}, {}, {}, {}, {}
@@ -177,9 +173,9 @@ def tile_vitsattention_pa_t_kernel(tc, logits, v, emb_rel_v, Wo, bo, out):
             nc.vector.tensor_reduce(
                 out=neg_max[m][:], in_=folded[m][:, :, 0 : SEQ // 8], axis=AXIS.X, op=ALU.max, negate=True
             )
-            band[m] = small.tile(band_shape, F32, name="band", tag="band")
+            shifted[m] = small.tile(band_shape, F32, name="shifted", tag="shifted")
             nc.gpsimd.tensor_tensor(
-                out=band[m][:],
+                out=shifted[m][:],
                 in0=band_logits[m][:, :, 0:OFFSETS],
                 in1=neg_max[m][:].unsqueeze(2).to_broadcast(band_shape),
                 op=ALU.add,
@@ -228,14 +224,12 @@ def tile_vitsattention_pa_t_kernel(tc, logits, v, emb_rel_v, Wo, bo, out):
             )
 
         def band_exponential(m):
-            nc.scalar.activation(out=band[m][:], in_=band[m][:], func=ACT.Exp)
-
-        def cut_band(m):
+            nc.scalar.activation(out=band[m % 2][:, :, 0:OFFSETS], in_=shifted[m][:], func=ACT.Exp)
             first_row = first_row_of(m // HEADS)
             if first_row == 0:
                 nc.gpsimd.affine_select(
-                    out=band[m][:, 0, :],
-                    in_=band[m][:, 0, :],
+                    out=band[m % 2][:, 0, 0:OFFSETS],
+                    in_=band[m % 2][:, 0, 0:OFFSETS],
                     pattern=[[1, OFFSETS]],
                     compare_op=ALU.is_ge,
                     fill=0.0,
@@ -244,31 +238,23 @@ def tile_vitsattention_pa_t_kernel(tc, logits, v, emb_rel_v, Wo, bo, out):
                 )
             if first_row == SEQ - ROWS:
                 nc.gpsimd.affine_select(
-                    out=band[m][:, TILES - 1, :],
-                    in_=band[m][:, TILES - 1, :],
+                    out=band[m % 2][:, TILES - 1, 0:OFFSETS],
+                    in_=band[m % 2][:, TILES - 1, 0:OFFSETS],
                     pattern=[[-1, OFFSETS]],
                     compare_op=ALU.is_ge,
                     fill=0.0,
                     base=P - 1 + WINDOW,
                     channel_multiplier=-1,
                 )
-            pieces = band_pieces[m % 2]
-            rest = small.tile(band_shape, F32, tag="rest")
-            nc.gpsimd.tensor_copy(out=pieces[:, :, 0:OFFSETS], in_=band[m][:])
-            nc.gpsimd.tensor_tensor(out=rest[:], in0=band[m][:], in1=pieces[:, :, 0:OFFSETS], op=ALU.subtract)
-            nc.gpsimd.tensor_copy(out=pieces[:, :, OFFSETS : 2 * OFFSETS], in_=rest[:])
-            nc.gpsimd.tensor_tensor(
-                out=pieces[:, :, 2 * OFFSETS : 3 * OFFSETS], in0=rest[:], in1=pieces[:, :, OFFSETS : 2 * OFFSETS], op=ALU.subtract
-            )
 
         def turn_band(m):
-            band_bank[m] = psum_one.tile([P, P], BF16, name="band_bank", tag="band_bank")
+            band_bank[m] = psum_one.tile([P, P], F32, name="band_bank", tag="band_bank")
             nc.tensor.transpose(
-                out=band_bank[m][:], in_=band_pieces[m % 2][:].rearrange("p a c -> p (a c)"), identity=identity_bf16[:]
+                out=band_bank[m][:], in_=band[m % 2][:].rearrange("p a c -> p (a c)"), identity=identity_f32[:]
             )
 
         def empty_band(m):
-            band_turned[m] = work.tile([P, P], BF16, name="band_turned", tag="band_turned")
+            band_turned[m] = work.tile([P, P], F32, name="band_turned", tag="band_turned")
             nc.scalar.copy(out=band_turned[m][:], in_=band_bank[m][:])
 
         def relative(m):
@@ -390,9 +376,6 @@ def tile_vitsattention_pa_t_kernel(tc, logits, v, emb_rel_v, Wo, bo, out):
                 exponential(now, 0)
             if is_pair(before):
                 empty_band(before)
-            if is_pair(now):
-                band_exponential(now)
-                cut_band(now)
             if turned_slab is not None:
                 turn_merged(turned_slab)
             if first_slab is not None:
@@ -411,6 +394,8 @@ def tile_vitsattention_pa_t_kernel(tc, logits, v, emb_rel_v, Wo, bo, out):
             for q in range(HALF_HEADS):
                 if h == group_step(q):
                     group_values(q)
+            if h == 0:
+                nc.vector.tensor_copy(out=rel_values[:], in_=rel_values_bf16[:])
             if h == 3:
                 group_weights()
             if h == 4:
@@ -424,6 +409,7 @@ def tile_vitsattention_pa_t_kernel(tc, logits, v, emb_rel_v, Wo, bo, out):
                 fold(ahead, SEQ // 8)
             if is_pair(now):
                 exponential(now, 1)
+                band_exponential(now)
             if is_pair(before):
                 quantise_e(before)
             if is_pair(now):
@@ -450,9 +436,11 @@ def tile_vitsattention_pa_t_kernel(tc, logits, v, emb_rel_v, Wo, bo, out):
             load(1)
             load_values(0)
             load_band(1)
+            load(2)
             load_values(KEY_PASSES)
             load_constants()
-            for m in range(2, AHEAD - 1):
+            load_band(2)
+            for m in range(3, AHEAD - 1):
                 load(m)
                 load_band(m)
             for h in range(-1, PAIRS):

@@ -24,14 +24,15 @@ KEY_PASSES = SEQ // K_PASS
 MATRIX = SEQ * SEQ
 
 TILES = 2
+SLAB_TILES = HEADS * TILES
 ROWS = TILES * P
 SLABS_PER_BATCH = SEQ // ROWS
 SLABS = BATCH * SLABS_PER_BATCH
 PAIRS = SLABS * HEADS
 HALF_HEADS = NHEADS * KEY_PASSES
-BAND_ROWS = P // TILES
+BAND_ROWS = P // SLAB_TILES
 BAND_SLOT = 16
-AHEAD = 5
+AHEAD = 3
 
 FLOPS = (
     2 * NHEADS * SEQ * SEQ * HEAD_DIM + 2 * NHEADS * SEQ * OFFSETS * HEAD_DIM + 2 * BATCH * SEQ * FEATURES * FEATURES
@@ -54,10 +55,15 @@ def tile_vitsattention_pa_t_kernel(tc, logits, v, emb_rel_v, Wo, bo, out):
 
         identity_f32 = const.tile([P, P], F32)
         make_identity(nc, identity_f32[:])
-        rel_values_bf16 = const.tile([P, TILES, HEAD_DIM], BF16)
+        table = const.tile([P, 1], F32)
+        nc.vector.memset(table[:], 0.0)
+        nc.scalar.activation(out=table[:], in_=table[:], func=ACT.Exp)
+        rel_values_bf16 = const.tile([P, SLAB_TILES, HEAD_DIM], BF16)
         nc.vector.memset(rel_values_bf16[:], 0.0)
-        rel_values = const.tile([P, TILES, HEAD_DIM], F32)
-        band = [const.tile([P, TILES, BAND_ROWS], F32, name="band_%d" % k) for k in range(2)]
+        rel_values = const.tile([P, SLAB_TILES, HEAD_DIM], F32)
+        for i in range(SLAB_TILES):
+            nc.scalar.dma_start(out=rel_values_bf16[i * BAND_ROWS : i * BAND_ROWS + OFFSETS, i, :], in_=emb_rel_v[0])
+        band = [const.tile([P, SLAB_TILES, BAND_ROWS], F32, name="band_%d" % k) for k in range(2)]
         for k in range(2):
             nc.gpsimd.memset(band[k][:], 0.0)
         ones = const.tile([P, P], BF16)
@@ -71,8 +77,6 @@ def tile_vitsattention_pa_t_kernel(tc, logits, v, emb_rel_v, Wo, bo, out):
         w_scales = const.tile([P, FEATURES], U8, align_bytes=64)
 
         def load_constants():
-            for a in range(TILES):
-                nc.sync.dma_start(out=rel_values_bf16[a * BAND_ROWS : a * BAND_ROWS + OFFSETS, a, :], in_=emb_rel_v[0])
             nc.sync.dma_start(out=bias_row[0:1, :], in_=bo.unsqueeze(0))
             nc.sync.dma_start(
                 out=w_rows[:].rearrange("p (u s) o -> p u s o", u=2),
@@ -93,7 +97,7 @@ def tile_vitsattention_pa_t_kernel(tc, logits, v, emb_rel_v, Wo, bo, out):
         e_bank, e_words, e_codes, e_scales = {}, {}, {}, {}
         band_bank, band_turned, ctx_bank, rel_bank, rel = {}, {}, {}, {}, {}
         merged, m_bank, m_words, m_codes, m_scales, out_bank, result = {}, {}, {}, {}, {}, {}, {}
-        band_shape = [P, TILES, OFFSETS]
+        band_shape = [P, SLAB_TILES, OFFSETS]
 
         def batch_of(s):
             return (s // SLABS_PER_BATCH + 1) % BATCH
@@ -107,29 +111,38 @@ def tile_vitsattention_pa_t_kernel(tc, logits, v, emb_rel_v, Wo, bo, out):
         def head_of_piece(q):
             return ((q // (HEADS * KEY_PASSES) + 1) % BATCH) * HEADS + (q // KEY_PASSES) % HEADS
 
-        def load(m):
-            rows = slice(first_row_of(m // HEADS), first_row_of(m // HEADS) + ROWS)
-            raw[m] = loads.tile([P, TILES, SEQ], BF16, name="raw", tag="raw")
-            nc.sync.dma_start(out=raw[m][:], in_=logits[head_of(m), rows, :].rearrange("(a p) k -> p a k", p=P))
+        def tiles_of(m):
+            return slice((m % HEADS) * TILES, (m % HEADS + 1) * TILES)
+
+        def load(m, tiles_at_once=TILES):
+            s = m // HEADS
+            if m % HEADS == 0:
+                raw[s] = loads.tile([P, SLAB_TILES, SEQ], BF16, name="raw", tag="raw")
+            for a in range(0, TILES, tiles_at_once):
+                rows = slice(first_row_of(s) + a * P, first_row_of(s) + (a + tiles_at_once) * P)
+                where = raw[s][:, tiles_of(m).start + a : tiles_of(m).start + a + tiles_at_once, :]
+                nc.sync.dma_start(out=where, in_=logits[head_of(m), rows, :].rearrange("(a p) k -> p a k", p=P))
 
         def load_band(m):
             flat = logits.rearrange("n q k -> (n q k)")
             start = head_of(m) * MATRIX + first_row_of(m // HEADS) * (SEQ + 1) - WINDOW
-            band_logits[m] = small.tile([P, TILES, BAND_SLOT], BF16, name="band_logits", tag="band_logits", bufs=AHEAD + 1)
-            slots = band_logits[m]
+            s = m // HEADS
+            if m % HEADS == 0:
+                band_logits[s] = small.tile([P, SLAB_TILES, BAND_SLOT], BF16, name="band_logits", tag="band_logits")
+            slots = band_logits[s][:, tiles_of(m), :]
 
             def load_windows(where, begin, tiles, rows):
                 source = flat[begin : begin + tiles * rows * (SEQ + 1)].rearrange("(a p c) -> p a c", p=rows, c=SEQ + 1)
                 nc.sync.dma_start(out=where, in_=source[:, :, 0:OFFSETS])
 
             if start < 0:
-                nc.gpsimd.memset(slots[:], 0.0)
+                nc.gpsimd.memset(slots, 0.0)
                 nc.sync.dma_start(out=slots[0:1, 0, WINDOW:OFFSETS], in_=flat[0 : WINDOW + 1].unsqueeze(0))
                 load_windows(slots[1:P, 0:1, 0:OFFSETS], start + SEQ + 1, 1, P - 1)
                 load_windows(slots[:, 1:TILES, 0:OFFSETS], start + P * (SEQ + 1), TILES - 1, P)
             elif start + ROWS * (SEQ + 1) > NHEADS * MATRIX:
                 end = TILES - 1
-                nc.gpsimd.memset(slots[:], 0.0)
+                nc.gpsimd.memset(slots, 0.0)
                 load_windows(slots[:, 0:end, 0:OFFSETS], start, end, P)
                 load_windows(slots[0 : P - 1, end : end + 1, 0:OFFSETS], start + end * P * (SEQ + 1), 1, P - 1)
                 nc.sync.dma_start(
@@ -160,24 +173,30 @@ def tile_vitsattention_pa_t_kernel(tc, logits, v, emb_rel_v, Wo, bo, out):
                 v_scales[n] = work.tile([P, KEY_PASSES, HEAD_DIM], U8, align_bytes=64, name="v_scales", tag="v_scales", bufs=4)
             quantise(nc, v_grouped[q][:].rearrange("p d t -> p (d t)"), v_codes[n][:, g, :], v_scales[n][:, g, :])
 
-        def fold(m, width):
-            if width == SEQ // 2:
-                folded[m] = work.tile([P, TILES, SEQ // 2], BF16, name="folded", tag="folded")
-            source = raw[m] if width == SEQ // 2 else folded[m]
+        def start_maximum(s):
+            folded[s] = work.tile([P, SLAB_TILES, SEQ // 2], BF16, name="folded", tag="folded")
+            neg_max[s] = small.tile([P, SLAB_TILES], F32, name="neg_max", tag="neg_max")
+
+        def fold(s, width, tiles=slice(0, SLAB_TILES)):
+            source = raw[s] if width == SEQ // 2 else folded[s]
             nc.vector.tensor_tensor(
-                out=folded[m][:, :, 0:width], in0=source[:, :, 0:width], in1=source[:, :, width : 2 * width], op=ALU.max
+                out=folded[s][:, tiles, 0:width],
+                in0=source[:, tiles, 0:width],
+                in1=source[:, tiles, width : 2 * width],
+                op=ALU.max,
             )
 
-        def row_maximum(m):
-            neg_max[m] = small.tile([P, TILES], F32, name="neg_max", tag="neg_max")
+        def row_maximum(s, tiles=slice(0, SLAB_TILES)):
             nc.vector.tensor_reduce(
-                out=neg_max[m][:], in_=folded[m][:, :, 0 : SEQ // 8], axis=AXIS.X, op=ALU.max, negate=True
+                out=neg_max[s][:, tiles], in_=folded[s][:, tiles, 0 : SEQ // 8], axis=AXIS.X, op=ALU.max, negate=True
             )
-            shifted[m] = small.tile(band_shape, F32, name="shifted", tag="shifted")
+
+        def shift_band(s):
+            shifted[s] = small.tile(band_shape, F32, name="shifted", tag="shifted")
             nc.gpsimd.tensor_tensor(
-                out=shifted[m][:],
-                in0=band_logits[m][:, :, 0:OFFSETS],
-                in1=neg_max[m][:].unsqueeze(2).to_broadcast(band_shape),
+                out=shifted[s][:],
+                in0=band_logits[s][:, :, 0:OFFSETS],
+                in1=neg_max[s][:].unsqueeze(2).to_broadcast(band_shape),
                 op=ALU.add,
             )
 
@@ -185,11 +204,12 @@ def tile_vitsattention_pa_t_kernel(tc, logits, v, emb_rel_v, Wo, bo, out):
             if a == 0:
                 e_rows[m] = work.tile([P, TILES, SEQ], BF16, name="e_rows", tag="e_rows", bufs=3)
                 z[m] = small.tile([P, TILES], F32, name="z", tag="z")
+            i = tiles_of(m).start + a
             nc.scalar.activation(
                 out=e_rows[m][:, a, :],
-                in_=raw[m][:, a, :],
+                in_=raw[m // HEADS][:, i, :],
                 func=ACT.Exp,
-                bias=neg_max[m][:, a : a + 1],
+                bias=neg_max[m // HEADS][:, i : i + 1],
                 scale=1.0,
                 accum_out=z[m][:, a : a + 1],
             )
@@ -223,46 +243,49 @@ def tile_vitsattention_pa_t_kernel(tc, logits, v, emb_rel_v, Wo, bo, out):
                 e_scales[m][:].rearrange("p g q -> p (g q)"),
             )
 
-        def band_exponential(m):
-            nc.scalar.activation(out=band[m % 2][:, :, 0:OFFSETS], in_=shifted[m][:], func=ACT.Exp)
-            first_row = first_row_of(m // HEADS)
-            if first_row == 0:
-                nc.gpsimd.affine_select(
-                    out=band[m % 2][:, 0, 0:OFFSETS],
-                    in_=band[m % 2][:, 0, 0:OFFSETS],
-                    pattern=[[1, OFFSETS]],
-                    compare_op=ALU.is_ge,
-                    fill=0.0,
-                    base=-WINDOW,
-                    channel_multiplier=1,
-                )
-            if first_row == SEQ - ROWS:
-                nc.gpsimd.affine_select(
-                    out=band[m % 2][:, TILES - 1, 0:OFFSETS],
-                    in_=band[m % 2][:, TILES - 1, 0:OFFSETS],
-                    pattern=[[-1, OFFSETS]],
-                    compare_op=ALU.is_ge,
-                    fill=0.0,
-                    base=P - 1 + WINDOW,
-                    channel_multiplier=-1,
-                )
+        def band_exponential(s):
+            bands = band[s % 2]
+            nc.scalar.activation(out=bands[:, :, 0:OFFSETS], in_=shifted[s][:], func=ACT.Exp)
+            for h in range(HEADS):
+                if first_row_of(s) == 0:
+                    first = bands[:, h * TILES, 0:OFFSETS]
+                    nc.gpsimd.affine_select(
+                        out=first,
+                        in_=first,
+                        pattern=[[1, OFFSETS]],
+                        compare_op=ALU.is_ge,
+                        fill=0.0,
+                        base=-WINDOW,
+                        channel_multiplier=1,
+                    )
+                if first_row_of(s) == SEQ - ROWS:
+                    last = bands[:, (h + 1) * TILES - 1, 0:OFFSETS]
+                    nc.gpsimd.affine_select(
+                        out=last,
+                        in_=last,
+                        pattern=[[-1, OFFSETS]],
+                        compare_op=ALU.is_ge,
+                        fill=0.0,
+                        base=P - 1 + WINDOW,
+                        channel_multiplier=-1,
+                    )
 
-        def turn_band(m):
-            band_bank[m] = psum_one.tile([P, P], F32, name="band_bank", tag="band_bank")
+        def turn_band(s):
+            band_bank[s] = psum_one.tile([P, P], F32, name="band_bank", tag="band_bank")
             nc.tensor.transpose(
-                out=band_bank[m][:], in_=band[m % 2][:].rearrange("p a c -> p (a c)"), identity=identity_f32[:]
+                out=band_bank[s][:], in_=band[s % 2][:].rearrange("p i c -> p (i c)"), identity=identity_f32[:]
             )
 
-        def empty_band(m):
-            band_turned[m] = work.tile([P, P], F32, name="band_turned", tag="band_turned")
-            nc.scalar.copy(out=band_turned[m][:], in_=band_bank[m][:])
+        def empty_band(s):
+            band_turned[s] = work.tile([P, P], F32, name="band_turned", tag="band_turned")
+            nc.scalar.copy(out=band_turned[s][:], in_=band_bank[s][:])
 
         def relative(m):
             rel_bank[m] = psum_one.tile([P, TILES, HEAD_DIM], F32, name="rel_bank", tag="rel_bank")
             nc.tensor.matmul(
                 out=rel_bank[m][:].rearrange("p a d -> p (a d)"),
-                lhsT=band_turned[m][:],
-                rhs=rel_values[:].rearrange("p a d -> p (a d)"),
+                lhsT=band_turned[m // HEADS][:],
+                rhs=rel_values[:, tiles_of(m), :].rearrange("p a d -> p (a d)"),
                 start=True,
                 stop=True,
             )
@@ -303,24 +326,26 @@ def tile_vitsattention_pa_t_kernel(tc, logits, v, emb_rel_v, Wo, bo, out):
                 op1=ALU.add,
             )
 
-        def turn_merged(s):
+        def start_output(s):
             m_bank[s] = psum_one.tile([P, 2, ROWS], F32, name="m_bank", tag="m_bank")
-            for a in range(TILES):
-                words = merged[s][:, a, :].bitcast(F32)
-                for u in range(2):
-                    nc.tensor.transpose(
-                        out=m_bank[s][:, u, a * P : (a + 1) * P], in_=words[:, u * P : (u + 1) * P], identity=identity_f32[:]
-                    )
-
-        def empty_merged(s):
             m_words[s] = work.tile([P, ROWS, 2], F32, align_bytes=64, name="m_words", tag="m_words")
-            nc.scalar.copy(out=m_words[s][:], in_=m_bank[s][:].rearrange("p u t -> p t u"))
-
-        def quantise_merged(s):
             m_codes[s] = work.tile([P, ROWS], U32, align_bytes=64, name="m_codes", tag="m_codes")
             m_scales[s] = work.tile([P, ROWS], U8, align_bytes=64, name="m_scales", tag="m_scales")
-            quantise(nc, m_words[s][:].rearrange("p t u -> p (t u)").bitcast(BF16), m_codes[s][:], m_scales[s][:])
             result[s] = work.tile([P, TILES, FEATURES], F32, name="result", tag="result")
+
+        def turn_merged(s, a):
+            words = merged[s][:, a, :].bitcast(F32)
+            for u in range(2):
+                nc.tensor.transpose(
+                    out=m_bank[s][:, u, a * P : (a + 1) * P], in_=words[:, u * P : (u + 1) * P], identity=identity_f32[:]
+                )
+
+        def empty_merged(s, rows=slice(0, ROWS)):
+            nc.scalar.copy(out=m_words[s][:, rows, :], in_=m_bank[s][:, :, rows].rearrange("p u t -> p t u"))
+
+        def quantise_merged(s, rows=slice(0, ROWS)):
+            words = m_words[s][:, rows, :].rearrange("p t u -> p (t u)")
+            quantise(nc, words.bitcast(BF16), m_codes[s][:, rows], m_scales[s][:, rows])
 
         def project(s, a):
             out_bank[s, a] = psum_one.tile([P, FEATURES], F32, name="out_bank", tag="out_bank")
@@ -337,91 +362,102 @@ def tile_vitsattention_pa_t_kernel(tc, logits, v, emb_rel_v, Wo, bo, out):
         def add_bias(s, a):
             nc.vector.tensor_tensor(out=result[s][:, a, :], in0=out_bank[s, a][:], in1=bias[:], op=ALU.add)
 
-        def store(s):
-            rows = slice(first_row_of(s), first_row_of(s) + ROWS)
-            nc.sync.dma_start(out=out[batch_of(s), rows, :].rearrange("(a p) o -> p a o", p=P), in_=result[s][:])
+        def store(s, a):
+            rows = slice(first_row_of(s) + a * P, first_row_of(s) + (a + 1) * P)
+            nc.sync.dma_start(out=out[batch_of(s), rows, :], in_=result[s][:, a, :])
 
         def is_pair(m):
             return 0 <= m < PAIRS
 
-        def slab_at(step):
-            return step // 2 if step % 2 == 0 and 0 <= step < PAIRS else None
-
         def group_step(q):
-            return q // 2 if q < HEADS * KEY_PASSES else 2 * q - 5
+            return 1 if q < HEADS * KEY_PASSES else 2 * q - 5
+
+        def slab_at(step):
+            return step // HEADS if step % HEADS == 0 and 0 <= step < PAIRS else None
+
+        def output_slab_at(step):
+            return slab_at(step) if step < PAIRS - HEADS else None
 
         def one_step(h):
-            ahead, now, before, divided = h + 1, h, h - 1, h - 2
-            turned_slab = slab_at(h - 4)
-            first_slab = slab_at(h - 5)
-            second_slab = slab_at(h - 6)
+            now, before, divided = h, h - 1, h - 2
+            next_slab = slab_at(h + 2)
+            begun_slab = slab_at(h + 1)
+            this_slab = slab_at(h)
+            band_slab = slab_at(h - 1)
+            turned_slab = output_slab_at(h - 4)
+            first_slab = output_slab_at(h - 5)
+            second_slab = output_slab_at(h - 6)
 
-            if is_pair(h + AHEAD):
-                load(h + AHEAD)
-                load_band(h + AHEAD)
-            for q in range(2 * HEADS * KEY_PASSES // 2, HALF_HEADS, KEY_PASSES):
+            m = h + AHEAD * HEADS
+            if is_pair(m):
+                load(m)
+                load_band(m)
+            for q in range(HEADS * KEY_PASSES, HALF_HEADS, KEY_PASSES):
                 if h == group_step(q) - 3:
                     load_values(q)
 
+            if band_slab is not None:
+                turn_band(band_slab)
             if is_pair(before):
-                turn_band(before)
                 turn_e(before, 1)
                 reciprocal(before)
-            if is_pair(ahead):
-                fold(ahead, SEQ // 2)
-            for q in range(HALF_HEADS):
+            if next_slab is not None:
+                start_maximum(next_slab)
+                fold(next_slab, SEQ // 2)
+            if begun_slab is not None:
+                fold(begun_slab, SEQ // 8)
+            for q in range(KEY_PASSES, HALF_HEADS):
                 if h == group_step(q) + 1:
                     quantise_values(q)
             if is_pair(now):
                 exponential(now, 0)
-            if is_pair(before):
-                empty_band(before)
+            if band_slab is not None:
+                empty_band(band_slab)
             if turned_slab is not None:
-                turn_merged(turned_slab)
+                start_output(turned_slab)
+                for a in range(TILES):
+                    turn_merged(turned_slab, a)
             if first_slab is not None:
                 quantise_merged(first_slab)
-            if is_pair(ahead):
-                fold(ahead, SEQ // 4)
-            if first_slab is not None:
                 project(first_slab, 0)
             if second_slab is not None:
                 project(second_slab, 1)
+            if is_pair(divided):
+                attend(divided)
             if is_pair(before):
                 relative(before)
 
             if is_pair(before):
                 empty_e(before, 1, nc.scalar.copy)
-            for q in range(HALF_HEADS):
-                if h == group_step(q):
-                    group_values(q)
-            if h == 0:
-                nc.vector.tensor_copy(out=rel_values[:], in_=rel_values_bf16[:])
             if h == 3:
                 group_weights()
             if h == 4:
                 finish_weights()
+            if begun_slab is not None:
+                row_maximum(begun_slab)
+                shift_band(begun_slab)
+            for q in range(KEY_PASSES, HALF_HEADS):
+                if h == group_step(q):
+                    group_values(q)
             if first_slab is not None:
                 add_bias(first_slab, 0)
+                store(first_slab, 0)
             if second_slab is not None:
                 add_bias(second_slab, 1)
-                store(second_slab)
-            if is_pair(ahead):
-                fold(ahead, SEQ // 8)
+                store(second_slab, 1)
+            if next_slab is not None:
+                fold(next_slab, SEQ // 4)
             if is_pair(now):
                 exponential(now, 1)
-                band_exponential(now)
+            if this_slab is not None:
+                band_exponential(this_slab)
             if is_pair(before):
                 quantise_e(before)
             if is_pair(now):
                 turn_e(now, 0)
 
-            if is_pair(before):
-                attend(before)
             if is_pair(divided):
                 normalise(divided, 0)
-            if is_pair(ahead):
-                row_maximum(ahead)
-            if is_pair(divided):
                 normalise(divided, 1)
             if is_pair(now):
                 empty_e(now, 0, nc.vector.tensor_copy if now % 2 == 0 else nc.scalar.copy)
@@ -430,20 +466,49 @@ def tile_vitsattention_pa_t_kernel(tc, logits, v, emb_rel_v, Wo, bo, out):
             if turned_slab is not None:
                 empty_merged(turned_slab)
 
+        def first_maxima():
+            start_maximum(0)
+            for tiles in (slice(0, 1), slice(1, TILES), slice(TILES, SLAB_TILES)):
+                for width in (SEQ // 2, SEQ // 4, SEQ // 8):
+                    fold(0, width, tiles)
+                row_maximum(0, tiles)
+            shift_band(0)
+
+        def last_slab():
+            s = SLABS - 1
+            start_output(s)
+            for a in range(TILES):
+                rows = slice(a * P, (a + 1) * P)
+                turn_merged(s, a)
+                empty_merged(s, rows)
+                quantise_merged(s, rows)
+                project(s, a)
+                add_bias(s, a)
+                store(s, a)
+
         with tc.manual_schedule():
-            load(0)
-            load_band(0)
+            load(0, 1)
             load(1)
-            load_values(0)
+            load_band(0)
             load_band(1)
+            load_values(0)
             load(2)
+            load(3)
             load_values(KEY_PASSES)
             load_constants()
             load_band(2)
-            for m in range(3, AHEAD - 1):
+            load_band(3)
+            for m in range(2 * HEADS, AHEAD * HEADS):
                 load(m)
                 load_band(m)
-            for h in range(-1, PAIRS):
+            first_maxima()
+            for q in range(KEY_PASSES):
+                group_values(q)
+            for q in range(KEY_PASSES):
+                quantise_values(q)
+            nc.vector.tensor_copy(out=rel_values[:], in_=rel_values_bf16[:])
+            for h in range(PAIRS):
                 one_step(h)
-        for h in range(PAIRS, PAIRS + 5):
+        for h in range(PAIRS, PAIRS + 3):
             one_step(h)
+        last_slab()

@@ -30,8 +30,10 @@ SLABS_PER_BATCH = SEQ // ROWS
 SLABS = BATCH * SLABS_PER_BATCH
 PAIRS = SLABS * HEADS
 HALF_HEADS = NHEADS * KEY_PASSES
+SPLIT = 3
 BAND_ROWS = P // SLAB_TILES
 BAND_SLOT = 16
+EARLY_STEPS = 4
 AHEAD = 3
 
 FLOPS = (
@@ -52,20 +54,40 @@ def tile_vitsattention_pa_t_kernel(tc, logits, v, emb_rel_v, Wo, bo, out):
         small = stack.enter_context(tc.tile_pool(name="small", bufs=4))
         psum_two = stack.enter_context(tc.psum_pool(name="psum_two", bufs=2))
         psum_one = stack.enter_context(tc.psum_pool(name="psum_one", bufs=1))
+        stack.enter_context(tc.manual_schedule())
 
         identity_f32 = const.tile([P, P], F32)
         make_identity(nc, identity_f32[:])
         table = const.tile([P, 1], F32)
         nc.vector.memset(table[:], 0.0)
         nc.scalar.activation(out=table[:], in_=table[:], func=ACT.Exp)
-        rel_values_bf16 = const.tile([P, SLAB_TILES, HEAD_DIM], BF16)
-        nc.vector.memset(rel_values_bf16[:], 0.0)
-        rel_values = const.tile([P, SLAB_TILES, HEAD_DIM], F32)
+        identity_bf16 = const.tile([P, P], BF16)
+        make_identity(nc, identity_bf16[:])
+        rel_values = const.tile([P, SLAB_TILES, HEAD_DIM], BF16)
+        nc.vector.memset(rel_values[:], 0.0)
+        emb_rows = const.tile([P, HEAD_DIM], BF16)
+        nc.vector.memset(emb_rows[:], 0.0)
+        nc.scalar.dma_start(out=emb_rows[0:OFFSETS, :], in_=emb_rel_v[0])
+        spread = const.tile([P, SLAB_TILES, BAND_ROWS], BF16)
+        nc.vector.memset(spread[:], 0.0)
         for i in range(SLAB_TILES):
-            nc.scalar.dma_start(out=rel_values_bf16[i * BAND_ROWS : i * BAND_ROWS + OFFSETS, i, :], in_=emb_rel_v[0])
-        band = [const.tile([P, SLAB_TILES, BAND_ROWS], F32, name="band_%d" % k) for k in range(2)]
+            nc.vector.tensor_copy(
+                out=spread[:, i, 0 : SPLIT * OFFSETS].rearrange("p (c j) -> p c j", c=SPLIT),
+                in_=identity_bf16[:, 0:OFFSETS].unsqueeze(1).to_broadcast([P, SPLIT, OFFSETS]),
+            )
+        band_pieces = [const.tile([P, SLAB_TILES, BAND_ROWS], BF16, name="band_pieces_%d" % k) for k in range(2)]
         for k in range(2):
-            nc.gpsimd.memset(band[k][:], 0.0)
+            nc.gpsimd.memset(band_pieces[k][:], 0.0)
+
+        def prepare_relative():
+            emb_bank = psum_one.tile([P, HEAD_DIM], F32, name="emb_bank", tag="out_bank")
+            nc.tensor.matmul(
+                out=emb_bank[:], lhsT=spread[:].rearrange("p i r -> p (i r)"), rhs=emb_rows[:], start=True, stop=True
+            )
+            for i in range(SLAB_TILES):
+                rows = slice(i * BAND_ROWS, (i + 1) * BAND_ROWS)
+                nc.scalar.copy(out=rel_values[rows, i, :], in_=emb_bank[rows, :])
+
         ones = const.tile([P, P], BF16)
         nc.vector.memset(ones[:], 1.0)
         bias_row = const.tile([P, FEATURES], BF16)
@@ -86,14 +108,16 @@ def tile_vitsattention_pa_t_kernel(tc, logits, v, emb_rel_v, Wo, bo, out):
         def group_weights():
             nc.vector.tensor_copy(out=w_grouped[:], in_=w_rows[:].rearrange("p t o -> p o t"))
 
-        def finish_weights():
+        def quantise_weights():
+            quantise(nc, w_grouped[:].rearrange("p o t -> p (o t)"), w_codes[:], w_scales[:])
+
+        def spread_bias():
             bias_bank = psum_one.tile([P, FEATURES], F32, name="out_bank", tag="out_bank")
             nc.tensor.matmul(out=bias_bank[:], lhsT=ones[:], rhs=bias_row[:], start=True, stop=True)
-            quantise(nc, w_grouped[:].rearrange("p o t -> p (o t)"), w_codes[:], w_scales[:])
             nc.vector.tensor_copy(out=bias[:], in_=bias_bank[:])
 
         raw, band_logits, v_rows, v_grouped, v_codes, v_scales = {}, {}, {}, {}, {}, {}
-        folded, neg_max, shifted, e_rows, z, inv_z = {}, {}, {}, {}, {}, {}
+        folded, neg_max, band, e_rows, z, inv_z = {}, {}, {}, {}, {}, {}
         e_bank, e_words, e_codes, e_scales = {}, {}, {}, {}
         band_bank, band_turned, ctx_bank, rel_bank, rel = {}, {}, {}, {}, {}
         merged, m_bank, m_words, m_codes, m_scales, out_bank, result = {}, {}, {}, {}, {}, {}, {}
@@ -186,15 +210,13 @@ def tile_vitsattention_pa_t_kernel(tc, logits, v, emb_rel_v, Wo, bo, out):
                 op=ALU.max,
             )
 
-        def row_maximum(s, tiles=slice(0, SLAB_TILES)):
-            nc.vector.tensor_reduce(
-                out=neg_max[s][:, tiles], in_=folded[s][:, tiles, 0 : SEQ // 8], axis=AXIS.X, op=ALU.max, negate=True
-            )
+        def row_maximum(s, source, tiles=slice(0, SLAB_TILES)):
+            nc.vector.tensor_reduce(out=neg_max[s][:, tiles], in_=source, axis=AXIS.X, op=ALU.max, negate=True)
 
         def shift_band(s):
-            shifted[s] = small.tile(band_shape, F32, name="shifted", tag="shifted")
+            band[s] = small.tile(band_shape, F32, name="band", tag="band")
             nc.gpsimd.tensor_tensor(
-                out=shifted[s][:],
+                out=band[s][:],
                 in0=band_logits[s][:, :, 0:OFFSETS],
                 in1=neg_max[s][:].unsqueeze(2).to_broadcast(band_shape),
                 op=ALU.add,
@@ -244,11 +266,12 @@ def tile_vitsattention_pa_t_kernel(tc, logits, v, emb_rel_v, Wo, bo, out):
             )
 
         def band_exponential(s):
-            bands = band[s % 2]
-            nc.scalar.activation(out=bands[:, :, 0:OFFSETS], in_=shifted[s][:], func=ACT.Exp)
+            nc.scalar.activation(out=band[s][:], in_=band[s][:], func=ACT.Exp)
+
+        def cut_band(s):
             for h in range(HEADS):
                 if first_row_of(s) == 0:
-                    first = bands[:, h * TILES, 0:OFFSETS]
+                    first = band[s][:, h * TILES, :]
                     nc.gpsimd.affine_select(
                         out=first,
                         in_=first,
@@ -259,7 +282,7 @@ def tile_vitsattention_pa_t_kernel(tc, logits, v, emb_rel_v, Wo, bo, out):
                         channel_multiplier=1,
                     )
                 if first_row_of(s) == SEQ - ROWS:
-                    last = bands[:, (h + 1) * TILES - 1, 0:OFFSETS]
+                    last = band[s][:, (h + 1) * TILES - 1, :]
                     nc.gpsimd.affine_select(
                         out=last,
                         in_=last,
@@ -269,19 +292,27 @@ def tile_vitsattention_pa_t_kernel(tc, logits, v, emb_rel_v, Wo, bo, out):
                         base=P - 1 + WINDOW,
                         channel_multiplier=-1,
                     )
+            pieces = band_pieces[s % 2]
+            rest = small.tile(band_shape, F32, tag="rest")
+            nc.gpsimd.tensor_copy(out=pieces[:, :, 0:OFFSETS], in_=band[s][:])
+            nc.gpsimd.tensor_tensor(out=rest[:], in0=band[s][:], in1=pieces[:, :, 0:OFFSETS], op=ALU.subtract)
+            nc.gpsimd.tensor_copy(out=pieces[:, :, OFFSETS : 2 * OFFSETS], in_=rest[:])
+            nc.gpsimd.tensor_tensor(
+                out=pieces[:, :, 2 * OFFSETS : 3 * OFFSETS], in0=rest[:], in1=pieces[:, :, OFFSETS : 2 * OFFSETS], op=ALU.subtract
+            )
 
         def turn_band(s):
-            band_bank[s] = psum_one.tile([P, P], F32, name="band_bank", tag="band_bank")
+            band_bank[s] = psum_one.tile([P, P], BF16, name="band_bank", tag="turned")
             nc.tensor.transpose(
-                out=band_bank[s][:], in_=band[s % 2][:].rearrange("p i c -> p (i c)"), identity=identity_f32[:]
+                out=band_bank[s][:], in_=band_pieces[s % 2][:].rearrange("p i r -> p (i r)"), identity=identity_bf16[:]
             )
 
         def empty_band(s):
-            band_turned[s] = work.tile([P, P], F32, name="band_turned", tag="band_turned")
+            band_turned[s] = work.tile([P, P], BF16, name="band_turned", tag="band_turned")
             nc.scalar.copy(out=band_turned[s][:], in_=band_bank[s][:])
 
         def relative(m):
-            rel_bank[m] = psum_one.tile([P, TILES, HEAD_DIM], F32, name="rel_bank", tag="rel_bank")
+            rel_bank[m] = psum_two.tile([P, TILES, HEAD_DIM], F32, name="rel_bank", tag="rel_bank")
             nc.tensor.matmul(
                 out=rel_bank[m][:].rearrange("p a d -> p (a d)"),
                 lhsT=band_turned[m // HEADS][:],
@@ -327,11 +358,11 @@ def tile_vitsattention_pa_t_kernel(tc, logits, v, emb_rel_v, Wo, bo, out):
             )
 
         def start_output(s):
-            m_bank[s] = psum_one.tile([P, 2, ROWS], F32, name="m_bank", tag="m_bank")
+            m_bank[s] = psum_one.tile([P, 2, ROWS], F32, name="m_bank", tag="turned")
             m_words[s] = work.tile([P, ROWS, 2], F32, align_bytes=64, name="m_words", tag="m_words")
             m_codes[s] = work.tile([P, ROWS], U32, align_bytes=64, name="m_codes", tag="m_codes")
             m_scales[s] = work.tile([P, ROWS], U8, align_bytes=64, name="m_scales", tag="m_scales")
-            result[s] = work.tile([P, TILES, FEATURES], F32, name="result", tag="result")
+            result[s] = work.tile([P, TILES, FEATURES], F32, name="result", tag="result", bufs=3)
 
         def turn_merged(s, a):
             words = merged[s][:, a, :].bitcast(F32)
@@ -347,8 +378,8 @@ def tile_vitsattention_pa_t_kernel(tc, logits, v, emb_rel_v, Wo, bo, out):
             words = m_words[s][:, rows, :].rearrange("p t u -> p (t u)")
             quantise(nc, words.bitcast(BF16), m_codes[s][:, rows], m_scales[s][:, rows])
 
-        def project(s, a):
-            out_bank[s, a] = psum_one.tile([P, FEATURES], F32, name="out_bank", tag="out_bank")
+        def project(s, a, bank=None):
+            out_bank[s, a] = bank or psum_one.tile([P, FEATURES], F32, name="out_bank", tag="out_bank")
             nc.tensor.matmul_mx(
                 out=out_bank[s, a][:],
                 lhsT=m_codes[s][:, a * P : (a + 1) * P].bitcast(FP8X4),
@@ -370,7 +401,7 @@ def tile_vitsattention_pa_t_kernel(tc, logits, v, emb_rel_v, Wo, bo, out):
             return 0 <= m < PAIRS
 
         def group_step(q):
-            return 1 if q < HEADS * KEY_PASSES else 2 * q - 5
+            return 1 + q // KEY_PASSES if q < HEADS * KEY_PASSES else 2 * q - 5
 
         def slab_at(step):
             return step // HEADS if step % HEADS == 0 and 0 <= step < PAIRS else None
@@ -379,14 +410,15 @@ def tile_vitsattention_pa_t_kernel(tc, logits, v, emb_rel_v, Wo, bo, out):
             return slab_at(step) if step < PAIRS - HEADS else None
 
         def one_step(h):
-            now, before, divided = h, h - 1, h - 2
+            now, before, attended, divided = h, h - 1, h - 2, h - 3
             next_slab = slab_at(h + 2)
             begun_slab = slab_at(h + 1)
             this_slab = slab_at(h)
             band_slab = slab_at(h - 1)
             turned_slab = output_slab_at(h - 4)
-            first_slab = output_slab_at(h - 5)
-            second_slab = output_slab_at(h - 6)
+            quantised_slab = output_slab_at(h - 5)
+            first_slab = output_slab_at(h - 6)
+            second_slab = output_slab_at(h - 7)
 
             m = h + AHEAD * HEADS
             if is_pair(m):
@@ -395,48 +427,61 @@ def tile_vitsattention_pa_t_kernel(tc, logits, v, emb_rel_v, Wo, bo, out):
             for q in range(HEADS * KEY_PASSES, HALF_HEADS, KEY_PASSES):
                 if h == group_step(q) - 3:
                     load_values(q)
+            if h == 5:
+                quantise_weights()
+                spread_bias()
 
-            if band_slab is not None:
-                turn_band(band_slab)
             if is_pair(before):
                 turn_e(before, 1)
+            if first_slab is not None:
+                project(first_slab, 0)
+            if second_slab is not None:
+                project(second_slab, 1)
+            if h >= EARLY_STEPS and is_pair(attended):
+                relative(attended)
+                attend(attended)
+            if is_pair(before):
                 reciprocal(before)
+            if is_pair(divided):
+                for a in range(TILES):
+                    normalise(divided, a)
+            if is_pair(now):
+                exponential(now, 0)
+                turn_e(now, 0)
+            if this_slab is not None and this_slab > 0:
+                band_exponential(this_slab)
+                cut_band(this_slab)
+            if is_pair(before):
+                empty_e(before, 1, nc.scalar.copy)
+            if h == 1:
+                band_exponential(0)
+                cut_band(0)
             if next_slab is not None:
                 start_maximum(next_slab)
                 fold(next_slab, SEQ // 2)
             if begun_slab is not None:
                 fold(begun_slab, SEQ // 8)
-            for q in range(KEY_PASSES, HALF_HEADS):
-                if h == group_step(q) + 1:
-                    quantise_values(q)
-            if is_pair(now):
-                exponential(now, 0)
-            if band_slab is not None:
-                empty_band(band_slab)
+            if quantised_slab is not None:
+                quantise_merged(quantised_slab)
+
+            if h == 2:
+                turn_band(0)
+                empty_band(0)
+            if h < EARLY_STEPS and is_pair(attended):
+                relative(attended)
+                attend(attended)
             if turned_slab is not None:
                 start_output(turned_slab)
                 for a in range(TILES):
                     turn_merged(turned_slab, a)
-            if first_slab is not None:
-                quantise_merged(first_slab)
-                project(first_slab, 0)
-            if second_slab is not None:
-                project(second_slab, 1)
-            if is_pair(divided):
-                attend(divided)
-            if is_pair(before):
-                relative(before)
-
-            if is_pair(before):
-                empty_e(before, 1, nc.scalar.copy)
-            if h == 3:
-                group_weights()
+            if band_slab is not None and band_slab > 0:
+                turn_band(band_slab)
             if h == 4:
-                finish_weights()
+                group_weights()
             if begun_slab is not None:
-                row_maximum(begun_slab)
+                row_maximum(begun_slab, folded[begun_slab][:, :, 0 : SEQ // 8])
                 shift_band(begun_slab)
-            for q in range(KEY_PASSES, HALF_HEADS):
+            for q in range(HALF_HEADS):
                 if h == group_step(q):
                     group_values(q)
             if first_slab is not None:
@@ -447,68 +492,96 @@ def tile_vitsattention_pa_t_kernel(tc, logits, v, emb_rel_v, Wo, bo, out):
                 store(second_slab, 1)
             if next_slab is not None:
                 fold(next_slab, SEQ // 4)
+
             if is_pair(now):
                 exponential(now, 1)
-            if this_slab is not None:
-                band_exponential(this_slab)
             if is_pair(before):
                 quantise_e(before)
+            for q in range(HALF_HEADS):
+                if h == group_step(q):
+                    quantise_values(q)
             if is_pair(now):
-                turn_e(now, 0)
-
-            if is_pair(divided):
-                normalise(divided, 0)
-                normalise(divided, 1)
-            if is_pair(now):
-                empty_e(now, 0, nc.vector.tensor_copy if now % 2 == 0 else nc.scalar.copy)
-            if is_pair(before):
-                empty_relative(before)
+                empty_e(now, 0, nc.vector.tensor_copy if now % 2 == 0 and now > 0 else nc.scalar.copy)
+            if h == 1:
+                prepare_relative()
+            if band_slab is not None and band_slab > 0:
+                empty_band(band_slab)
+            if is_pair(attended):
+                empty_relative(attended)
             if turned_slab is not None:
                 empty_merged(turned_slab)
+            if h == PAIRS - 1:
+                relative(before)
+                project(quantised_slab, 0)
+                add_bias(quantised_slab, 0)
+                store(quantised_slab, 0)
 
         def first_maxima():
             start_maximum(0)
-            for tiles in (slice(0, 1), slice(1, TILES), slice(TILES, SLAB_TILES)):
-                for width in (SEQ // 2, SEQ // 4, SEQ // 8):
-                    fold(0, width, tiles)
-                row_maximum(0, tiles)
+            for i in range(TILES):
+                row_maximum(0, raw[0][:, i : i + 1, :], slice(i, i + 1))
+            second_head = slice(TILES, SLAB_TILES)
+            for width in (SEQ // 2, SEQ // 4, SEQ // 8):
+                fold(0, width, second_head)
+            row_maximum(0, folded[0][:, second_head, 0 : SEQ // 8], second_head)
             shift_band(0)
 
-        def last_slab():
-            s = SLABS - 1
+        def drain():
+            last, s = PAIRS - 1, SLABS - 1
+            tile_rows = [slice(a * P, (a + 1) * P) for a in range(TILES)]
+            turn_e(last, 1)
+            attend(last - 1)
+            relative(last)
+            reciprocal(last)
+            for a in range(TILES):
+                normalise(last - 2, a)
+            empty_e(last, 1, nc.scalar.copy)
+            empty_relative(last - 1)
+            project(s - 2, 1)
+            start_output(s - 1)
+            for a in range(TILES):
+                turn_merged(s - 1, a)
+            quantise_e(last)
+            attend(last)
+            empty_relative(last)
+            empty_merged(s - 1)
+            for a in range(TILES):
+                normalise(last - 1, a)
+            add_bias(s - 2, 1)
+            store(s - 2, 1)
             start_output(s)
             for a in range(TILES):
-                rows = slice(a * P, (a + 1) * P)
+                normalise(last, a)
                 turn_merged(s, a)
-                empty_merged(s, rows)
-                quantise_merged(s, rows)
-                project(s, a)
+                empty_merged(s, tile_rows[a])
+            quantise_merged(s - 1)
+            for a in range(TILES):
+                project(s - 1, a, psum_two.tile([P, FEATURES], F32, name="out_of_rel", tag="rel_bank"))
+            quantise_merged(s, tile_rows[0])
+            project(s, 0)
+            add_bias(s - 1, 0)
+            store(s - 1, 0)
+            quantise_merged(s, tile_rows[1])
+            project(s, 1, psum_two.tile([P, FEATURES], F32, name="out_of_e", tag="e_bank"))
+            add_bias(s - 1, 1)
+            store(s - 1, 1)
+            for a in range(TILES):
                 add_bias(s, a)
                 store(s, a)
 
-        with tc.manual_schedule():
-            load(0, 1)
-            load(1)
-            load_band(0)
-            load_band(1)
-            load_values(0)
-            load(2)
-            load(3)
-            load_values(KEY_PASSES)
-            load_constants()
-            load_band(2)
-            load_band(3)
-            for m in range(2 * HEADS, AHEAD * HEADS):
-                load(m)
-                load_band(m)
-            first_maxima()
-            for q in range(KEY_PASSES):
-                group_values(q)
-            for q in range(KEY_PASSES):
-                quantise_values(q)
-            nc.vector.tensor_copy(out=rel_values[:], in_=rel_values_bf16[:])
-            for h in range(PAIRS):
-                one_step(h)
-        for h in range(PAIRS, PAIRS + 3):
+        load(0, 1)
+        for m in range(1, 2 * HEADS):
+            load(m)
+        for m in range(2 * HEADS):
+            load_band(m)
+        load_values(0)
+        for m in range(2 * HEADS, AHEAD * HEADS):
+            load(m)
+        load_values(KEY_PASSES)
+        for m in range(2 * HEADS, AHEAD * HEADS):
+            load_band(m)
+        load_constants()
+        first_maxima()
+        for h in range(PAIRS):
             one_step(h)
-        last_slab()
+        drain()

@@ -390,6 +390,17 @@ def tile_vitsattention_pa_t_kernel(tc, logits, v, emb_rel_v, Wo, bo, out):
                 stop=True,
             )
 
+        def redo(s, a):
+            nc.tensor.matmul_mx(
+                out=out_bank[s, a][:],
+                lhsT=m_codes[s][:, a * P : (a + 1) * P].bitcast(FP8X4),
+                lhsT_scale=m_scales[s][:, a * P : (a + 1) * P],
+                rhs=w_codes[:].bitcast(FP8X4),
+                rhs_scale=w_scales[:],
+                start=True,
+                stop=True,
+            )
+
         def add_bias(s, a):
             nc.vector.tensor_tensor(out=result[s][:, a, :], in0=out_bank[s, a][:], in1=bias[:], op=ALU.add)
 
@@ -437,9 +448,12 @@ def tile_vitsattention_pa_t_kernel(tc, logits, v, emb_rel_v, Wo, bo, out):
                 project(first_slab, 0)
             if second_slab is not None:
                 project(second_slab, 1)
+            if first_slab is not None:
+                redo(first_slab, 0)
+            if second_slab is not None:
+                redo(second_slab, 1)
             if h >= EARLY_STEPS and is_pair(attended):
                 relative(attended)
-                attend(attended)
             if is_pair(before):
                 reciprocal(before)
             if is_pair(divided):
@@ -469,6 +483,7 @@ def tile_vitsattention_pa_t_kernel(tc, logits, v, emb_rel_v, Wo, bo, out):
                 empty_band(0)
             if h < EARLY_STEPS and is_pair(attended):
                 relative(attended)
+            if True and is_pair(attended):
                 attend(attended)
             if turned_slab is not None:
                 start_output(turned_slab)
@@ -493,6 +508,8 @@ def tile_vitsattention_pa_t_kernel(tc, logits, v, emb_rel_v, Wo, bo, out):
             if next_slab is not None:
                 fold(next_slab, SEQ // 4)
 
+            if h == PAIRS - 1:
+                return
             if is_pair(now):
                 exponential(now, 1)
             if is_pair(before):
@@ -510,11 +527,6 @@ def tile_vitsattention_pa_t_kernel(tc, logits, v, emb_rel_v, Wo, bo, out):
                 empty_relative(attended)
             if turned_slab is not None:
                 empty_merged(turned_slab)
-            if h == PAIRS - 1:
-                relative(before)
-                project(quantised_slab, 0)
-                add_bias(quantised_slab, 0)
-                store(quantised_slab, 0)
 
         def first_maxima():
             start_maximum(0)
@@ -529,13 +541,22 @@ def tile_vitsattention_pa_t_kernel(tc, logits, v, emb_rel_v, Wo, bo, out):
         def drain():
             last, s = PAIRS - 1, SLABS - 1
             tile_rows = [slice(a * P, (a + 1) * P) for a in range(TILES)]
+            exponential(last, 1)
             turn_e(last, 1)
+            quantise_e(last - 1)
+            empty_e(last, 0, nc.vector.tensor_copy)
+            project(s - 2, 0)
+            empty_band(s)
+            empty_relative(last - 2)
+            relative(last - 1)
             attend(last - 1)
-            relative(last)
+            add_bias(s - 2, 0)
+            store(s - 2, 0)
             reciprocal(last)
+            empty_e(last, 1, nc.scalar.copy)
+            relative(last)
             for a in range(TILES):
                 normalise(last - 2, a)
-            empty_e(last, 1, nc.scalar.copy)
             empty_relative(last - 1)
             project(s - 2, 1)
             start_output(s - 1)

@@ -187,7 +187,8 @@ def tile_vitsattention_pa_t_kernel(tc, logits, v, emb_rel_v, Wo, bo, out):
         def group_values(q):
             v_grouped[q] = work.tile([P, HEAD_DIM, PACK], BF16, align_bytes=64, name="v_grouped", tag="v_grouped", bufs=3)
             nc.vector.tensor_copy(
-                out=v_grouped[q][:], in_=v_rows[head_of_piece(q)][:, q % KEY_PASSES, :, :].rearrange("p t d -> p d t")
+                out=v_grouped[q][:].rearrange("p (c i) t -> p c t i", i=4),
+                in_=v_rows[head_of_piece(q)][:, q % KEY_PASSES, :, :].rearrange("p t (c i) -> p c t i", i=4),
             )
 
         def quantise_values(q):
@@ -223,22 +224,27 @@ def tile_vitsattention_pa_t_kernel(tc, logits, v, emb_rel_v, Wo, bo, out):
             )
 
         def exponential(m, a):
+            s, i = m // HEADS, tiles_of(m).start + a
             if a == 0:
                 e_rows[m] = work.tile([P, TILES, SEQ], BF16, name="e_rows", tag="e_rows", bufs=3)
-                z[m] = small.tile([P, TILES], F32, name="z", tag="z")
-            i = tiles_of(m).start + a
+            if i == 0:
+                z[s] = small.tile([P, SLAB_TILES], F32, name="z", tag="z")
             nc.scalar.activation(
                 out=e_rows[m][:, a, :],
-                in_=raw[m // HEADS][:, i, :],
+                in_=raw[s][:, i, :],
                 func=ACT.Exp,
-                bias=neg_max[m // HEADS][:, i : i + 1],
+                bias=neg_max[s][:, i : i + 1],
                 scale=1.0,
-                accum_out=z[m][:, a : a + 1],
+                accum_out=z[s][:, i : i + 1],
             )
 
-        def reciprocal(m):
-            inv_z[m] = small.tile([P, TILES], F32, name="inv_z", tag="inv_z")
-            nc.vector.reciprocal(out=inv_z[m][:], in_=z[m][:])
+        def reciprocal(s):
+            inv_z[s] = small.tile([P, SLAB_TILES], F32, name="inv_z", tag="inv_z")
+            nc.vector.reciprocal(out=inv_z[s][:], in_=z[s][:])
+
+        def inverse(m, a):
+            i = tiles_of(m).start + a
+            return inv_z[m // HEADS][:, i : i + 1]
 
         def turn_e(m, a):
             e_bank[m, a] = psum_two.tile([P, KEY_PASSES, 2, P], F32, name="e_bank", tag="e_bank")
@@ -325,7 +331,7 @@ def tile_vitsattention_pa_t_kernel(tc, logits, v, emb_rel_v, Wo, bo, out):
             rel[m] = work.tile([P, TILES, HEAD_DIM], F32, name="rel", tag="rel", bufs=3)
             for a in range(TILES):
                 nc.scalar.activation(
-                    out=rel[m][:, a, :], in_=rel_bank[m][:, a, :], func=ACT.Copy, scale=inv_z[m][:, a : a + 1]
+                    out=rel[m][:, a, :], in_=rel_bank[m][:, a, :], func=ACT.Copy, scale=inverse(m, a)
                 )
 
         def attend(m):
@@ -351,7 +357,7 @@ def tile_vitsattention_pa_t_kernel(tc, logits, v, emb_rel_v, Wo, bo, out):
             nc.vector.scalar_tensor_tensor(
                 out=merged[s][:, a, h * HEAD_DIM : (h + 1) * HEAD_DIM],
                 in0=ctx_bank[m][:, a, :],
-                scalar=inv_z[m][:, a : a + 1],
+                scalar=inverse(m, a),
                 in1=rel[m][:, a, :],
                 op0=ALU.mult,
                 op1=ALU.add,
@@ -426,6 +432,7 @@ def tile_vitsattention_pa_t_kernel(tc, logits, v, emb_rel_v, Wo, bo, out):
             begun_slab = slab_at(h + 1)
             this_slab = slab_at(h)
             band_slab = slab_at(h - 1)
+            summed_slab = slab_at(h - 2)
             turned_slab = output_slab_at(h - 4)
             quantised_slab = output_slab_at(h - 5)
             first_slab = output_slab_at(h - 6)
@@ -454,8 +461,8 @@ def tile_vitsattention_pa_t_kernel(tc, logits, v, emb_rel_v, Wo, bo, out):
                 redo(second_slab, 1)
             if h >= EARLY_STEPS and is_pair(attended):
                 relative(attended)
-            if is_pair(before):
-                reciprocal(before)
+            if summed_slab is not None:
+                reciprocal(summed_slab)
             if is_pair(divided):
                 for a in range(TILES):
                     normalise(divided, a)
@@ -494,17 +501,19 @@ def tile_vitsattention_pa_t_kernel(tc, logits, v, emb_rel_v, Wo, bo, out):
             if h == 4:
                 group_weights()
             if begun_slab is not None:
-                row_maximum(begun_slab, folded[begun_slab][:, :, 0 : SEQ // 8])
-                shift_band(begun_slab)
-            for q in range(HALF_HEADS):
-                if h == group_step(q):
-                    group_values(q)
+                fold(begun_slab, SEQ // 16)
             if first_slab is not None:
                 add_bias(first_slab, 0)
                 store(first_slab, 0)
             if second_slab is not None:
                 add_bias(second_slab, 1)
                 store(second_slab, 1)
+            if begun_slab is not None:
+                row_maximum(begun_slab, folded[begun_slab][:, :, 0 : SEQ // 16])
+                shift_band(begun_slab)
+            for q in range(HALF_HEADS):
+                if h == group_step(q):
+                    group_values(q)
             if next_slab is not None:
                 fold(next_slab, SEQ // 4)
 
@@ -518,7 +527,7 @@ def tile_vitsattention_pa_t_kernel(tc, logits, v, emb_rel_v, Wo, bo, out):
                 if h == group_step(q):
                     quantise_values(q)
             if is_pair(now):
-                empty_e(now, 0, nc.vector.tensor_copy if now % 2 == 0 and now > 0 else nc.scalar.copy)
+                empty_e(now, 0, nc.vector.tensor_copy if now % 4 != 1 and now > EARLY_STEPS else nc.scalar.copy)
             if h == 1:
                 prepare_relative()
             if band_slab is not None and band_slab > 0:
@@ -552,7 +561,7 @@ def tile_vitsattention_pa_t_kernel(tc, logits, v, emb_rel_v, Wo, bo, out):
             attend(last - 1)
             add_bias(s - 2, 0)
             store(s - 2, 0)
-            reciprocal(last)
+            reciprocal(s)
             empty_e(last, 1, nc.scalar.copy)
             relative(last)
             for a in range(TILES):

@@ -187,8 +187,7 @@ def tile_vitsattention_pa_t_kernel(tc, logits, v, emb_rel_v, Wo, bo, out):
         def group_values(q):
             v_grouped[q] = work.tile([P, HEAD_DIM, PACK], BF16, align_bytes=64, name="v_grouped", tag="v_grouped", bufs=3)
             nc.vector.tensor_copy(
-                out=v_grouped[q][:].rearrange("p (c i) t -> p c t i", i=4),
-                in_=v_rows[head_of_piece(q)][:, q % KEY_PASSES, :, :].rearrange("p t (c i) -> p c t i", i=4),
+                out=v_grouped[q][:], in_=v_rows[head_of_piece(q)][:, q % KEY_PASSES, :, :].rearrange("p t d -> p d t")
             )
 
         def quantise_values(q):
@@ -473,7 +472,7 @@ def tile_vitsattention_pa_t_kernel(tc, logits, v, emb_rel_v, Wo, bo, out):
                 band_exponential(this_slab)
                 cut_band(this_slab)
             if is_pair(before):
-                empty_e(before, 1, nc.scalar.copy)
+                empty_e(before, 1, nc.vector.tensor_copy if h >= PAIRS - 2 else nc.scalar.copy)
             if h == 1:
                 band_exponential(0)
                 cut_band(0)
@@ -527,7 +526,7 @@ def tile_vitsattention_pa_t_kernel(tc, logits, v, emb_rel_v, Wo, bo, out):
                 if h == group_step(q):
                     quantise_values(q)
             if is_pair(now):
-                empty_e(now, 0, nc.vector.tensor_copy if now % 4 != 1 and now > EARLY_STEPS else nc.scalar.copy)
+                empty_e(now, 0, nc.vector.tensor_copy if (now % 2 == 0 or now >= PAIRS - 3) and now > EARLY_STEPS else nc.scalar.copy)
             if h == 1:
                 prepare_relative()
             if band_slab is not None and band_slab > 0:

@@ -50,7 +50,7 @@ def tile_vitsattention_pa_t_kernel(tc, logits, v, emb_rel_v, Wo, bo, out):
     with ExitStack() as stack:
         const = stack.enter_context(tc.tile_pool(name="const", bufs=1))
         loads = stack.enter_context(tc.tile_pool(name="loads", bufs=AHEAD + 1))
-        work = stack.enter_context(tc.tile_pool(name="work", bufs=2))
+        work = stack.enter_context(tc.tile_pool(name="work", bufs=4))
         small = stack.enter_context(tc.tile_pool(name="small", bufs=4))
         psum_two = stack.enter_context(tc.psum_pool(name="psum_two", bufs=2))
         psum_one = stack.enter_context(tc.psum_pool(name="psum_one", bufs=1))
@@ -185,7 +185,7 @@ def tile_vitsattention_pa_t_kernel(tc, logits, v, emb_rel_v, Wo, bo, out):
             )
 
         def group_values(q):
-            v_grouped[q] = work.tile([P, HEAD_DIM, PACK], BF16, align_bytes=64, name="v_grouped", tag="v_grouped", bufs=3)
+            v_grouped[q] = work.tile([P, HEAD_DIM, PACK], BF16, align_bytes=64, name="v_grouped", tag="v_grouped")
             nc.vector.tensor_copy(
                 out=v_grouped[q][:], in_=v_rows[head_of_piece(q)][:, q % KEY_PASSES, :, :].rearrange("p t d -> p d t")
             )
@@ -193,8 +193,8 @@ def tile_vitsattention_pa_t_kernel(tc, logits, v, emb_rel_v, Wo, bo, out):
         def quantise_values(q):
             n, g = head_of_piece(q), q % KEY_PASSES
             if g == 0:
-                v_codes[n] = work.tile([P, KEY_PASSES, HEAD_DIM], U32, align_bytes=64, name="v_codes", tag="v_codes", bufs=4)
-                v_scales[n] = work.tile([P, KEY_PASSES, HEAD_DIM], U8, align_bytes=64, name="v_scales", tag="v_scales", bufs=4)
+                v_codes[n] = work.tile([P, KEY_PASSES, HEAD_DIM], U32, align_bytes=64, name="v_codes", tag="v_codes")
+                v_scales[n] = work.tile([P, KEY_PASSES, HEAD_DIM], U8, align_bytes=64, name="v_scales", tag="v_scales")
             quantise(nc, v_grouped[q][:].rearrange("p d t -> p (d t)"), v_codes[n][:, g, :], v_scales[n][:, g, :])
 
         def start_maximum(s):
@@ -225,7 +225,7 @@ def tile_vitsattention_pa_t_kernel(tc, logits, v, emb_rel_v, Wo, bo, out):
         def exponential(m, a):
             s, i = m // HEADS, tiles_of(m).start + a
             if a == 0:
-                e_rows[m] = work.tile([P, TILES, SEQ], BF16, name="e_rows", tag="e_rows", bufs=3)
+                e_rows[m] = work.tile([P, TILES, SEQ], BF16, name="e_rows", tag="e_rows")
             if i == 0:
                 z[s] = small.tile([P, SLAB_TILES], F32, name="z", tag="z")
             nc.scalar.activation(
@@ -327,7 +327,7 @@ def tile_vitsattention_pa_t_kernel(tc, logits, v, emb_rel_v, Wo, bo, out):
             )
 
         def empty_relative(m):
-            rel[m] = work.tile([P, TILES, HEAD_DIM], F32, name="rel", tag="rel", bufs=3)
+            rel[m] = work.tile([P, TILES, HEAD_DIM], F32, name="rel", tag="rel")
             for a in range(TILES):
                 nc.scalar.activation(
                     out=rel[m][:, a, :], in_=rel_bank[m][:, a, :], func=ACT.Copy, scale=inverse(m, a)
@@ -367,7 +367,7 @@ def tile_vitsattention_pa_t_kernel(tc, logits, v, emb_rel_v, Wo, bo, out):
             m_words[s] = work.tile([P, ROWS, 2], F32, align_bytes=64, name="m_words", tag="m_words")
             m_codes[s] = work.tile([P, ROWS], U32, align_bytes=64, name="m_codes", tag="m_codes")
             m_scales[s] = work.tile([P, ROWS], U8, align_bytes=64, name="m_scales", tag="m_scales")
-            result[s] = work.tile([P, TILES, FEATURES], F32, name="result", tag="result", bufs=3)
+            result[s] = work.tile([P, TILES, FEATURES], F32, name="result", tag="result")
 
         def turn_merged(s, a):
             words = merged[s][:, a, :].bitcast(F32)
@@ -526,7 +526,7 @@ def tile_vitsattention_pa_t_kernel(tc, logits, v, emb_rel_v, Wo, bo, out):
                 if h == group_step(q):
                     quantise_values(q)
             if is_pair(now):
-                empty_e(now, 0, nc.vector.tensor_copy if (now % 2 == 0 or now >= PAIRS - 3) and now > EARLY_STEPS else nc.scalar.copy)
+                empty_e(now, 0, nc.vector.tensor_copy if (now % 2 == 0 or now % 8 == 3 or now >= PAIRS - 3) and now > EARLY_STEPS else nc.scalar.copy)
             if h == 1:
                 prepare_relative()
             if band_slab is not None and band_slab > 0:

from contextlib import ExitStack

import concourse.mybir as mybir
from concourse.masks import make_identity

F32 = mybir.dt.float32
BF16 = mybir.dt.bfloat16
U32 = mybir.dt.uint32
U8 = mybir.dt.uint8
FP8X4 = mybir.dt.float8_e4m3fn_x4
ALU = mybir.AluOpType
ACT = mybir.ActivationFunctionType
AXIS = mybir.AxisListType

P = 128
PACK = 4
K_PASS = P * PACK

BATCH, HEADS, SEQ, HEAD_DIM, WINDOW = 4, 2, 1024, 256, 4
NHEADS = BATCH * HEADS
FEATURES = HEADS * HEAD_DIM
OFFSETS = 2 * WINDOW + 1
KEY_PASSES = SEQ // K_PASS
MATRIX = SEQ * SEQ

TILES = 2
SLAB_TILES = HEADS * TILES
ROWS = TILES * P
SLABS_PER_BATCH = SEQ // ROWS
SLABS = BATCH * SLABS_PER_BATCH
PAIRS = SLABS * HEADS
HALF_HEADS = NHEADS * KEY_PASSES
SPLIT = 3
BAND_ROWS = P // SLAB_TILES
BAND_SLOT = 16
EARLY_STEPS = 4
AHEAD = 3

FLOPS = (
    2 * NHEADS * SEQ * SEQ * HEAD_DIM + 2 * NHEADS * SEQ * OFFSETS * HEAD_DIM + 2 * BATCH * SEQ * FEATURES * FEATURES
)


def quantise(nc, grouped, codes, scales):
    nc.vector.quantize_mx(out=codes.bitcast(FP8X4), scales=scales, in_=grouped)


def tile_vitsattention_pa_t_kernel(tc, logits, v, emb_rel_v, Wo, bo, out):
    nc = tc.nc
    with ExitStack() as stack:
        const = stack.enter_context(tc.tile_pool(name="const", bufs=1))
        loads = stack.enter_context(tc.tile_pool(name="loads", bufs=AHEAD + 1))
        work = stack.enter_context(tc.tile_pool(name="work", bufs=4))
        small = stack.enter_context(tc.tile_pool(name="small", bufs=4))
        psum_two = stack.enter_context(tc.psum_pool(name="psum_two", bufs=2))
        psum_one = stack.enter_context(tc.psum_pool(name="psum_one", bufs=1))
        stack.enter_context(tc.manual_schedule())

        identity_f32 = const.tile([P, P], F32)
        make_identity(nc, identity_f32[:])
        table = const.tile([P, 1], F32)
        nc.vector.memset(table[:], 0.0)
        nc.scalar.activation(out=table[:], in_=table[:], func=ACT.Exp)
        identity_bf16 = const.tile([P, P], BF16)
        make_identity(nc, identity_bf16[:])
        rel_values = const.tile([P, SLAB_TILES, HEAD_DIM], BF16)
        nc.vector.memset(rel_values[:], 0.0)
        emb_rows = const.tile([P, HEAD_DIM], BF16)
        nc.vector.memset(emb_rows[:], 0.0)
        nc.scalar.dma_start(out=emb_rows[0:OFFSETS, :], in_=emb_rel_v[0])
        spread = const.tile([P, SLAB_TILES, BAND_ROWS], BF16)
        nc.vector.memset(spread[:], 0.0)
        for i in range(SLAB_TILES):
            nc.vector.tensor_copy(
                out=spread[:, i, 0 : SPLIT * OFFSETS].rearrange("p (c j) -> p c j", c=SPLIT),
                in_=identity_bf16[:, 0:OFFSETS].unsqueeze(1).to_broadcast([P, SPLIT, OFFSETS]),
            )
        band_pieces = [const.tile([P, SLAB_TILES, BAND_ROWS], BF16, name="band_pieces_%d" % k) for k in range(2)]
        for k in range(2):
            nc.gpsimd.memset(band_pieces[k][:], 0.0)

        def prepare_relative():
            emb_bank = psum_one.tile([P, HEAD_DIM], F32, name="emb_bank", tag="out_bank")
            nc.tensor.matmul(
                out=emb_bank[:], lhsT=spread[:].rearrange("p i r -> p (i r)"), rhs=emb_rows[:], start=True, stop=True
            )
            for i in range(SLAB_TILES):
                rows = slice(i * BAND_ROWS, (i + 1) * BAND_ROWS)
                nc.scalar.copy(out=rel_values[rows, i, :], in_=emb_bank[rows, :])

        ones = const.tile([P, P], BF16)
        nc.vector.memset(ones[:], 1.0)
        bias_row = const.tile([P, FEATURES], BF16)
        nc.vector.memset(bias_row[:], 0.0)
        bias = const.tile([P, FEATURES], F32)
        w_rows = const.tile([P, PACK, FEATURES], BF16)
        w_grouped = const.tile([P, FEATURES, PACK], BF16, align_bytes=64)
        w_codes = const.tile([P, FEATURES], U32, align_bytes=64)
        w_scales = const.tile([P, FEATURES], U8, align_bytes=64)

        def load_constants():
            nc.sync.dma_start(out=bias_row[0:1, :], in_=bo.unsqueeze(0))
            nc.sync.dma_start(
                out=w_rows[:].rearrange("p (u s) o -> p u s o", u=2),
                in_=Wo.rearrange("(u p s) o -> p u s o", u=2, s=2),
            )

        def group_weights():
            nc.vector.tensor_copy(out=w_grouped[:], in_=w_rows[:].rearrange("p t o -> p o t"))

        def quantise_weights():
            quantise(nc, w_grouped[:].rearrange("p o t -> p (o t)"), w_codes[:], w_scales[:])

        def spread_bias():
            bias_bank = psum_one.tile([P, FEATURES], F32, name="out_bank", tag="out_bank")
            nc.tensor.matmul(out=bias_bank[:], lhsT=ones[:], rhs=bias_row[:], start=True, stop=True)
            nc.vector.tensor_copy(out=bias[:], in_=bias_bank[:])

        raw, band_logits, v_rows, v_grouped, v_codes, v_scales = {}, {}, {}, {}, {}, {}
        folded, neg_max, band, e_rows, z, inv_z = {}, {}, {}, {}, {}, {}
        e_bank, e_words, e_codes, e_scales = {}, {}, {}, {}
        band_bank, band_turned, ctx_bank, rel_bank, rel = {}, {}, {}, {}, {}
        merged, m_bank, m_words, m_codes, m_scales, out_bank, result = {}, {}, {}, {}, {}, {}, {}
        band_shape = [P, SLAB_TILES, OFFSETS]

        def batch_of(s):
            return (s // SLABS_PER_BATCH + 1) % BATCH

        def first_row_of(s):
            return (s % SLABS_PER_BATCH) * ROWS

        def head_of(m):
            return batch_of(m // HEADS) * HEADS + m % HEADS

        def head_of_piece(q):
            return ((q // (HEADS * KEY_PASSES) + 1) % BATCH) * HEADS + (q // KEY_PASSES) % HEADS

        def tiles_of(m):
            return slice((m % HEADS) * TILES, (m % HEADS + 1) * TILES)

        def load(m, tiles_at_once=TILES):
            s = m // HEADS
            if m % HEADS == 0:
                raw[s] = loads.tile([P, SLAB_TILES, SEQ], BF16, name="raw", tag="raw")
            for a in range(0, TILES, tiles_at_once):
                rows = slice(first_row_of(s) + a * P, first_row_of(s) + (a + tiles_at_once) * P)
                where = raw[s][:, tiles_of(m).start + a : tiles_of(m).start + a + tiles_at_once, :]
                nc.sync.dma_start(out=where, in_=logits[head_of(m), rows, :].rearrange("(a p) k -> p a k", p=P))

        def load_band(m):
            flat = logits.rearrange("n q k -> (n q k)")
            start = head_of(m) * MATRIX + first_row_of(m // HEADS) * (SEQ + 1) - WINDOW
            s = m // HEADS
            if m % HEADS == 0:
                band_logits[s] = small.tile([P, SLAB_TILES, BAND_SLOT], BF16, name="band_logits", tag="band_logits")
            slots = band_logits[s][:, tiles_of(m), :]

            def load_windows(where, begin, tiles, rows):
                source = flat[begin : begin + tiles * rows * (SEQ + 1)].rearrange("(a p c) -> p a c", p=rows, c=SEQ + 1)
                nc.sync.dma_start(out=where, in_=source[:, :, 0:OFFSETS])

            if start < 0:
                nc.gpsimd.memset(slots, 0.0)
                nc.sync.dma_start(out=slots[0:1, 0, WINDOW:OFFSETS], in_=flat[0 : WINDOW + 1].unsqueeze(0))
                load_windows(slots[1:P, 0:1, 0:OFFSETS], start + SEQ + 1, 1, P - 1)
                load_windows(slots[:, 1:TILES, 0:OFFSETS], start + P * (SEQ + 1), TILES - 1, P)
            elif start + ROWS * (SEQ + 1) > NHEADS * MATRIX:
                end = TILES - 1
                nc.gpsimd.memset(slots, 0.0)
                load_windows(slots[:, 0:end, 0:OFFSETS], start, end, P)
                load_windows(slots[0 : P - 1, end : end + 1, 0:OFFSETS], start + end * P * (SEQ + 1), 1, P - 1)
                nc.sync.dma_start(
                    out=slots[P - 1 : P, end, 0 : WINDOW + 1],
                    in_=flat[NHEADS * MATRIX - WINDOW - 1 : NHEADS * MATRIX].unsqueeze(0),
                )
            else:
                load_windows(slots[:, :, 0:OFFSETS], start, TILES, P)

        def load_values(q):
            n = head_of_piece(q)
            v_rows[n] = loads.tile([P, KEY_PASSES, PACK, HEAD_DIM], BF16, name="v_rows", tag="v_rows", bufs=3)
            nc.sync.dma_start(
                out=v_rows[n][:].rearrange("p g (u s) d -> p g u s d", u=2),
                in_=v[n].rearrange("(g u p s) d -> p g u s d", g=KEY_PASSES, u=2, s=2),
            )

        def group_values(q):
            v_grouped[q] = work.tile([P, HEAD_DIM, PACK], BF16, align_bytes=64, name="v_grouped", tag="v_grouped")
            nc.vector.tensor_copy(
                out=v_grouped[q][:], in_=v_rows[head_of_piece(q)][:, q % KEY_PASSES, :, :].rearrange("p t d -> p d t")
            )

        def quantise_values(q):
            n, g = head_of_piece(q), q % KEY_PASSES
            if g == 0:
                v_codes[n] = work.tile([P, KEY_PASSES, HEAD_DIM], U32, align_bytes=64, name="v_codes", tag="v_codes")
                v_scales[n] = work.tile([P, KEY_PASSES, HEAD_DIM], U8, align_bytes=64, name="v_scales", tag="v_scales")
            quantise(nc, v_grouped[q][:].rearrange("p d t -> p (d t)"), v_codes[n][:, g, :], v_scales[n][:, g, :])

        def start_maximum(s):
            folded[s] = work.tile([P, SLAB_TILES, SEQ // 2], BF16, name="folded", tag="folded")
            neg_max[s] = small.tile([P, SLAB_TILES], F32, name="neg_max", tag="neg_max")

        def fold(s, width, tiles=slice(0, SLAB_TILES)):
            source = raw[s] if width == SEQ // 2 else folded[s]
            nc.vector.tensor_tensor(
                out=folded[s][:, tiles, 0:width],
                in0=source[:, tiles, 0:width],
                in1=source[:, tiles, width : 2 * width],
                op=ALU.max,
            )

        def row_maximum(s, source, tiles=slice(0, SLAB_TILES)):
            nc.vector.tensor_reduce(out=neg_max[s][:, tiles], in_=source, axis=AXIS.X, op=ALU.max, negate=True)

        def shift_band(s):
            band[s] = small.tile(band_shape, F32, name="band", tag="band")
            nc.gpsimd.tensor_tensor(
                out=band[s][:],
                in0=band_logits[s][:, :, 0:OFFSETS],
                in1=neg_max[s][:].unsqueeze(2).to_broadcast(band_shape),
                op=ALU.add,
            )

        def exponential(m, a):
            s, i = m // HEADS, tiles_of(m).start + a
            if a == 0:
                e_rows[m] = work.tile([P, TILES, SEQ], BF16, name="e_rows", tag="e_rows")
            if i == 0:
                z[s] = small.tile([P, SLAB_TILES], F32, name="z", tag="z")
            nc.scalar.activation(
                out=e_rows[m][:, a, :],
                in_=raw[s][:, i, :],
                func=ACT.Exp,
                bias=neg_max[s][:, i : i + 1],
                scale=1.0,
                accum_out=z[s][:, i : i + 1],
            )

        def reciprocal(s):
            inv_z[s] = small.tile([P, SLAB_TILES], F32, name="inv_z", tag="inv_z")
            nc.vector.reciprocal(out=inv_z[s][:], in_=z[s][:])

        def inverse(m, a):
            i = tiles_of(m).start + a
            return inv_z[m // HEADS][:, i : i + 1]

        def turn_e(m, a):
            e_bank[m, a] = psum_two.tile([P, KEY_PASSES, 2, P], F32, name="e_bank", tag="e_bank")
            words = e_rows[m][:, a, :].bitcast(F32)
            for g in range(KEY_PASSES):
                for u in range(2):
                    first = (2 * g + u) * P
                    nc.tensor.transpose(
                        out=e_bank[m, a][:, g, u, :], in_=words[:, first : first + P], identity=identity_f32[:]
                    )

        def empty_e(m, a, copy):
            if a == 0:
                e_words[m] = work.tile([P, KEY_PASSES, ROWS, 2], F32, align_bytes=64, name="e_words", tag="e_words")
            copy(out=e_words[m][:, :, a * P : (a + 1) * P, :], in_=e_bank[m, a][:].rearrange("p g u q -> p g q u"))

        def quantise_e(m):
            e_codes[m] = work.tile([P, KEY_PASSES, ROWS], U32, align_bytes=64, name="e_codes", tag="e_codes")
            e_scales[m] = work.tile([P, KEY_PASSES, ROWS], U8, align_bytes=64, name="e_scales", tag="e_scales")
            quantise(
                nc,
                e_words[m][:].rearrange("p g q u -> p (g q u)").bitcast(BF16),
                e_codes[m][:].rearrange("p g q -> p (g q)"),
                e_scales[m][:].rearrange("p g q -> p (g q)"),
            )

        def band_exponential(s):
            nc.scalar.activation(out=band[s][:], in_=band[s][:], func=ACT.Exp)

        def cut_band(s):
            for h in range(HEADS):
                if first_row_of(s) == 0:
                    first = band[s][:, h * TILES, :]
                    nc.gpsimd.affine_select(
                        out=first,
                        in_=first,
                        pattern=[[1, OFFSETS]],
                        compare_op=ALU.is_ge,
                        fill=0.0,
                        base=-WINDOW,
                        channel_multiplier=1,
                    )
                if first_row_of(s) == SEQ - ROWS:
                    last = band[s][:, (h + 1) * TILES - 1, :]
                    nc.gpsimd.affine_select(
                        out=last,
                        in_=last,
                        pattern=[[-1, OFFSETS]],
                        compare_op=ALU.is_ge,
                        fill=0.0,
                        base=P - 1 + WINDOW,
                        channel_multiplier=-1,
                    )
            pieces = band_pieces[s % 2]
            rest = small.tile(band_shape, F32, tag="rest")
            nc.gpsimd.tensor_copy(out=pieces[:, :, 0:OFFSETS], in_=band[s][:])
            nc.gpsimd.tensor_tensor(out=rest[:], in0=band[s][:], in1=pieces[:, :, 0:OFFSETS], op=ALU.subtract)
            nc.gpsimd.tensor_copy(out=pieces[:, :, OFFSETS : 2 * OFFSETS], in_=rest[:])
            nc.gpsimd.tensor_tensor(
                out=pieces[:, :, 2 * OFFSETS : 3 * OFFSETS], in0=rest[:], in1=pieces[:, :, OFFSETS : 2 * OFFSETS], op=ALU.subtract
            )

        def turn_band(s):
            band_bank[s] = psum_one.tile([P, P], BF16, name="band_bank", tag="turned")
            nc.tensor.transpose(
                out=band_bank[s][:], in_=band_pieces[s % 2][:].rearrange("p i r -> p (i r)"), identity=identity_bf16[:]
            )

        def empty_band(s):
            band_turned[s] = work.tile([P, P], BF16, name="band_turned", tag="band_turned")
            nc.scalar.copy(out=band_turned[s][:], in_=band_bank[s][:])

        def relative(m):
            rel_bank[m] = psum_two.tile([P, TILES, HEAD_DIM], F32, name="rel_bank", tag="rel_bank")
            nc.tensor.matmul(
                out=rel_bank[m][:].rearrange("p a d -> p (a d)"),
                lhsT=band_turned[m // HEADS][:],
                rhs=rel_values[:, tiles_of(m), :].rearrange("p a d -> p (a d)"),
                start=True,
                stop=True,
            )

        def empty_relative(m):
            rel[m] = work.tile([P, TILES, HEAD_DIM], F32, name="rel", tag="rel")
            for a in range(TILES):
                nc.scalar.activation(
                    out=rel[m][:, a, :], in_=rel_bank[m][:, a, :], func=ACT.Copy, scale=inverse(m, a)
                )

        def attend(m):
            n = head_of(m)
            ctx_bank[m] = psum_two.tile([P, TILES, HEAD_DIM], F32, name="ctx_bank", tag="ctx_bank")
            for a in range(TILES):
                queries = slice(a * P, (a + 1) * P)
                for g in range(KEY_PASSES):
                    nc.tensor.matmul_mx(
                        out=ctx_bank[m][:, a, :],
                        lhsT=e_codes[m][:, g, queries].bitcast(FP8X4),
                        lhsT_scale=e_scales[m][:, g, queries],
                        rhs=v_codes[n][:, g, :].bitcast(FP8X4),
                        rhs_scale=v_scales[n][:, g, :],
                        start=(g == 0),
                        stop=(g == KEY_PASSES - 1),
                    )

        def normalise(m, a):
            s, h = m // HEADS, m % HEADS
            if h == 0 and a == 0:
                merged[s] = work.tile([P, TILES, FEATURES], BF16, name="merged", tag="merged")
            nc.vector.scalar_tensor_tensor(
                out=merged[s][:, a, h * HEAD_DIM : (h + 1) * HEAD_DIM],
                in0=ctx_bank[m][:, a, :],
                scalar=inverse(m, a),
                in1=rel[m][:, a, :],
                op0=ALU.mult,
                op1=ALU.add,
            )

        def start_output(s):
            m_bank[s] = psum_one.tile([P, 2, ROWS], F32, name="m_bank", tag="turned")
            m_words[s] = work.tile([P, ROWS, 2], F32, align_bytes=64, name="m_words", tag="m_words")
            m_codes[s] = work.tile([P, ROWS], U32, align_bytes=64, name="m_codes", tag="m_codes")
            m_scales[s] = work.tile([P, ROWS], U8, align_bytes=64, name="m_scales", tag="m_scales")
            result[s] = work.tile([P, TILES, FEATURES], F32, name="result", tag="result")

        def turn_merged(s, a):
            words = merged[s][:, a, :].bitcast(F32)
            for u in range(2):
                nc.tensor.transpose(
                    out=m_bank[s][:, u, a * P : (a + 1) * P], in_=words[:, u * P : (u + 1) * P], identity=identity_f32[:]
                )

        def empty_merged(s, rows=slice(0, ROWS)):
            nc.scalar.copy(out=m_words[s][:, rows, :], in_=m_bank[s][:, :, rows].rearrange("p u t -> p t u"))

        def quantise_merged(s, rows=slice(0, ROWS)):
            words = m_words[s][:, rows, :].rearrange("p t u -> p (t u)")
            quantise(nc, words.bitcast(BF16), m_codes[s][:, rows], m_scales[s][:, rows])

        def project(s, a, bank=None):
            out_bank[s, a] = bank or psum_one.tile([P, FEATURES], F32, name="out_bank", tag="out_bank")
            nc.tensor.matmul_mx(
                out=out_bank[s, a][:],
                lhsT=m_codes[s][:, a * P : (a + 1) * P].bitcast(FP8X4),
                lhsT_scale=m_scales[s][:, a * P : (a + 1) * P],
                rhs=w_codes[:].bitcast(FP8X4),
                rhs_scale=w_scales[:],
                start=True,
                stop=True,
            )

        def redo(s, a):
            nc.tensor.matmul_mx(
                out=out_bank[s, a][:],
                lhsT=m_codes[s][:, a * P : (a + 1) * P].bitcast(FP8X4),
                lhsT_scale=m_scales[s][:, a * P : (a + 1) * P],
                rhs=w_codes[:].bitcast(FP8X4),
                rhs_scale=w_scales[:],
                start=True,
                stop=True,
            )

        def add_bias(s, a):
            nc.vector.tensor_tensor(out=result[s][:, a, :], in0=out_bank[s, a][:], in1=bias[:], op=ALU.add)

        def store(s, a):
            rows = slice(first_row_of(s) + a * P, first_row_of(s) + (a + 1) * P)
            nc.sync.dma_start(out=out[batch_of(s), rows, :], in_=result[s][:, a, :])

        def is_pair(m):
            return 0 <= m < PAIRS

        def group_step(q):
            return 1 + q // KEY_PASSES if q < HEADS * KEY_PASSES else 2 * q - 5

        def slab_at(step):
            return step // HEADS if step % HEADS == 0 and 0 <= step < PAIRS else None

        def output_slab_at(step):
            return slab_at(step) if step < PAIRS - HEADS else None

        def one_step(h):
            now, before, attended, divided = h, h - 1, h - 2, h - 3
            next_slab = slab_at(h + 2)
            begun_slab = slab_at(h + 1)
            this_slab = slab_at(h)
            band_slab = slab_at(h - 1)
            summed_slab = slab_at(h - 2)
            turned_slab = output_slab_at(h - 4)
            quantised_slab = output_slab_at(h - 5)
            first_slab = output_slab_at(h - 6)
            second_slab = output_slab_at(h - 7)

            m = h + AHEAD * HEADS
            if is_pair(m):
                load(m)
                load_band(m)
            for q in range(HEADS * KEY_PASSES, HALF_HEADS, KEY_PASSES):
                if h == group_step(q) - 3:
                    load_values(q)
            if h == 5:
                quantise_weights()
                spread_bias()

            if is_pair(before):
                turn_e(before, 1)
            if first_slab is not None:
                project(first_slab, 0)
            if second_slab is not None:
                project(second_slab, 1)
            if first_slab is not None:
                redo(first_slab, 0)
            if second_slab is not None:
                redo(second_slab, 1)
            if h >= EARLY_STEPS and is_pair(attended):
                relative(attended)
            if summed_slab is not None:
                reciprocal(summed_slab)
            if is_pair(divided):
                for a in range(TILES):
                    normalise(divided, a)
            if is_pair(now):
                exponential(now, 0)
                turn_e(now, 0)
            if this_slab is not None and this_slab > 0:
                band_exponential(this_slab)
                cut_band(this_slab)
            if is_pair(before):
                empty_e(before, 1, nc.vector.tensor_copy if h >= PAIRS - 2 else nc.scalar.copy)
            if h == 1:
                band_exponential(0)
                cut_band(0)
            if next_slab is not None:
                start_maximum(next_slab)
                fold(next_slab, SEQ // 2)
            if begun_slab is not None:
                fold(begun_slab, SEQ // 8)
            if quantised_slab is not None:
                quantise_merged(quantised_slab)

            if h == 2:
                turn_band(0)
                empty_band(0)
            if h < EARLY_STEPS and is_pair(attended):
                relative(attended)
            if True and is_pair(attended):
                attend(attended)
            if turned_slab is not None:
                start_output(turned_slab)
                for a in range(TILES):
                    turn_merged(turned_slab, a)
            if band_slab is not None and band_slab > 0:
                turn_band(band_slab)
            if h == 4:
                group_weights()
            if begun_slab is not None:
                fold(begun_slab, SEQ // 16)
            if first_slab is not None:
                add_bias(first_slab, 0)
                store(first_slab, 0)
            if second_slab is not None:
                add_bias(second_slab, 1)
                store(second_slab, 1)
            if begun_slab is not None:
                row_maximum(begun_slab, folded[begun_slab][:, :, 0 : SEQ // 16])
                shift_band(begun_slab)
            for q in range(HALF_HEADS):
                if h == group_step(q):
                    group_values(q)
            if next_slab is not None:
                fold(next_slab, SEQ // 4)

            if h == PAIRS - 1:
                return
            if is_pair(now):
                exponential(now, 1)
            if is_pair(before):
                quantise_e(before)
            for q in range(HALF_HEADS):
                if h == group_step(q):
                    quantise_values(q)
            if is_pair(now):
                empty_e(now, 0, nc.vector.tensor_copy if (now % 2 == 0 or now % 8 == 3 or now >= PAIRS - 3) and now > EARLY_STEPS else nc.scalar.copy)
            if h == 1:
                prepare_relative()
            if band_slab is not None and band_slab > 0:
                empty_band(band_slab)
            if is_pair(attended):
                empty_relative(attended)
            if turned_slab is not None:
                empty_merged(turned_slab)

        def first_maxima():
            start_maximum(0)
            for i in range(TILES):
                row_maximum(0, raw[0][:, i : i + 1, :], slice(i, i + 1))
            second_head = slice(TILES, SLAB_TILES)
            for width in (SEQ // 2, SEQ // 4, SEQ // 8):
                fold(0, width, second_head)
            row_maximum(0, folded[0][:, second_head, 0 : SEQ // 8], second_head)
            shift_band(0)

        def drain():
            last, s = PAIRS - 1, SLABS - 1
            tile_rows = [slice(a * P, (a + 1) * P) for a in range(TILES)]
            exponential(last, 1)
            turn_e(last, 1)
            quantise_e(last - 1)
            empty_e(last, 0, nc.vector.tensor_copy)
            project(s - 2, 0)
            empty_band(s)
            empty_relative(last - 2)
            relative(last - 1)
            attend(last - 1)
            add_bias(s - 2, 0)
            store(s - 2, 0)
            reciprocal(s)
            empty_e(last, 1, nc.scalar.copy)
            relative(last)
            for a in range(TILES):
                normalise(last - 2, a)
            empty_relative(last - 1)
            project(s - 2, 1)
            start_output(s - 1)
            for a in range(TILES):
                turn_merged(s - 1, a)
            quantise_e(last)
            attend(last)
            empty_relative(last)
            empty_merged(s - 1)
            for a in range(TILES):
                normalise(last - 1, a)
            add_bias(s - 2, 1)
            store(s - 2, 1)
            start_output(s)
            for a in range(TILES):
                normalise(last, a)
                turn_merged(s, a)
                empty_merged(s, tile_rows[a])
            quantise_merged(s - 1)
            for a in range(TILES):
                project(s - 1, a, psum_two.tile([P, FEATURES], F32, name="out_of_rel", tag="rel_bank"))
            quantise_merged(s, tile_rows[0])
            project(s, 0)
            add_bias(s - 1, 0)
            store(s - 1, 0)
            quantise_merged(s, tile_rows[1])
            project(s, 1, psum_two.tile([P, FEATURES], F32, name="out_of_e", tag="e_bank"))
            add_bias(s - 1, 1)
            store(s - 1, 1)
            for a in range(TILES):
                add_bias(s, a)
                store(s, a)

        load(0, 1)
        for m in range(1, 2 * HEADS):
            load(m)
        for m in range(2 * HEADS):
            load_band(m)
        load_values(0)
        for m in range(2 * HEADS, AHEAD * HEADS):
            load(m)
        load_values(KEY_PASSES)
        for m in range(2 * HEADS, AHEAD * HEADS):
            load_band(m)
        load_constants()
        first_maxima()
        for h in range(PAIRS):
            one_step(h)
        drain()
